import numpy as np
import ml_dtypes


def mxq(x, axis, fmt="e4m3"):
    dtype, down = {"e4m3": (ml_dtypes.float8_e4m3fn, 7), "e5m2": (ml_dtypes.float8_e5m2, 14)}[fmt]
    v = np.moveaxis(np.asarray(x, np.float32).astype(ml_dtypes.bfloat16).astype(np.float64), axis, -1)
    blocks = v.reshape(v.shape[:-1] + (-1, 32))
    amax = np.abs(blocks).max(-1, keepdims=True)
    byte = np.maximum(np.where(amax > 0, np.frexp(amax)[1] - 1 + 127, 0) - down, 1)
    scale = np.exp2(byte - 127.0)
    codes = (blocks / scale).astype(np.float32).astype(dtype).astype(np.float64)
    return np.moveaxis((codes * scale).reshape(v.shape), -1, axis)


WIDE = False


def mx_kscale(k):
    if not WIDE:
        return np.ones(k)
    levels = np.array([10, -10, 5, -5, 0])
    a = np.random.permutation(np.resize(levels, k // 512 * 4)).reshape(k // 512, 4)
    idx = np.arange(k)
    return np.exp2(a[idx // 512, idx % 128 // 32])


BF16 = ml_dtypes.bfloat16


def bf(x):
    return np.asarray(x, np.float32).astype(BF16)


def f64(x):
    return np.asarray(x).astype(np.float64)


E2M1 = np.array([0.0, 0.5, 1.0, 1.5, 2.0, 3.0, 4.0, 6.0, -0.0, -0.5, -1.0, -1.5, -2.0, -3.0, -4.0, -6.0])


def pack_weight(w, fmt):
    k, n = w.shape
    w = f64(bf(w)).reshape(k // 32, 32, n)
    amax = np.abs(w).max(1)
    if fmt == "e4m3":
        byte = np.frexp(amax)[1] - 1 + 127 - 7
    else:
        mant, ex = np.frexp(amax / 6.0)
        byte = np.where(mant > 0.5, ex, ex - 1) + 127
    byte = np.clip(np.where(amax > 0, byte, 1), 1, 254)
    scaled = (w * np.exp2(127.0 - byte)[:, None, :]).reshape(k, n).astype(np.float32)
    by_word = np.ascontiguousarray(scaled.reshape(k // 512, 128, 4, n).transpose(0, 1, 3, 2))
    if fmt == "e4m3":
        words = by_word.astype(ml_dtypes.float8_e4m3fn).view(np.uint8)
    else:
        c = by_word.astype(ml_dtypes.float4_e2m1fn).view(np.uint8) & 0xF
        words = c[..., 0::2] | (c[..., 1::2] << 4)
    return np.ascontiguousarray(words), np.ascontiguousarray(byte.astype(np.uint8).reshape(k // 512, 16, n))


def unpack_weight(words, scales, fmt):
    g, p, n, _ = words.shape
    if fmt == "e4m3":
        vals = np.ascontiguousarray(words).view(ml_dtypes.float8_e4m3fn).astype(np.float64)
    else:
        nib = np.empty((g, p, n, 4), np.uint8)
        nib[..., 0::2] = words & 0xF
        nib[..., 1::2] = words >> 4
        vals = E2M1[nib]
    vals = vals * np.repeat(np.exp2(scales.astype(np.float64) - 127.0), 8, axis=1)[..., None]
    return vals.transpose(0, 1, 3, 2).reshape(g * 512, n)

def pack4(w):
    words, scales = pack_weight(w, "e2m1")
    return words.reshape(words.shape[0], 128, -1), scales


def unpack4(words, scales):
    return unpack_weight(words.reshape(words.shape[0], 128, -1, 2), scales, "e2m1")


B, N, IN_DIM, OUT_DIM, NUM_F = 2, 256, 1024, 768, 8


def silu(v):
    return v / (1.0 + np.exp(-v))


def setup_inputs():
    t = mx_kscale(IN_DIM)
    x = bf(np.random.standard_normal((B, N, IN_DIM)))
    base_weight_words, base_weight_scales = pack4((np.random.standard_normal((OUT_DIM, IN_DIM)) / np.sqrt(IN_DIM)).T)
    return {"x": x,
            "base_weight_words": base_weight_words,
            "base_weight_scales": base_weight_scales,
            "grid": bf(np.arange(NUM_F) + 1.0),
            "scale_sp": bf(1.0 + 0.1 * np.random.standard_normal(OUT_DIM)),
            "coef": bf(np.random.uniform(size=(IN_DIM, NUM_F)) * t[:, None]),
            "conv_w": bf(np.random.standard_normal((NUM_F, OUT_DIM, IN_DIM)) / np.sqrt(IN_DIM) / t[None, None, :]),
            "conv_b": bf(np.random.standard_normal((NUM_F, OUT_DIM)) * 0.1)}


def reference(x, base_weight_words, base_weight_scales, grid, scale_sp, coef, conv_w, conv_b):
    x = f64(x)
    b, n, d = x.shape
    xf = x.reshape(b * n, d)
    base_out = mxq(silu(xf), 1, "e4m3") @ unpack4(base_weight_words, base_weight_scales)
    s = np.sin(xf[:, None, :] * f64(grid)[None, :, None]) * f64(coef).T[None, :, :]
    sq = mxq(s, 2, "e4m3")
    wq = mxq(f64(conv_w), 2, "e4m3")
    spline = np.matmul(sq.transpose(1, 0, 2), wq.transpose(0, 2, 1)).transpose(1, 0, 2) + f64(conv_b)[None, :, :]
    out = base_out + spline.sum(axis=1) * f64(scale_sp)
    return out.reshape(b, n, OUT_DIM)

@@ -1,0 +1,265 @@
+import math
+from contextlib import ExitStack
+
+import concourse.bass as bass
+import concourse.mybir as mybir
+import concourse.tile as tile
+from concourse.masks import make_identity
+
+F32 = mybir.dt.float32
+BF16 = mybir.dt.bfloat16
+I32 = mybir.dt.int32
+U32 = mybir.dt.uint32
+U8 = mybir.dt.uint8
+FP8X4 = mybir.dt.float8_e4m3fn_x4
+FP4X4 = mybir.dt.float4_e2m1fn_x4
+ACT = mybir.ActivationFunctionType
+ALU = mybir.AluOpType
+AX = mybir.AxisListType
+
+P = 128
+TOK = 512
+K = 1024
+OUT = 768
+NF = 8
+NG = 2
+NT = OUT // P
+NM = TOK // P
+
+FLOPS = 2 * TOK * K * OUT * (NF + 1)
+
+
+def tile_efficient_skan_batch_kernel(
+    tc, x, base_weight_words, base_weight_scales, grid, scale_sp, coef, conv_w, conv_b, out
+):
+    nc = tc.nc
+    with ExitStack() as ctx:
+        const = ctx.enter_context(tc.tile_pool(name="const", bufs=1))
+        wpool = ctx.enter_context(tc.tile_pool(name="wraw", bufs=3))
+        wgpool = ctx.enter_context(tc.tile_pool(name="wg", bufs=2))
+        wqpool = ctx.enter_context(tc.tile_pool(name="wq", bufs=3))
+        kpool = ctx.enter_context(tc.tile_pool(name="k", bufs=2))
+        rpool = ctx.enter_context(tc.tile_pool(name="r", bufs=3))
+        scpool = ctx.enter_context(tc.tile_pool(name="sc", bufs=2))
+        gpool = ctx.enter_context(tc.tile_pool(name="grp", bufs=2))
+        swpool = ctx.enter_context(tc.tile_pool(name="sw", bufs=3))
+        opool = ctx.enter_context(tc.tile_pool(name="o", bufs=3))
+        psum = ctx.enter_context(tc.psum_pool(name="psum", bufs=8))
+
+        xv = x.rearrange("b n k -> (b n) k").rearrange("(m p) k -> m p k", p=P)
+        x_sb = const.tile([P, NM, K], BF16, name="x_sb")
+        for m in range(NM):
+            nc.sync.dma_start(out=x_sb[:, m, :], in_=xv[m])
+
+        gb = const.tile([P, NF], BF16, name="gb")
+        nc.scalar.dma_start(out=gb[:], in_=grid.partition_broadcast(P))
+        craw = const.tile([P, NG, 4 * NF], BF16, name="craw")
+        nc.scalar.dma_start(
+            out=craw[:], in_=coef.rearrange("(g p j) f -> p g (j f)", g=NG, p=P)
+        )
+        braw = const.tile([P, P], BF16, name="braw")
+        nc.vector.memset(braw[:], 0.0)
+        nc.scalar.dma_start(
+            out=braw[0 : NF * NT, :], in_=conv_b.rearrange("f (t c) -> (f t) c", c=P)
+        )
+        nc.scalar.dma_start(
+            out=braw[NF * NT : NF * NT + NT, :], in_=scale_sp.rearrange("(t c) -> t c", c=P)
+        )
+
+        w4w = const.tile([P, NG, 2 * OUT], U8, name="w4w", align_bytes=64)
+        nc.sync.dma_start(
+            out=w4w[:].bitcast(I32),
+            in_=base_weight_words.rearrange("g p n -> p g n").bitcast(I32),
+        )
+        w4s = const.tile([P, NG, OUT], U8, name="w4s", align_bytes=64)
+        nc.vector.memset(w4s[:].bitcast(I32), 0)
+        w4sv = base_weight_scales.rearrange("g (q r) n -> r q g n", r=4)
+        for r in range(4):
+            nc.sync.dma_start(out=w4s[r:P:32, :, :].bitcast(I32), in_=w4sv[r].bitcast(I32))
+
+        ident = const.tile([P, P], F32, name="ident")
+        make_identity(nc, ident[:])
+        identb = const.tile([P, P], BF16, name="identb")
+        make_identity(nc, identb[:])
+
+        g32 = const.tile([P, NF], F32, name="g32")
+        nc.vector.tensor_copy(out=g32[:], in_=gb[:])
+        cturn = const.tile([P, NF], F32, name="cturn")
+        nc.vector.tensor_scalar(
+            out=cturn[:], in0=g32[:], scalar1=1.0 / (2.0 * math.pi), scalar2=None, op0=ALU.mult
+        )
+        coefT = const.tile([P, NF * NG * 4], F32, name="coefT")
+        nc.vector.tensor_copy(
+            out=coefT[:].rearrange("p (f g j) -> p f g j", f=NF, g=NG),
+            in_=craw[:].rearrange("p g (j f) -> p f g j", f=NF),
+        )
+
+        xT = const.tile([P, NG * 4, TOK], BF16, name="xT")
+        silu_g = const.tile([P, NG, TOK, 4], BF16, name="silu_g", align_bytes=64)
+        for m in range(NM):
+            xw = x_sb[:, m, :].bitcast(F32)
+            xpa = psum.tile([P, 4, P], F32, tag="bank", name="xpa")
+            xpv = psum.tile([P, 4, P], F32, tag="bank", name="xpv")
+            for q in range(4):
+                g, u = divmod(q, 2)
+                nc.tensor.transpose(xpv[:, q, :], xw[:, 256 * g + u : 256 * (g + 1) : 2], ident[:])
+            for q in range(4):
+                g, u = divmod(q, 2)
+                nc.tensor.transpose(xpa[:, q, :], xw[:, 256 * g + u : 256 * (g + 1) : 2], ident[:])
+            nc.vector.tensor_copy(
+                out=xT[:, :, m * P : (m + 1) * P].rearrange("p (q e) t -> p q e t", e=2),
+                in_=xpv[:].bitcast(BF16).rearrange("p q (t e) -> p q e t", e=2),
+            )
+            xab = xpa[:].bitcast(BF16)
+            for g in range(NG):
+                nc.scalar.activation(
+                    out=silu_g[:, g, m * P : (m + 1) * P, :].rearrange("p t (u e) -> p t u e", e=2),
+                    in_=xab[:, 2 * g : 2 * g + 2, :].rearrange("p u (t e) -> p t u e", e=2),
+                    func=ACT.Silu,
+                )
+
+        bps = psum.tile([P, P], BF16, tag="bank", name="bps")
+        nc.tensor.transpose(bps[:], braw[:], identb[:])
+        bT = const.tile([P, 64], F32, name="bT")
+        nc.vector.tensor_copy(out=bT[:, 0 : NF * NT + NT], in_=bps[:, 0 : NF * NT + NT])
+        bsum = const.tile([P, NT], F32, name="bsum")
+        nc.vector.tensor_reduce(
+            out=bsum[:],
+            in_=bT[:, 0 : NF * NT].rearrange("p (f t) -> p t f", t=NT),
+            axis=AX.X,
+            op=ALU.add,
+        )
+        sbs = const.tile([P, NT], F32, name="sbs")
+        nc.vector.tensor_mul(out=sbs[:], in0=bsum[:], in1=bT[:, NF * NT : NF * NT + NT])
+
+        sil_w = const.tile([P, NG, TOK], U32, name="sil_w", align_bytes=64)
+        sil_s = const.tile([P, NG, TOK], U8, name="sil_s", align_bytes=64)
+        nc.vector.quantize_mx(
+            out=sil_w[:].rearrange("p g t -> p (g t)").bitcast(FP8X4),
+            scales=sil_s[:].rearrange("p g t -> p (g t)"),
+            in_=silu_g[:].rearrange("p g t j -> p (g t j)"),
+        )
+        basec = []
+        for t in range(NT):
+            bacc = psum.tile([P, TOK], F32, tag="bank", name="bacc")
+            for g in range(NG):
+                nc.tensor.matmul_mx(
+                    out=bacc[:],
+                    lhsT=w4w[:, g, 2 * P * t : 2 * P * (t + 1)].bitcast(FP4X4),
+                    lhsT_scale=w4s[:, g, P * t : P * (t + 1)],
+                    rhs=sil_w[:, g, :].bitcast(FP8X4),
+                    rhs_scale=sil_s[:, g, :],
+                    start=(g == 0),
+                    stop=(g == NG - 1),
+                )
+            bc = const.tile([P, TOK], F32, name="basec%d" % t)
+            nc.scalar.activation(out=bc[:], in_=bacc[:], func=ACT.Identity, bias=sbs[:, t : t + 1])
+            basec.append(bc)
+
+        def load_w(f):
+            wraw = wpool.tile([P, NT, K], BF16, name="wraw")
+            nc.sync.dma_start(out=wraw[:], in_=conv_w[f].rearrange("(t p) k -> p t k", p=P))
+            return wraw
+
+        def prep_w(wraw):
+            wg = wgpool.tile([P, NT * NG * P * 4], BF16, name="wg", align_bytes=64)
+            wgw = wg[:].bitcast(F32)
+            for t in range(NT):
+                ww = wraw[:, t, :].bitcast(F32)
+                wps = psum.tile([P, 4, P], F32, tag="bank", name="wps")
+                for q in range(4):
+                    g, u = divmod(q, 2)
+                    nc.tensor.transpose(
+                        wps[:, q, :], ww[:, 256 * g + u : 256 * (g + 1) : 2], ident[:]
+                    )
+                nc.scalar.copy(
+                    out=wgw[:, 512 * t : 512 * (t + 1)].rearrange("p (g o u) -> p g o u", g=NG, u=2),
+                    in_=wps[:].rearrange("p (g u) o -> p g o u", u=2),
+                )
+            wq = wqpool.tile([P, NT * NG * P], U32, name="wq", align_bytes=64)
+            wsc = wqpool.tile([P, NT * NG * P], U8, name="wsc", align_bytes=64)
+            for c in range(3):
+                nc.vector.quantize_mx(
+                    out=wq[:, 512 * c : 512 * (c + 1)].bitcast(FP8X4),
+                    scales=wsc[:, 512 * c : 512 * (c + 1)],
+                    in_=wg[:, 2048 * c : 2048 * (c + 1)],
+                )
+            return wq, wsc
+
+        raws = [load_w(0), load_w(1)]
+        wcur = prep_w(raws[0])
+
+        acc = [psum.tile([P, TOK], F32, tag="bank", name="acc%d" % t) for t in range(NT)]
+
+        for f in range(NF):
+            if f + 2 < NF:
+                raws.append(load_w(f + 2))
+            for g in range(NG):
+                xr = xT[:, 4 * g : 4 * g + 4, :].rearrange("p j t -> p (j t)")
+                kk = kpool.tile([P, 4 * TOK], I32, name="kk")
+                nc.vector.tensor_scalar(
+                    out=kk[:], in0=xr, scalar1=cturn[:, f : f + 1], scalar2=None, op0=ALU.mult
+                )
+                rr = rpool.tile([P, 4 * TOK], F32, name="rr")
+                nc.vector.scalar_tensor_tensor(
+                    out=rr[:],
+                    in0=xr,
+                    scalar=cturn[:, f : f + 1],
+                    in1=kk[:],
+                    op0=ALU.mult,
+                    op1=ALU.subtract,
+                )
+                nc.scalar.activation(out=rr[:], in_=rr[:], func=ACT.Sin, scale=2.0 * math.pi)
+                sc = scpool.tile([P, 4, TOK], BF16, name="sc")
+                for j in range(4):
+                    ci = (f * NG + g) * 4 + j
+                    nc.scalar.activation(
+                        out=sc[:, j, :],
+                        in_=rr[:, TOK * j : TOK * (j + 1)],
+                        func=ACT.Copy,
+                        scale=coefT[:, ci : ci + 1],
+                    )
+                grp = gpool.tile([P, TOK, 4], BF16, name="grp", align_bytes=64)
+                nc.vector.tensor_copy(
+                    out=grp[:].rearrange("p (c i) j -> p c j i", i=4),
+                    in_=sc[:].rearrange("p j (c i) -> p c j i", i=4),
+                )
+                sw = swpool.tile([P, TOK], U32, name="sw", align_bytes=64)
+                ss = swpool.tile([P, TOK], U8, name="ss", align_bytes=64)
+                nc.vector.quantize_mx(
+                    out=sw[:].bitcast(FP8X4),
+                    scales=ss[:],
+                    in_=grp[:].rearrange("p t j -> p (t j)"),
+                )
+                wq, wsc = wcur
+                for t in range(NT):
+                    lo = (t * NG + g) * P
+                    nc.tensor.matmul_mx(
+                        out=acc[t][:],
+                        lhsT=wq[:, lo : lo + P].bitcast(FP8X4),
+                        lhsT_scale=wsc[:, lo : lo + P],
+                        rhs=sw[:].bitcast(FP8X4),
+                        rhs_scale=ss[:],
+                        start=(f == 0 and g == 0),
+                        stop=(f == NF - 1 and g == NG - 1),
+                    )
+            if f + 1 < NF:
+                wcur = prep_w(raws[f + 1])
+
+        outv = out.rearrange("b n o -> (b n) o").rearrange("(m p) o -> p m o", p=P)
+        for t in range(NT):
+            ot = opool.tile([P, TOK], F32, name="ot")
+            nc.vector.scalar_tensor_tensor(
+                out=ot[:],
+                in0=acc[t][:],
+                scalar=bT[:, NF * NT + t : NF * NT + t + 1],
+                in1=basec[t][:],
+                op0=ALU.mult,
+                op1=ALU.add,
+            )
+            fps = psum.tile([P, NM, P], F32, tag="bank", name="fps")
+            for m in range(NM):
+                nc.tensor.transpose(fps[:, m, :], ot[:, m * P : (m + 1) * P], ident[:])
+            of = opool.tile([P, NM, P], F32, name="of")
+            nc.scalar.copy(out=of[:], in_=fps[:])
+            nc.sync.dma_start(out=outv[:, :, t * P : (t + 1) * P], in_=of[:])

@@ -1,9 +1,7 @@
 import math
 from contextlib import ExitStack
 
-import concourse.bass as bass
 import concourse.mybir as mybir
-import concourse.tile as tile
 from concourse.masks import make_identity
 
 F32 = mybir.dt.float32
@@ -15,7 +13,6 @@ FP8X4 = mybir.dt.float8_e4m3fn_x4
 FP4X4 = mybir.dt.float4_e2m1fn_x4
 ACT = mybir.ActivationFunctionType
 ALU = mybir.AluOpType
-AX = mybir.AxisListType
 
 P = 128
 TOK = 512
@@ -25,8 +22,19 @@ NF = 8
 NG = 2
 NT = OUT // P
 NM = TOK // P
+HT = 256
+NU = 2 * NF * NG
 
 FLOPS = 2 * TOK * K * OUT * (NF + 1)
+
+K_ON_G = (0,)
+K_MOD = 1
+T_UNITS = ()
+T_MOD = 1
+EV_ON_V = (3,)
+EV_MOD = 4
+BANKS_PER_IT = 4
+PIN = False
 
 
 def tile_efficient_skan_batch_kernel(
@@ -35,16 +43,18 @@ def tile_efficient_skan_batch_kernel(
     nc = tc.nc
     with ExitStack() as ctx:
         const = ctx.enter_context(tc.tile_pool(name="const", bufs=1))
-        wpool = ctx.enter_context(tc.tile_pool(name="wraw", bufs=3))
+        wpool = ctx.enter_context(tc.tile_pool(name="wraw", bufs=2))
         wgpool = ctx.enter_context(tc.tile_pool(name="wg", bufs=2))
-        wqpool = ctx.enter_context(tc.tile_pool(name="wq", bufs=3))
-        kpool = ctx.enter_context(tc.tile_pool(name="k", bufs=2))
+        kpool = ctx.enter_context(tc.tile_pool(name="k", bufs=3))
         rpool = ctx.enter_context(tc.tile_pool(name="r", bufs=3))
-        scpool = ctx.enter_context(tc.tile_pool(name="sc", bufs=2))
-        gpool = ctx.enter_context(tc.tile_pool(name="grp", bufs=2))
-        swpool = ctx.enter_context(tc.tile_pool(name="sw", bufs=3))
-        opool = ctx.enter_context(tc.tile_pool(name="o", bufs=3))
-        psum = ctx.enter_context(tc.psum_pool(name="psum", bufs=8))
+        snpool = ctx.enter_context(tc.tile_pool(name="sn", bufs=2))
+        scpool = ctx.enter_context(tc.tile_pool(name="sc", bufs=3))
+        gpool = ctx.enter_context(tc.tile_pool(name="grp", bufs=3))
+        swpool = ctx.enter_context(tc.tile_pool(name="sw", bufs=6))
+        opool = ctx.enter_context(tc.tile_pool(name="o", bufs=2))
+        psum = ctx.enter_context(tc.psum_pool(name="psum", bufs=2))
+        if PIN:
+            ctx.enter_context(tc.manual_schedule())
 
         xv = x.rearrange("b n k -> (b n) k").rearrange("(m p) k -> m p k", p=P)
         x_sb = const.tile([P, NM, K], BF16, name="x_sb")
@@ -57,14 +67,14 @@ def tile_efficient_skan_batch_kernel(
         nc.scalar.dma_start(
             out=craw[:], in_=coef.rearrange("(g p j) f -> p g (j f)", g=NG, p=P)
         )
-        braw = const.tile([P, P], BF16, name="braw")
-        nc.vector.memset(braw[:], 0.0)
-        nc.scalar.dma_start(
-            out=braw[0 : NF * NT, :], in_=conv_b.rearrange("f (t c) -> (f t) c", c=P)
-        )
-        nc.scalar.dma_start(
-            out=braw[NF * NT : NF * NT + NT, :], in_=scale_sp.rearrange("(t c) -> t c", c=P)
-        )
+        rb = const.tile([P, OUT], BF16, name="rb")
+        nc.gpsimd.memset(rb[:], 0.0)
+        rs = const.tile([P, OUT], BF16, name="rs")
+        nc.gpsimd.memset(rs[:], 0.0)
+        ones = const.tile([P, P], BF16, name="ones")
+        nc.gpsimd.memset(ones[:], 1.0)
+        nc.scalar.dma_start(out=rb[0:NF, :], in_=conv_b)
+        nc.scalar.dma_start(out=rs[0:1, :], in_=scale_sp.rearrange("(a o) -> a o", a=1))
 
         w4w = const.tile([P, NG, 2 * OUT], U8, name="w4w", align_bytes=64)
         nc.sync.dma_start(
@@ -79,8 +89,16 @@ def tile_efficient_skan_batch_kernel(
 
         ident = const.tile([P, P], F32, name="ident")
         make_identity(nc, ident[:])
-        identb = const.tile([P, P], BF16, name="identb")
-        make_identity(nc, identb[:])
+
+        raws = {}
+
+        def load_w(f):
+            wraw = wpool.tile([P, NT, K], BF16, name="wraw")
+            nc.sync.dma_start(out=wraw[:], in_=conv_w[f].rearrange("(t p) k -> p t k", p=P))
+            raws[f] = wraw
+
+        for f in range(2):
+            load_w(f)
 
         g32 = const.tile([P, NF], F32, name="g32")
         nc.vector.tensor_copy(out=g32[:], in_=gb[:])
@@ -94,172 +112,282 @@ def tile_efficient_skan_batch_kernel(
             in_=craw[:].rearrange("p g (j f) -> p f g j", f=NF),
         )
 
-        xT = const.tile([P, NG * 4, TOK], BF16, name="xT")
-        silu_g = const.tile([P, NG, TOK, 4], BF16, name="silu_g", align_bytes=64)
-        for m in range(NM):
-            xw = x_sb[:, m, :].bitcast(F32)
-            xpa = psum.tile([P, 4, P], F32, tag="bank", name="xpa")
-            xpv = psum.tile([P, 4, P], F32, tag="bank", name="xpv")
+        xbank = {}
+        xs = {}
+
+        def make_xt(h, tag):
+            for g in range(NG):
+                xb = psum.tile([P, 2, HT], F32, tag=tag, name="xb")
+                for mi in range(2):
+                    xw = x_sb[:, 2 * h + mi, :].bitcast(F32)
+                    for u in range(2):
+                        nc.tensor.transpose(
+                            xb[:, u, mi * P : (mi + 1) * P],
+                            xw[:, 256 * g + u : 256 * (g + 1) : 2],
+                            ident[:],
+                        )
+                xc = const.tile([P, 4 * HT], BF16, name="xs%d%d" % (h, g))
+                nc.scalar.copy(out=xc[:].bitcast(F32), in_=xb[:].rearrange("p u t -> p (u t)"))
+                xbank[(h, g)] = xb
+                xs[(h, g)] = xc
+
+        make_xt(0, "x")
+
+        wgs = {}
+        wqs = {}
+
+        def w_bank(b):
+            f, t = divmod(b, NT)
+            if t == 0:
+                wgs[f] = wgpool.tile([P, NG, OUT, 4], BF16, name="wg", align_bytes=64)
+            wgw = wgs[f][:].rearrange("p g o j -> p g (o j)").bitcast(F32)
+            ww = raws[f][:, t, :].bitcast(F32)
+            wps = psum.tile([P, 4, P], F32, tag="w", name="wps")
             for q in range(4):
                 g, u = divmod(q, 2)
-                nc.tensor.transpose(xpv[:, q, :], xw[:, 256 * g + u : 256 * (g + 1) : 2], ident[:])
-            for q in range(4):
-                g, u = divmod(q, 2)
-                nc.tensor.transpose(xpa[:, q, :], xw[:, 256 * g + u : 256 * (g + 1) : 2], ident[:])
-            nc.vector.tensor_copy(
-                out=xT[:, :, m * P : (m + 1) * P].rearrange("p (q e) t -> p q e t", e=2),
-                in_=xpv[:].bitcast(BF16).rearrange("p q (t e) -> p q e t", e=2),
-            )
-            xab = xpa[:].bitcast(BF16)
-            for g in range(NG):
-                nc.scalar.activation(
-                    out=silu_g[:, g, m * P : (m + 1) * P, :].rearrange("p t (u e) -> p t u e", e=2),
-                    in_=xab[:, 2 * g : 2 * g + 2, :].rearrange("p u (t e) -> p t u e", e=2),
-                    func=ACT.Silu,
-                )
+                nc.tensor.transpose(wps[:, q, :], ww[:, 256 * g + u : 256 * (g + 1) : 2], ident[:])
+            dst = wgw[:, :, 2 * P * t : 2 * P * (t + 1)].rearrange("p g (o u) -> p g o u", u=2)
+            src = wps[:].rearrange("p (g u) o -> p g o u", u=2)
+            if b % EV_MOD in EV_ON_V:
+                nc.vector.tensor_copy(out=dst, in_=src)
+            else:
+                nc.scalar.copy(out=dst, in_=src)
+            if t == NT - 1 and f + 2 < NF:
+                load_w(f + 2)
 
-        bps = psum.tile([P, P], BF16, tag="bank", name="bps")
-        nc.tensor.transpose(bps[:], braw[:], identb[:])
-        bT = const.tile([P, 64], F32, name="bT")
-        nc.vector.tensor_copy(out=bT[:, 0 : NF * NT + NT], in_=bps[:, 0 : NF * NT + NT])
-        bsum = const.tile([P, NT], F32, name="bsum")
-        nc.vector.tensor_reduce(
-            out=bsum[:],
-            in_=bT[:, 0 : NF * NT].rearrange("p (f t) -> p t f", t=NT),
-            axis=AX.X,
-            op=ALU.add,
-        )
-        sbs = const.tile([P, NT], F32, name="sbs")
-        nc.vector.tensor_mul(out=sbs[:], in0=bsum[:], in1=bT[:, NF * NT : NF * NT + NT])
-
-        sil_w = const.tile([P, NG, TOK], U32, name="sil_w", align_bytes=64)
-        sil_s = const.tile([P, NG, TOK], U8, name="sil_s", align_bytes=64)
-        nc.vector.quantize_mx(
-            out=sil_w[:].rearrange("p g t -> p (g t)").bitcast(FP8X4),
-            scales=sil_s[:].rearrange("p g t -> p (g t)"),
-            in_=silu_g[:].rearrange("p g t j -> p (g t j)"),
-        )
-        basec = []
-        for t in range(NT):
-            bacc = psum.tile([P, TOK], F32, tag="bank", name="bacc")
-            for g in range(NG):
-                nc.tensor.matmul_mx(
-                    out=bacc[:],
-                    lhsT=w4w[:, g, 2 * P * t : 2 * P * (t + 1)].bitcast(FP4X4),
-                    lhsT_scale=w4s[:, g, P * t : P * (t + 1)],
-                    rhs=sil_w[:, g, :].bitcast(FP8X4),
-                    rhs_scale=sil_s[:, g, :],
-                    start=(g == 0),
-                    stop=(g == NG - 1),
-                )
-            bc = const.tile([P, TOK], F32, name="basec%d" % t)
-            nc.scalar.activation(out=bc[:], in_=bacc[:], func=ACT.Identity, bias=sbs[:, t : t + 1])
-            basec.append(bc)
-
-        def load_w(f):
-            wraw = wpool.tile([P, NT, K], BF16, name="wraw")
-            nc.sync.dma_start(out=wraw[:], in_=conv_w[f].rearrange("(t p) k -> p t k", p=P))
-            return wraw
-
-        def prep_w(wraw):
-            wg = wgpool.tile([P, NT * NG * P * 4], BF16, name="wg", align_bytes=64)
-            wgw = wg[:].bitcast(F32)
-            for t in range(NT):
-                ww = wraw[:, t, :].bitcast(F32)
-                wps = psum.tile([P, 4, P], F32, tag="bank", name="wps")
-                for q in range(4):
-                    g, u = divmod(q, 2)
-                    nc.tensor.transpose(
-                        wps[:, q, :], ww[:, 256 * g + u : 256 * (g + 1) : 2], ident[:]
-                    )
-                nc.scalar.copy(
-                    out=wgw[:, 512 * t : 512 * (t + 1)].rearrange("p (g o u) -> p g o u", g=NG, u=2),
-                    in_=wps[:].rearrange("p (g u) o -> p g o u", u=2),
-                )
-            wq = wqpool.tile([P, NT * NG * P], U32, name="wq", align_bytes=64)
-            wsc = wqpool.tile([P, NT * NG * P], U8, name="wsc", align_bytes=64)
+        def w_quant(f):
+            wq = const.tile([P, NG * OUT], U32, name="wq%d" % f, align_bytes=64)
+            wsc = const.tile([P, NG * OUT], U8, name="wsc%d" % f, align_bytes=64)
+            wgf = wgs[f][:].rearrange("p g o j -> p (g o j)")
             for c in range(3):
                 nc.vector.quantize_mx(
                     out=wq[:, 512 * c : 512 * (c + 1)].bitcast(FP8X4),
                     scales=wsc[:, 512 * c : 512 * (c + 1)],
-                    in_=wg[:, 2048 * c : 2048 * (c + 1)],
+                    in_=wgf[:, 2048 * c : 2048 * (c + 1)],
                 )
-            return wq, wsc
+            wqs[f] = (wq, wsc)
 
-        raws = [load_w(0), load_w(1)]
-        wcur = prep_w(raws[0])
+        silu_g = const.tile([P, NG, TOK, 4], BF16, name="silu_g", align_bytes=64)
+        sil_w = const.tile([P, NG, TOK], U32, name="sil_w", align_bytes=64)
+        sil_s = const.tile([P, NG, TOK], U8, name="sil_s", align_bytes=64)
+        spb = const.tile([P, OUT], F32, name="spb")
+        sbb = const.tile([P, OUT], F32, name="sbb")
+        cm = [const.tile([P, OUT], F32, name="cm%d" % m) for m in range(NM)]
 
-        acc = [psum.tile([P, TOK], F32, tag="bank", name="acc%d" % t) for t in range(NT)]
+        def silu_part():
+            for m in range(NM):
+                xw = x_sb[:, m, :].bitcast(F32)
+                xpa = psum.tile([P, 4, P], F32, tag="acc", bufs=4, name="xpa")
+                for q in range(4):
+                    g, u = divmod(q, 2)
+                    nc.tensor.transpose(
+                        xpa[:, q, :], xw[:, 256 * g + u : 256 * (g + 1) : 2], ident[:]
+                    )
+                xab = xpa[:].bitcast(BF16)
+                for g in range(NG):
+                    nc.scalar.activation(
+                        out=silu_g[:, g, m * P : (m + 1) * P, :].rearrange(
+                            "p t (u e) -> p t u e", e=2
+                        ),
+                        in_=xab[:, 2 * g : 2 * g + 2, :].rearrange("p u (t e) -> p t u e", e=2),
+                        func=ACT.Silu,
+                    )
 
-        for f in range(NF):
-            if f + 2 < NF:
-                raws.append(load_w(f + 2))
-            for g in range(NG):
-                xr = xT[:, 4 * g : 4 * g + 4, :].rearrange("p j t -> p (j t)")
-                kk = kpool.tile([P, 4 * TOK], I32, name="kk")
+        def bias_part():
+            for lo, hi in ((0, 512), (512, OUT)):
+                sps = psum.tile([P, 512], F32, tag="w", name="sps")
+                nc.tensor.matmul(sps[:, 0 : hi - lo], lhsT=ones[:], rhs=rs[:, lo:hi], start=True, stop=True)
+                nc.scalar.copy(out=spb[:, lo:hi], in_=sps[:, 0 : hi - lo])
+                bps = psum.tile([P, 512], F32, tag="w", name="bps")
+                nc.tensor.matmul(bps[:, 0 : hi - lo], lhsT=ones[:], rhs=rb[:, lo:hi], start=True, stop=True)
+                nc.vector.tensor_tensor(
+                    out=sbb[:, lo:hi], in0=bps[:, 0 : hi - lo], in1=spb[:, lo:hi], op=ALU.mult
+                )
+
+        def base_part():
+            nc.vector.quantize_mx(
+                out=sil_w[:].rearrange("p g t -> p (g t)").bitcast(FP8X4),
+                scales=sil_s[:].rearrange("p g t -> p (g t)"),
+                in_=silu_g[:].rearrange("p g t j -> p (g t j)"),
+            )
+            for m in range(NM):
+                ba = psum.tile([P, 512], F32, tag="acc", bufs=4, name="ba")
+                bb = psum.tile([P, 512], F32, tag="acc", bufs=4, name="bb")
+                for dst, lo, n in ((ba[:, 0:512], 0, 512), (bb[:, 0:128], 512, 128), (bb[:, 128:256], 640, 128)):
+                    for g in range(NG):
+                        nc.tensor.matmul_mx(
+                            out=dst,
+                            lhsT=sil_w[:, g, m * P : (m + 1) * P].bitcast(FP8X4),
+                            lhsT_scale=sil_s[:, g, m * P : (m + 1) * P],
+                            rhs=w4w[:, g, 2 * lo : 2 * (lo + n)].bitcast(FP4X4),
+                            rhs_scale=w4s[:, g, lo : lo + n],
+                            start=(g == 0),
+                            stop=(g == NG - 1),
+                        )
+                nc.vector.tensor_tensor(out=cm[m][:, 0:512], in0=ba[:], in1=sbb[:, 0:512], op=ALU.add)
+                nc.vector.tensor_tensor(
+                    out=cm[m][:, 512:OUT], in0=bb[:, 0:256], in1=sbb[:, 512:OUT], op=ALU.add
+                )
+
+        kt = {}
+        rt = {}
+        sct = {}
+        grt = {}
+        swt = {}
+        acc = {}
+
+        def unit(n):
+            h, rest = divmod(n, NF * NG)
+            f, g = divmod(rest, NG)
+            return h, f, g
+
+        def s1(n):
+            h, f, g = unit(n)
+            kk = kpool.tile([P, 4 * HT], I32, name="kk")
+            if n % K_MOD in K_ON_G:
+                nc.gpsimd.tensor_scalar(
+                    out=kk[:], in0=xs[(h, g)][:], scalar1=cturn[:, f : f + 1], scalar2=0.0,
+                    op0=ALU.mult, op1=ALU.add,
+                )
+            else:
                 nc.vector.tensor_scalar(
-                    out=kk[:], in0=xr, scalar1=cturn[:, f : f + 1], scalar2=None, op0=ALU.mult
-                )
-                rr = rpool.tile([P, 4 * TOK], F32, name="rr")
-                nc.vector.scalar_tensor_tensor(
-                    out=rr[:],
-                    in0=xr,
-                    scalar=cturn[:, f : f + 1],
-                    in1=kk[:],
+                    out=kk[:], in0=xs[(h, g)][:], scalar1=cturn[:, f : f + 1], scalar2=None,
                     op0=ALU.mult,
-                    op1=ALU.subtract,
                 )
+            kt[n] = kk
+
+        def s2(n):
+            h, f, g = unit(n)
+            rr = rpool.tile([P, 4 * HT], F32, name="rr")
+            nc.vector.scalar_tensor_tensor(
+                out=rr[:],
+                in0=xbank[(h, g)][:].rearrange("p u t -> p (u t)").bitcast(BF16),
+                scalar=cturn[:, f : f + 1],
+                in1=kt[n][:],
+                op0=ALU.mult,
+                op1=ALU.subtract,
+            )
+            rt[n] = rr
+
+        def s3(n):
+            h, f, g = unit(n)
+            rr = rt[n]
+            ci = (f * NG + g) * 4
+            if n % T_MOD in T_UNITS:
+                sn = snpool.tile([P, HT, 4], F32, name="sn")
+                nc.scalar.activation(
+                    out=sn[:].rearrange("p t (u e) -> p t u e", e=2),
+                    in_=rr[:].rearrange("p (u t e) -> p t u e", u=2, e=2),
+                    func=ACT.Sin,
+                    scale=2.0 * math.pi,
+                )
+                sct[n] = sn
+            else:
                 nc.scalar.activation(out=rr[:], in_=rr[:], func=ACT.Sin, scale=2.0 * math.pi)
-                sc = scpool.tile([P, 4, TOK], BF16, name="sc")
+                sc = scpool.tile([P, 4, HT], BF16, name="sc")
+                rv = rr[:].rearrange("p (u t e) -> p u e t", u=2, e=2)
                 for j in range(4):
-                    ci = (f * NG + g) * 4 + j
                     nc.scalar.activation(
                         out=sc[:, j, :],
-                        in_=rr[:, TOK * j : TOK * (j + 1)],
+                        in_=rv[:, j // 2, j % 2, :],
                         func=ACT.Copy,
-                        scale=coefT[:, ci : ci + 1],
+                        scale=coefT[:, ci + j : ci + j + 1],
                     )
-                grp = gpool.tile([P, TOK, 4], BF16, name="grp", align_bytes=64)
+                sct[n] = sc
+
+        def s4(n):
+            h, f, g = unit(n)
+            ci = (f * NG + g) * 4
+            grp = gpool.tile([P, HT, 4], BF16, name="grp", align_bytes=64)
+            if n % T_MOD in T_UNITS:
+                nc.vector.tensor_tensor(
+                    out=grp[:],
+                    in0=sct[n][:],
+                    in1=coefT[:, ci : ci + 4].unsqueeze(1).to_broadcast([P, HT, 4]),
+                    op=ALU.mult,
+                )
+            else:
                 nc.vector.tensor_copy(
                     out=grp[:].rearrange("p (c i) j -> p c j i", i=4),
-                    in_=sc[:].rearrange("p j (c i) -> p c j i", i=4),
+                    in_=sct[n][:].rearrange("p j (c i) -> p c j i", i=4),
                 )
-                sw = swpool.tile([P, TOK], U32, name="sw", align_bytes=64)
-                ss = swpool.tile([P, TOK], U8, name="ss", align_bytes=64)
-                nc.vector.quantize_mx(
-                    out=sw[:].bitcast(FP8X4),
-                    scales=ss[:],
-                    in_=grp[:].rearrange("p t j -> p (t j)"),
-                )
-                wq, wsc = wcur
-                for t in range(NT):
-                    lo = (t * NG + g) * P
+            grt[n] = grp
+
+        def s5(n):
+            sw = swpool.tile([P, HT], U32, name="sw", align_bytes=64)
+            ss = swpool.tile([P, HT], U8, name="ss", align_bytes=64)
+            nc.vector.quantize_mx(
+                out=sw[:].bitcast(FP8X4), scales=ss[:], in_=grt[n][:].rearrange("p t j -> p (t j)")
+            )
+            swt[n] = (sw, ss)
+
+        def s6(n):
+            h, f, g = unit(n)
+            if f == 0 and g == 0:
+                for mi in range(2):
+                    acc[(h, mi, 0)] = psum.tile([P, 512], F32, tag="acc", bufs=4, name="acca")
+                    acc[(h, mi, 1)] = psum.tile([P, 512], F32, tag="acc", bufs=4, name="accb")
+            sw, ss = swt[n]
+            wq, wsc = wqs[f]
+            for mi in range(2):
+                for part, lo, nn in ((0, 0, 512), (1, 512, 256)):
                     nc.tensor.matmul_mx(
-                        out=acc[t][:],
-                        lhsT=wq[:, lo : lo + P].bitcast(FP8X4),
-                        lhsT_scale=wsc[:, lo : lo + P],
-                        rhs=sw[:].bitcast(FP8X4),
-                        rhs_scale=ss[:],
+                        out=acc[(h, mi, part)][:, 0:nn],
+                        lhsT=sw[:, mi * P : (mi + 1) * P].bitcast(FP8X4),
+                        lhsT_scale=ss[:, mi * P : (mi + 1) * P],
+                        rhs=wq[:, g * OUT + lo : g * OUT + lo + nn].bitcast(FP8X4),
+                        rhs_scale=wsc[:, g * OUT + lo : g * OUT + lo + nn],
                         start=(f == 0 and g == 0),
                         stop=(f == NF - 1 and g == NG - 1),
                     )
-            if f + 1 < NF:
-                wcur = prep_w(raws[f + 1])
 
-        outv = out.rearrange("b n o -> (b n) o").rearrange("(m p) o -> p m o", p=P)
-        for t in range(NT):
-            ot = opool.tile([P, TOK], F32, name="ot")
-            nc.vector.scalar_tensor_tensor(
-                out=ot[:],
-                in0=acc[t][:],
-                scalar=bT[:, NF * NT + t : NF * NT + t + 1],
-                in1=basec[t][:],
-                op0=ALU.mult,
-                op1=ALU.add,
-            )
-            fps = psum.tile([P, NM, P], F32, tag="bank", name="fps")
-            for m in range(NM):
-                nc.tensor.transpose(fps[:, m, :], ot[:, m * P : (m + 1) * P], ident[:])
-            of = opool.tile([P, NM, P], F32, name="of")
-            nc.scalar.copy(out=of[:], in_=fps[:])
-            nc.sync.dma_start(out=outv[:, :, t * P : (t + 1) * P], in_=of[:])
+        outv = out.rearrange("b n o -> (b n) o").rearrange("(m p) o -> m p o", p=P)
+
+        def finish(h):
+            for mi in range(2):
+                m = 2 * h + mi
+                ot = opool.tile([P, OUT], F32, name="ot")
+                nc.vector.tensor_tensor(
+                    out=ot[:, 0:512], in0=acc[(h, mi, 0)][:], in1=spb[:, 0:512], op=ALU.mult
+                )
+                nc.vector.tensor_tensor(
+                    out=ot[:, 512:OUT], in0=acc[(h, mi, 1)][:, 0:256], in1=spb[:, 512:OUT], op=ALU.mult
+                )
+                nc.vector.tensor_tensor(out=ot[:], in0=ot[:], in1=cm[m][:], op=ALU.add)
+                nc.sync.dma_start(out=outv[m], in_=ot[:])
+
+        nbanks = NF * NT
+        next_bank = 0
+        quant_due = []
+        for it in range(NU + 6):
+            if it < NU:
+                s1(it)
+            if 0 <= it - 1 < NU:
+                s2(it - 1)
+            if it == 1:
+                silu_part()
+            if it == 2:
+                bias_part()
+            if it == 3:
+                base_part()
+            if 0 <= it - 2 < NU:
+                s3(it - 2)
+            for f in quant_due:
+                w_quant(f)
+            quant_due = []
+            for i in range(BANKS_PER_IT):
+                if it >= 1 and next_bank < nbanks:
+                    w_bank(next_bank)
+                    if next_bank % NT == NT - 1:
+                        quant_due.append(next_bank // NT)
+                    next_bank += 1
+                    if next_bank == nbanks:
+                        make_xt(1, "w")
+            if 0 <= it - 3 < NU:
+                s4(it - 3)
+            if 0 <= it - 5 < NU:
+                s6(it - 5)
+                if (it - 5) % (NF * NG) == NF * NG - 1:
+                    finish((it - 5) // (NF * NG))
+            if 0 <= it - 4 < NU:
+                s5(it - 4)

@@ -27,10 +27,8 @@ NU = 2 * NF * NG
 
 FLOPS = 2 * TOK * K * OUT * (NF + 1)
 
-K_ON_G = (0,)
-K_MOD = 1
-T_UNITS = ()
-T_MOD = 1
+K_SET = tuple(range(32))
+T_SET = ()
 EV_ON_V = (3,)
 EV_MOD = 4
 BANKS_PER_IT = 4
@@ -105,6 +103,16 @@ def tile_efficient_skan_batch_kernel(
         cturn = const.tile([P, NF], F32, name="cturn")
         nc.vector.tensor_scalar(
             out=cturn[:], in0=g32[:], scalar1=1.0 / (2.0 * math.pi), scalar2=None, op0=ALU.mult
+        )
+        gzero = const.tile([P, NF], F32, name="gzero")
+        nc.vector.tensor_scalar(out=gzero[:], in0=g32[:], scalar1=0.0, scalar2=None, op0=ALU.is_equal)
+        gsafe = const.tile([P, NF], F32, name="gsafe")
+        nc.vector.tensor_add(out=gsafe[:], in0=g32[:], in1=gzero[:])
+        ginv = const.tile([P, NF], F32, name="ginv")
+        nc.vector.reciprocal(out=ginv[:], in_=gsafe[:])
+        negp = const.tile([P, NF], F32, name="negp")
+        nc.vector.tensor_scalar(
+            out=negp[:], in0=ginv[:], scalar1=-2.0 * math.pi, scalar2=None, op0=ALU.mult
         )
         coefT = const.tile([P, NF * NG * 4], F32, name="coefT")
         nc.vector.tensor_copy(
@@ -244,7 +252,7 @@ def tile_efficient_skan_batch_kernel(
         def s1(n):
             h, f, g = unit(n)
             kk = kpool.tile([P, 4 * HT], I32, name="kk")
-            if n % K_MOD in K_ON_G:
+            if n in K_SET:
                 nc.gpsimd.tensor_scalar(
                     out=kk[:], in0=xs[(h, g)][:], scalar1=cturn[:, f : f + 1], scalar2=0.0,
                     op0=ALU.mult, op1=ALU.add,
@@ -261,11 +269,11 @@ def tile_efficient_skan_batch_kernel(
             rr = rpool.tile([P, 4 * HT], F32, name="rr")
             nc.vector.scalar_tensor_tensor(
                 out=rr[:],
-                in0=xbank[(h, g)][:].rearrange("p u t -> p (u t)").bitcast(BF16),
-                scalar=cturn[:, f : f + 1],
-                in1=kt[n][:],
+                in0=kt[n][:],
+                scalar=negp[:, f : f + 1],
+                in1=xbank[(h, g)][:].rearrange("p u t -> p (u t)").bitcast(BF16),
                 op0=ALU.mult,
-                op1=ALU.subtract,
+                op1=ALU.add,
             )
             rt[n] = rr
 
@@ -273,17 +281,17 @@ def tile_efficient_skan_batch_kernel(
             h, f, g = unit(n)
             rr = rt[n]
             ci = (f * NG + g) * 4
-            if n % T_MOD in T_UNITS:
+            if n in T_SET:
                 sn = snpool.tile([P, HT, 4], F32, name="sn")
                 nc.scalar.activation(
                     out=sn[:].rearrange("p t (u e) -> p t u e", e=2),
                     in_=rr[:].rearrange("p (u t e) -> p t u e", u=2, e=2),
                     func=ACT.Sin,
-                    scale=2.0 * math.pi,
+                    scale=g32[:, f : f + 1],
                 )
                 sct[n] = sn
             else:
-                nc.scalar.activation(out=rr[:], in_=rr[:], func=ACT.Sin, scale=2.0 * math.pi)
+                nc.scalar.activation(out=rr[:], in_=rr[:], func=ACT.Sin, scale=g32[:, f : f + 1])
                 sc = scpool.tile([P, 4, HT], BF16, name="sc")
                 rv = rr[:].rearrange("p (u t e) -> p u e t", u=2, e=2)
                 for j in range(4):
@@ -299,7 +307,7 @@ def tile_efficient_skan_batch_kernel(
             h, f, g = unit(n)
             ci = (f * NG + g) * 4
             grp = gpool.tile([P, HT, 4], BF16, name="grp", align_bytes=64)
-            if n % T_MOD in T_UNITS:
+            if n in T_SET:
                 nc.vector.tensor_tensor(
                     out=grp[:],
                     in0=sct[n][:],

@@ -13,6 +13,7 @@ FP8X4 = mybir.dt.float8_e4m3fn_x4
 FP4X4 = mybir.dt.float4_e2m1fn_x4
 ACT = mybir.ActivationFunctionType
 ALU = mybir.AluOpType
+AX = mybir.AxisListType
 
 P = 128
 TOK = 512
@@ -27,12 +28,13 @@ NU = 2 * NF * NG
 
 FLOPS = 2 * TOK * K * OUT * (NF + 1)
 
-K_SET = tuple(range(32))
-T_SET = ()
-EV_ON_V = (3,)
-EV_MOD = 4
-BANKS_PER_IT = 4
+K_SET = ()
+T_SET = (0, 1, 3, 4, 6, 7, 9, 10, 12, 13)
+EV_SET = ()
+FIN_V = ()
+BANKS_PER_IT = 3
 PIN = False
+WB = 3
 
 
 def tile_efficient_skan_batch_kernel(
@@ -41,7 +43,7 @@ def tile_efficient_skan_batch_kernel(
     nc = tc.nc
     with ExitStack() as ctx:
         const = ctx.enter_context(tc.tile_pool(name="const", bufs=1))
-        wpool = ctx.enter_context(tc.tile_pool(name="wraw", bufs=2))
+        wpool = ctx.enter_context(tc.tile_pool(name="wraw", bufs=WB))
         wgpool = ctx.enter_context(tc.tile_pool(name="wg", bufs=2))
         kpool = ctx.enter_context(tc.tile_pool(name="k", bufs=3))
         rpool = ctx.enter_context(tc.tile_pool(name="r", bufs=3))
@@ -49,7 +51,7 @@ def tile_efficient_skan_batch_kernel(
         scpool = ctx.enter_context(tc.tile_pool(name="sc", bufs=3))
         gpool = ctx.enter_context(tc.tile_pool(name="grp", bufs=3))
         swpool = ctx.enter_context(tc.tile_pool(name="sw", bufs=6))
-        opool = ctx.enter_context(tc.tile_pool(name="o", bufs=2))
+        opool = ctx.enter_context(tc.tile_pool(name="o", bufs=3))
         psum = ctx.enter_context(tc.psum_pool(name="psum", bufs=2))
         if PIN:
             ctx.enter_context(tc.manual_schedule())
@@ -65,14 +67,14 @@ def tile_efficient_skan_batch_kernel(
         nc.scalar.dma_start(
             out=craw[:], in_=coef.rearrange("(g p j) f -> p g (j f)", g=NG, p=P)
         )
-        rb = const.tile([P, OUT], BF16, name="rb")
-        nc.gpsimd.memset(rb[:], 0.0)
-        rs = const.tile([P, OUT], BF16, name="rs")
-        nc.gpsimd.memset(rs[:], 0.0)
-        ones = const.tile([P, P], BF16, name="ones")
-        nc.gpsimd.memset(ones[:], 1.0)
-        nc.scalar.dma_start(out=rb[0:NF, :], in_=conv_b)
-        nc.scalar.dma_start(out=rs[0:1, :], in_=scale_sp.rearrange("(a o) -> a o", a=1))
+        braw = const.tile([P, P], BF16, name="braw")
+        nc.vector.memset(braw[:], 0.0)
+        nc.scalar.dma_start(
+            out=braw[0 : NF * NT, :], in_=conv_b.rearrange("f (t c) -> (f t) c", c=P)
+        )
+        nc.scalar.dma_start(
+            out=braw[NF * NT : NF * NT + NT, :], in_=scale_sp.rearrange("(t c) -> t c", c=P)
+        )
 
         w4w = const.tile([P, NG, 2 * OUT], U8, name="w4w", align_bytes=64)
         nc.sync.dma_start(
@@ -87,6 +89,8 @@ def tile_efficient_skan_batch_kernel(
 
         ident = const.tile([P, P], F32, name="ident")
         make_identity(nc, ident[:])
+        identb = const.tile([P, P], BF16, name="identb")
+        make_identity(nc, identb[:])
 
         raws = {}
 
@@ -95,7 +99,7 @@ def tile_efficient_skan_batch_kernel(
             nc.sync.dma_start(out=wraw[:], in_=conv_w[f].rearrange("(t p) k -> p t k", p=P))
             raws[f] = wraw
 
-        for f in range(2):
+        for f in range(WB):
             load_w(f)
 
         g32 = const.tile([P, NF], F32, name="g32")
@@ -104,28 +108,19 @@ def tile_efficient_skan_batch_kernel(
         nc.vector.tensor_scalar(
             out=cturn[:], in0=g32[:], scalar1=1.0 / (2.0 * math.pi), scalar2=None, op0=ALU.mult
         )
-        gzero = const.tile([P, NF], F32, name="gzero")
-        nc.vector.tensor_scalar(out=gzero[:], in0=g32[:], scalar1=0.0, scalar2=None, op0=ALU.is_equal)
-        gsafe = const.tile([P, NF], F32, name="gsafe")
-        nc.vector.tensor_add(out=gsafe[:], in0=g32[:], in1=gzero[:])
-        ginv = const.tile([P, NF], F32, name="ginv")
-        nc.vector.reciprocal(out=ginv[:], in_=gsafe[:])
-        negp = const.tile([P, NF], F32, name="negp")
-        nc.vector.tensor_scalar(
-            out=negp[:], in0=ginv[:], scalar1=-2.0 * math.pi, scalar2=None, op0=ALU.mult
-        )
         coefT = const.tile([P, NF * NG * 4], F32, name="coefT")
         nc.vector.tensor_copy(
             out=coefT[:].rearrange("p (f g j) -> p f g j", f=NF, g=NG),
             in_=craw[:].rearrange("p g (j f) -> p f g j", f=NF),
         )
 
-        xbank = {}
         xs = {}
+        xbank = {}
+        silu_g = const.tile([P, NG, TOK, 4], BF16, name="silu_g", align_bytes=64)
 
-        def make_xt(h, tag):
+        def make_xt(h):
             for g in range(NG):
-                xb = psum.tile([P, 2, HT], F32, tag=tag, name="xb")
+                xb = psum.tile([P, 2, HT], F32, tag="acc", bufs=6, name="xb")
                 for mi in range(2):
                     xw = x_sb[:, 2 * h + mi, :].bitcast(F32)
                     for u in range(2):
@@ -136,10 +131,18 @@ def tile_efficient_skan_batch_kernel(
                         )
                 xc = const.tile([P, 4 * HT], BF16, name="xs%d%d" % (h, g))
                 nc.scalar.copy(out=xc[:].bitcast(F32), in_=xb[:].rearrange("p u t -> p (u t)"))
-                xbank[(h, g)] = xb
                 xs[(h, g)] = xc
+                xbank[(h, g)] = xb
 
-        make_xt(0, "x")
+        def silu_part(h):
+            for g in range(NG):
+                nc.scalar.activation(
+                    out=silu_g[:, g, h * HT : (h + 1) * HT, :].rearrange("p t (u e) -> p t u e", e=2),
+                    in_=xbank[(h, g)][:].bitcast(BF16).rearrange("p u (t e) -> p t u e", e=2),
+                    func=ACT.Silu,
+                )
+
+        make_xt(0)
 
         wgs = {}
         wqs = {}
@@ -147,70 +150,51 @@ def tile_efficient_skan_batch_kernel(
         def w_bank(b):
             f, t = divmod(b, NT)
             if t == 0:
-                wgs[f] = wgpool.tile([P, NG, OUT, 4], BF16, name="wg", align_bytes=64)
-            wgw = wgs[f][:].rearrange("p g o j -> p g (o j)").bitcast(F32)
+                wgs[f] = wgpool.tile([P, NT * NG * P * 4], BF16, name="wg", align_bytes=64)
+            wgw = wgs[f][:].bitcast(F32)
             ww = raws[f][:, t, :].bitcast(F32)
             wps = psum.tile([P, 4, P], F32, tag="w", name="wps")
             for q in range(4):
                 g, u = divmod(q, 2)
                 nc.tensor.transpose(wps[:, q, :], ww[:, 256 * g + u : 256 * (g + 1) : 2], ident[:])
-            dst = wgw[:, :, 2 * P * t : 2 * P * (t + 1)].rearrange("p g (o u) -> p g o u", u=2)
+            dst = wgw[:, 512 * t : 512 * (t + 1)].rearrange("p (g o u) -> p g o u", g=NG, u=2)
             src = wps[:].rearrange("p (g u) o -> p g o u", u=2)
-            if b % EV_MOD in EV_ON_V:
+            if b in EV_SET:
                 nc.vector.tensor_copy(out=dst, in_=src)
             else:
                 nc.scalar.copy(out=dst, in_=src)
-            if t == NT - 1 and f + 2 < NF:
-                load_w(f + 2)
+            if t == NT - 1 and f + WB < NF:
+                load_w(f + WB)
 
         def w_quant(f):
-            wq = const.tile([P, NG * OUT], U32, name="wq%d" % f, align_bytes=64)
-            wsc = const.tile([P, NG * OUT], U8, name="wsc%d" % f, align_bytes=64)
-            wgf = wgs[f][:].rearrange("p g o j -> p (g o j)")
+            wq = const.tile([P, NT * NG * P], U32, name="wq%d" % f, align_bytes=64)
+            wsc = const.tile([P, NT * NG * P], U8, name="wsc%d" % f, align_bytes=64)
             for c in range(3):
                 nc.vector.quantize_mx(
                     out=wq[:, 512 * c : 512 * (c + 1)].bitcast(FP8X4),
                     scales=wsc[:, 512 * c : 512 * (c + 1)],
-                    in_=wgf[:, 2048 * c : 2048 * (c + 1)],
+                    in_=wgs[f][:, 2048 * c : 2048 * (c + 1)],
                 )
             wqs[f] = (wq, wsc)
 
-        silu_g = const.tile([P, NG, TOK, 4], BF16, name="silu_g", align_bytes=64)
+        bT = const.tile([P, 64], F32, name="bT")
+        bsum = const.tile([P, NT], F32, name="bsum")
+        sbs = const.tile([P, NT], F32, name="sbs")
         sil_w = const.tile([P, NG, TOK], U32, name="sil_w", align_bytes=64)
         sil_s = const.tile([P, NG, TOK], U8, name="sil_s", align_bytes=64)
-        spb = const.tile([P, OUT], F32, name="spb")
-        sbb = const.tile([P, OUT], F32, name="sbb")
-        cm = [const.tile([P, OUT], F32, name="cm%d" % m) for m in range(NM)]
-
-        def silu_part():
-            for m in range(NM):
-                xw = x_sb[:, m, :].bitcast(F32)
-                xpa = psum.tile([P, 4, P], F32, tag="acc", bufs=4, name="xpa")
-                for q in range(4):
-                    g, u = divmod(q, 2)
-                    nc.tensor.transpose(
-                        xpa[:, q, :], xw[:, 256 * g + u : 256 * (g + 1) : 2], ident[:]
-                    )
-                xab = xpa[:].bitcast(BF16)
-                for g in range(NG):
-                    nc.scalar.activation(
-                        out=silu_g[:, g, m * P : (m + 1) * P, :].rearrange(
-                            "p t (u e) -> p t u e", e=2
-                        ),
-                        in_=xab[:, 2 * g : 2 * g + 2, :].rearrange("p u (t e) -> p t u e", e=2),
-                        func=ACT.Silu,
-                    )
+        basec = []
 
         def bias_part():
-            for lo, hi in ((0, 512), (512, OUT)):
-                sps = psum.tile([P, 512], F32, tag="w", name="sps")
-                nc.tensor.matmul(sps[:, 0 : hi - lo], lhsT=ones[:], rhs=rs[:, lo:hi], start=True, stop=True)
-                nc.scalar.copy(out=spb[:, lo:hi], in_=sps[:, 0 : hi - lo])
-                bps = psum.tile([P, 512], F32, tag="w", name="bps")
-                nc.tensor.matmul(bps[:, 0 : hi - lo], lhsT=ones[:], rhs=rb[:, lo:hi], start=True, stop=True)
-                nc.vector.tensor_tensor(
-                    out=sbb[:, lo:hi], in0=bps[:, 0 : hi - lo], in1=spb[:, lo:hi], op=ALU.mult
-                )
+            bps = psum.tile([P, P], BF16, tag="w", name="bps")
+            nc.tensor.transpose(bps[:], braw[:], identb[:])
+            nc.vector.tensor_copy(out=bT[:, 0 : NF * NT + NT], in_=bps[:, 0 : NF * NT + NT])
+            nc.vector.tensor_reduce(
+                out=bsum[:],
+                in_=bT[:, 0 : NF * NT].rearrange("p (f t) -> p t f", t=NT),
+                axis=AX.X,
+                op=ALU.add,
+            )
+            nc.vector.tensor_mul(out=sbs[:], in0=bsum[:], in1=bT[:, NF * NT : NF * NT + NT])
 
         def base_part():
             nc.vector.quantize_mx(
@@ -218,31 +202,28 @@ def tile_efficient_skan_batch_kernel(
                 scales=sil_s[:].rearrange("p g t -> p (g t)"),
                 in_=silu_g[:].rearrange("p g t j -> p (g t j)"),
             )
-            for m in range(NM):
-                ba = psum.tile([P, 512], F32, tag="acc", bufs=4, name="ba")
-                bb = psum.tile([P, 512], F32, tag="acc", bufs=4, name="bb")
-                for dst, lo, n in ((ba[:, 0:512], 0, 512), (bb[:, 0:128], 512, 128), (bb[:, 128:256], 640, 128)):
-                    for g in range(NG):
-                        nc.tensor.matmul_mx(
-                            out=dst,
-                            lhsT=sil_w[:, g, m * P : (m + 1) * P].bitcast(FP8X4),
-                            lhsT_scale=sil_s[:, g, m * P : (m + 1) * P],
-                            rhs=w4w[:, g, 2 * lo : 2 * (lo + n)].bitcast(FP4X4),
-                            rhs_scale=w4s[:, g, lo : lo + n],
-                            start=(g == 0),
-                            stop=(g == NG - 1),
-                        )
-                nc.vector.tensor_tensor(out=cm[m][:, 0:512], in0=ba[:], in1=sbb[:, 0:512], op=ALU.add)
-                nc.vector.tensor_tensor(
-                    out=cm[m][:, 512:OUT], in0=bb[:, 0:256], in1=sbb[:, 512:OUT], op=ALU.add
-                )
+            for t in range(NT):
+                bacc = psum.tile([P, TOK], F32, tag="acc", bufs=6, name="bacc")
+                for g in range(NG):
+                    nc.tensor.matmul_mx(
+                        out=bacc[:],
+                        lhsT=w4w[:, g, 2 * P * t : 2 * P * (t + 1)].bitcast(FP4X4),
+                        lhsT_scale=w4s[:, g, P * t : P * (t + 1)],
+                        rhs=sil_w[:, g, :].bitcast(FP8X4),
+                        rhs_scale=sil_s[:, g, :],
+                        start=(g == 0),
+                        stop=(g == NG - 1),
+                    )
+                bc = const.tile([P, TOK], F32, name="basec%d" % t)
+                nc.scalar.activation(out=bc[:], in_=bacc[:], func=ACT.Identity, bias=sbs[:, t : t + 1])
+                basec.append(bc)
 
         kt = {}
         rt = {}
         sct = {}
         grt = {}
         swt = {}
-        acc = {}
+        acc = []
 
         def unit(n):
             h, rest = divmod(n, NF * NG)
@@ -269,11 +250,11 @@ def tile_efficient_skan_batch_kernel(
             rr = rpool.tile([P, 4 * HT], F32, name="rr")
             nc.vector.scalar_tensor_tensor(
                 out=rr[:],
-                in0=kt[n][:],
-                scalar=negp[:, f : f + 1],
-                in1=xbank[(h, g)][:].rearrange("p u t -> p (u t)").bitcast(BF16),
+                in0=xs[(h, g)][:],
+                scalar=cturn[:, f : f + 1],
+                in1=kt[n][:],
                 op0=ALU.mult,
-                op1=ALU.add,
+                op1=ALU.subtract,
             )
             rt[n] = rr
 
@@ -287,11 +268,11 @@ def tile_efficient_skan_batch_kernel(
                     out=sn[:].rearrange("p t (u e) -> p t u e", e=2),
                     in_=rr[:].rearrange("p (u t e) -> p t u e", u=2, e=2),
                     func=ACT.Sin,
-                    scale=g32[:, f : f + 1],
+                    scale=2.0 * math.pi,
                 )
                 sct[n] = sn
             else:
-                nc.scalar.activation(out=rr[:], in_=rr[:], func=ACT.Sin, scale=g32[:, f : f + 1])
+                nc.scalar.activation(out=rr[:], in_=rr[:], func=ACT.Sin, scale=2.0 * math.pi)
                 sc = scpool.tile([P, 4, HT], BF16, name="sc")
                 rv = rr[:].rearrange("p (u t e) -> p u e t", u=2, e=2)
                 for j in range(4):
@@ -331,38 +312,49 @@ def tile_efficient_skan_batch_kernel(
 
         def s6(n):
             h, f, g = unit(n)
-            if f == 0 and g == 0:
-                for mi in range(2):
-                    acc[(h, mi, 0)] = psum.tile([P, 512], F32, tag="acc", bufs=4, name="acca")
-                    acc[(h, mi, 1)] = psum.tile([P, 512], F32, tag="acc", bufs=4, name="accb")
+            if n == 0:
+                for t in range(NT):
+                    acc.append(psum.tile([P, TOK], F32, tag="acc", bufs=6, name="acc%d" % t))
             sw, ss = swt[n]
             wq, wsc = wqs[f]
-            for mi in range(2):
-                for part, lo, nn in ((0, 0, 512), (1, 512, 256)):
-                    nc.tensor.matmul_mx(
-                        out=acc[(h, mi, part)][:, 0:nn],
-                        lhsT=sw[:, mi * P : (mi + 1) * P].bitcast(FP8X4),
-                        lhsT_scale=ss[:, mi * P : (mi + 1) * P],
-                        rhs=wq[:, g * OUT + lo : g * OUT + lo + nn].bitcast(FP8X4),
-                        rhs_scale=wsc[:, g * OUT + lo : g * OUT + lo + nn],
-                        start=(f == 0 and g == 0),
-                        stop=(f == NF - 1 and g == NG - 1),
-                    )
+            for t in range(NT):
+                lo = (t * NG + g) * P
+                nc.tensor.matmul_mx(
+                    out=acc[t][:, h * HT : (h + 1) * HT],
+                    lhsT=wq[:, lo : lo + P].bitcast(FP8X4),
+                    lhsT_scale=wsc[:, lo : lo + P],
+                    rhs=sw[:].bitcast(FP8X4),
+                    rhs_scale=ss[:],
+                    start=(f == 0 and g == 0),
+                    stop=(f == NF - 1 and g == NG - 1),
+                )
 
-        outv = out.rearrange("b n o -> (b n) o").rearrange("(m p) o -> m p o", p=P)
+        outv = out.rearrange("b n o -> (b n) o").rearrange("(m p) o -> p m o", p=P)
 
         def finish(h):
-            for mi in range(2):
-                m = 2 * h + mi
-                ot = opool.tile([P, OUT], F32, name="ot")
-                nc.vector.tensor_tensor(
-                    out=ot[:, 0:512], in0=acc[(h, mi, 0)][:], in1=spb[:, 0:512], op=ALU.mult
+            for tp in range(NT // 2):
+                fps = psum.tile([P, 2, 2, P], F32, tag="w", name="fps")
+                for tt in range(2):
+                    t = 2 * tp + tt
+                    ot = opool.tile([P, HT], F32, name="ot")
+                    nc.vector.scalar_tensor_tensor(
+                        out=ot[:],
+                        in0=acc[t][:, h * HT : (h + 1) * HT],
+                        scalar=bT[:, NF * NT + t : NF * NT + t + 1],
+                        in1=basec[t][:, h * HT : (h + 1) * HT],
+                        op0=ALU.mult,
+                        op1=ALU.add,
+                    )
+                    for mi in range(2):
+                        nc.tensor.transpose(fps[:, mi, tt, :], ot[:, mi * P : (mi + 1) * P], ident[:])
+                of = opool.tile([P, 2, 2 * P], F32, name="of")
+                if (h, tp) in FIN_V:
+                    nc.vector.tensor_copy(out=of[:], in_=fps[:].rearrange("p m t o -> p m (t o)"))
+                else:
+                    nc.scalar.copy(out=of[:], in_=fps[:].rearrange("p m t o -> p m (t o)"))
+                nc.sync.dma_start(
+                    out=outv[:, 2 * h : 2 * h + 2, 2 * P * tp : 2 * P * (tp + 1)], in_=of[:]
                 )
-                nc.vector.tensor_tensor(
-                    out=ot[:, 512:OUT], in0=acc[(h, mi, 1)][:, 0:256], in1=spb[:, 512:OUT], op=ALU.mult
-                )
-                nc.vector.tensor_tensor(out=ot[:], in0=ot[:], in1=cm[m][:], op=ALU.add)
-                nc.sync.dma_start(out=outv[m], in_=ot[:])
 
         nbanks = NF * NT
         next_bank = 0
@@ -373,7 +365,9 @@ def tile_efficient_skan_batch_kernel(
             if 0 <= it - 1 < NU:
                 s2(it - 1)
             if it == 1:
-                silu_part()
+                make_xt(1)
+                silu_part(0)
+                silu_part(1)
             if it == 2:
                 bias_part()
             if it == 3:
@@ -389,8 +383,6 @@ def tile_efficient_skan_batch_kernel(
                     if next_bank % NT == NT - 1:
                         quant_due.append(next_bank // NT)
                     next_bank += 1
-                    if next_bank == nbanks:
-                        make_xt(1, "w")
             if 0 <= it - 3 < NU:
                 s4(it - 3)
             if 0 <= it - 5 < NU:

@@ -24,17 +24,15 @@ NG = 2
 NT = OUT // P
 NM = TOK // P
 HT = 256
-NU = 2 * NF * NG
 
 FLOPS = 2 * TOK * K * OUT * (NF + 1)
 
-K_SET = ()
-T_SET = (0, 1, 3, 4, 6, 7, 9, 10, 12, 13)
+SPLIT_F = (0, 7)
+T_SET = (0, 1, 6, 12, 18)
 EV_SET = ()
-FIN_V = ()
-BANKS_PER_IT = 3
-PIN = False
-WB = 3
+FIN_V = (1, 3, 5)
+LEAD = 6
+WB = 2
 
 
 def tile_efficient_skan_batch_kernel(
@@ -45,16 +43,16 @@ def tile_efficient_skan_batch_kernel(
         const = ctx.enter_context(tc.tile_pool(name="const", bufs=1))
         wpool = ctx.enter_context(tc.tile_pool(name="wraw", bufs=WB))
         wgpool = ctx.enter_context(tc.tile_pool(name="wg", bufs=2))
+        wqpool = ctx.enter_context(tc.tile_pool(name="wq", bufs=3))
         kpool = ctx.enter_context(tc.tile_pool(name="k", bufs=3))
         rpool = ctx.enter_context(tc.tile_pool(name="r", bufs=3))
         snpool = ctx.enter_context(tc.tile_pool(name="sn", bufs=2))
         scpool = ctx.enter_context(tc.tile_pool(name="sc", bufs=3))
         gpool = ctx.enter_context(tc.tile_pool(name="grp", bufs=3))
-        swpool = ctx.enter_context(tc.tile_pool(name="sw", bufs=6))
-        opool = ctx.enter_context(tc.tile_pool(name="o", bufs=3))
+        swpool = ctx.enter_context(tc.tile_pool(name="sw", bufs=4))
+        otpool = ctx.enter_context(tc.tile_pool(name="ot", bufs=3))
+        ofpool = ctx.enter_context(tc.tile_pool(name="of", bufs=4))
         psum = ctx.enter_context(tc.psum_pool(name="psum", bufs=2))
-        if PIN:
-            ctx.enter_context(tc.manual_schedule())
 
         xv = x.rearrange("b n k -> (b n) k").rearrange("(m p) k -> m p k", p=P)
         x_sb = const.tile([P, NM, K], BF16, name="x_sb")
@@ -114,7 +112,7 @@ def tile_efficient_skan_batch_kernel(
             in_=craw[:].rearrange("p g (j f) -> p f g j", f=NF),
         )
 
-        xs = {}
+        xs = [const.tile([P, 2, TOK, 2], BF16, name="xs%d" % g) for g in range(NG)]
         xbank = {}
         silu_g = const.tile([P, NG, TOK, 4], BF16, name="silu_g", align_bytes=64)
 
@@ -129,9 +127,12 @@ def tile_efficient_skan_batch_kernel(
                             xw[:, 256 * g + u : 256 * (g + 1) : 2],
                             ident[:],
                         )
-                xc = const.tile([P, 4 * HT], BF16, name="xs%d%d" % (h, g))
-                nc.scalar.copy(out=xc[:].bitcast(F32), in_=xb[:].rearrange("p u t -> p (u t)"))
-                xs[(h, g)] = xc
+                nc.scalar.copy(
+                    out=xs[g][:].rearrange("p u t e -> p u (t e)").bitcast(F32)[
+                        :, :, h * HT : (h + 1) * HT
+                    ],
+                    in_=xb[:],
+                )
                 xbank[(h, g)] = xb
 
         def silu_part(h):
@@ -143,6 +144,7 @@ def tile_efficient_skan_batch_kernel(
                 )
 
         make_xt(0)
+        make_xt(1)
 
         wgs = {}
         wqs = {}
@@ -167,13 +169,13 @@ def tile_efficient_skan_batch_kernel(
                 load_w(f + WB)
 
         def w_quant(f):
-            wq = const.tile([P, NT * NG * P], U32, name="wq%d" % f, align_bytes=64)
-            wsc = const.tile([P, NT * NG * P], U8, name="wsc%d" % f, align_bytes=64)
-            for c in range(3):
+            wq = wqpool.tile([P, NT * NG * P], U32, name="wq", align_bytes=64)
+            wsc = wqpool.tile([P, NT * NG * P], U8, name="wsc", align_bytes=64)
+            for lo, n in ((0, 1024), (1024, 512)):
                 nc.vector.quantize_mx(
-                    out=wq[:, 512 * c : 512 * (c + 1)].bitcast(FP8X4),
-                    scales=wsc[:, 512 * c : 512 * (c + 1)],
-                    in_=wgs[f][:, 2048 * c : 2048 * (c + 1)],
+                    out=wq[:, lo : lo + n].bitcast(FP8X4),
+                    scales=wsc[:, lo : lo + n],
+                    in_=wgs[f][:, 4 * lo : 4 * (lo + n)],
                 )
             wqs[f] = (wq, wsc)
 
@@ -218,6 +220,16 @@ def tile_efficient_skan_batch_kernel(
                 nc.scalar.activation(out=bc[:], in_=bacc[:], func=ACT.Identity, bias=sbs[:, t : t + 1])
                 basec.append(bc)
 
+        units = []
+        for f in range(NF):
+            for g in range(NG):
+                if f in SPLIT_F:
+                    units.append((f, g, 0, HT))
+                    units.append((f, g, HT, TOK))
+                else:
+                    units.append((f, g, 0, TOK))
+        nu = len(units)
+
         kt = {}
         rt = {}
         sct = {}
@@ -225,74 +237,66 @@ def tile_efficient_skan_batch_kernel(
         swt = {}
         acc = []
 
-        def unit(n):
-            h, rest = divmod(n, NF * NG)
-            f, g = divmod(rest, NG)
-            return h, f, g
-
         def s1(n):
-            h, f, g = unit(n)
-            kk = kpool.tile([P, 4 * HT], I32, name="kk")
-            if n in K_SET:
-                nc.gpsimd.tensor_scalar(
-                    out=kk[:], in0=xs[(h, g)][:], scalar1=cturn[:, f : f + 1], scalar2=0.0,
-                    op0=ALU.mult, op1=ALU.add,
-                )
-            else:
-                nc.vector.tensor_scalar(
-                    out=kk[:], in0=xs[(h, g)][:], scalar1=cturn[:, f : f + 1], scalar2=None,
-                    op0=ALU.mult,
-                )
+            f, g, t0, t1 = units[n]
+            kk = kpool.tile([P, 2, t1 - t0, 2], I32, name="kk")
+            nc.vector.tensor_scalar(
+                out=kk[:].rearrange("p u t e -> p u (t e)"),
+                in0=xs[g][:, :, t0:t1, :].rearrange("p u t e -> p u (t e)"),
+                scalar1=cturn[:, f : f + 1],
+                scalar2=None,
+                op0=ALU.mult,
+            )
             kt[n] = kk
 
         def s2(n):
-            h, f, g = unit(n)
-            rr = rpool.tile([P, 4 * HT], F32, name="rr")
+            f, g, t0, t1 = units[n]
+            rr = rpool.tile([P, 2, t1 - t0, 2], F32, name="rr")
             nc.vector.scalar_tensor_tensor(
-                out=rr[:],
-                in0=xs[(h, g)][:],
+                out=rr[:].rearrange("p u t e -> p u (t e)"),
+                in0=xs[g][:, :, t0:t1, :].rearrange("p u t e -> p u (t e)"),
                 scalar=cturn[:, f : f + 1],
-                in1=kt[n][:],
+                in1=kt[n][:].rearrange("p u t e -> p u (t e)"),
                 op0=ALU.mult,
                 op1=ALU.subtract,
             )
             rt[n] = rr
 
         def s3(n):
-            h, f, g = unit(n)
+            f, g, t0, t1 = units[n]
             rr = rt[n]
             ci = (f * NG + g) * 4
             if n in T_SET:
-                sn = snpool.tile([P, HT, 4], F32, name="sn")
+                sn = snpool.tile([P, t1 - t0, 4], F32, name="sn")
                 nc.scalar.activation(
                     out=sn[:].rearrange("p t (u e) -> p t u e", e=2),
-                    in_=rr[:].rearrange("p (u t e) -> p t u e", u=2, e=2),
+                    in_=rr[:].rearrange("p u t e -> p t u e"),
                     func=ACT.Sin,
                     scale=2.0 * math.pi,
                 )
                 sct[n] = sn
             else:
-                nc.scalar.activation(out=rr[:], in_=rr[:], func=ACT.Sin, scale=2.0 * math.pi)
-                sc = scpool.tile([P, 4, HT], BF16, name="sc")
-                rv = rr[:].rearrange("p (u t e) -> p u e t", u=2, e=2)
+                flat = rr[:].rearrange("p u t e -> p (u t e)")
+                nc.scalar.activation(out=flat, in_=flat, func=ACT.Sin, scale=2.0 * math.pi)
+                sc = scpool.tile([P, 4, t1 - t0], BF16, name="sc")
                 for j in range(4):
                     nc.scalar.activation(
                         out=sc[:, j, :],
-                        in_=rv[:, j // 2, j % 2, :],
+                        in_=rr[:, j // 2, :, j % 2],
                         func=ACT.Copy,
                         scale=coefT[:, ci + j : ci + j + 1],
                     )
                 sct[n] = sc
 
         def s4(n):
-            h, f, g = unit(n)
+            f, g, t0, t1 = units[n]
             ci = (f * NG + g) * 4
-            grp = gpool.tile([P, HT, 4], BF16, name="grp", align_bytes=64)
+            grp = gpool.tile([P, t1 - t0, 4], BF16, name="grp", align_bytes=64)
             if n in T_SET:
                 nc.vector.tensor_tensor(
                     out=grp[:],
                     in0=sct[n][:],
-                    in1=coefT[:, ci : ci + 4].unsqueeze(1).to_broadcast([P, HT, 4]),
+                    in1=coefT[:, ci : ci + 4].unsqueeze(1).to_broadcast([P, t1 - t0, 4]),
                     op=ALU.mult,
                 )
             else:
@@ -303,24 +307,31 @@ def tile_efficient_skan_batch_kernel(
             grt[n] = grp
 
         def s5(n):
-            sw = swpool.tile([P, HT], U32, name="sw", align_bytes=64)
-            ss = swpool.tile([P, HT], U8, name="ss", align_bytes=64)
+            f, g, t0, t1 = units[n]
+            if t0 == 0:
+                sw = swpool.tile([P, TOK], U32, name="sw", align_bytes=64)
+                ss = swpool.tile([P, TOK], U8, name="ss", align_bytes=64)
+                swt[(f, g)] = (sw, ss)
+            sw, ss = swt[(f, g)]
             nc.vector.quantize_mx(
-                out=sw[:].bitcast(FP8X4), scales=ss[:], in_=grt[n][:].rearrange("p t j -> p (t j)")
+                out=sw[:, t0:t1].bitcast(FP8X4),
+                scales=ss[:, t0:t1],
+                in_=grt[n][:].rearrange("p t j -> p (t j)"),
             )
-            swt[n] = (sw, ss)
 
         def s6(n):
-            h, f, g = unit(n)
-            if n == 0:
+            f, g, t0, t1 = units[n]
+            if t1 != TOK:
+                return
+            if f == 0 and g == 0:
                 for t in range(NT):
                     acc.append(psum.tile([P, TOK], F32, tag="acc", bufs=6, name="acc%d" % t))
-            sw, ss = swt[n]
+            sw, ss = swt[(f, g)]
             wq, wsc = wqs[f]
             for t in range(NT):
                 lo = (t * NG + g) * P
                 nc.tensor.matmul_mx(
-                    out=acc[t][:, h * HT : (h + 1) * HT],
+                    out=acc[t][:],
                     lhsT=wq[:, lo : lo + P].bitcast(FP8X4),
                     lhsT_scale=wsc[:, lo : lo + P],
                     rhs=sw[:].bitcast(FP8X4),
@@ -331,63 +342,62 @@ def tile_efficient_skan_batch_kernel(
 
         outv = out.rearrange("b n o -> (b n) o").rearrange("(m p) o -> p m o", p=P)
 
-        def finish(h):
-            for tp in range(NT // 2):
-                fps = psum.tile([P, 2, 2, P], F32, tag="w", name="fps")
-                for tt in range(2):
-                    t = 2 * tp + tt
-                    ot = opool.tile([P, HT], F32, name="ot")
-                    nc.vector.scalar_tensor_tensor(
-                        out=ot[:],
-                        in0=acc[t][:, h * HT : (h + 1) * HT],
-                        scalar=bT[:, NF * NT + t : NF * NT + t + 1],
-                        in1=basec[t][:, h * HT : (h + 1) * HT],
-                        op0=ALU.mult,
-                        op1=ALU.add,
-                    )
-                    for mi in range(2):
-                        nc.tensor.transpose(fps[:, mi, tt, :], ot[:, mi * P : (mi + 1) * P], ident[:])
-                of = opool.tile([P, 2, 2 * P], F32, name="of")
-                if (h, tp) in FIN_V:
-                    nc.vector.tensor_copy(out=of[:], in_=fps[:].rearrange("p m t o -> p m (t o)"))
-                else:
-                    nc.scalar.copy(out=of[:], in_=fps[:].rearrange("p m t o -> p m (t o)"))
-                nc.sync.dma_start(
-                    out=outv[:, 2 * h : 2 * h + 2, 2 * P * tp : 2 * P * (tp + 1)], in_=of[:]
+        def finish():
+            for t in range(NT):
+                ot = otpool.tile([P, TOK], F32, name="ot")
+                nc.vector.scalar_tensor_tensor(
+                    out=ot[:],
+                    in0=acc[t][:],
+                    scalar=bT[:, NF * NT + t : NF * NT + t + 1],
+                    in1=basec[t][:],
+                    op0=ALU.mult,
+                    op1=ALU.add,
                 )
+                fps = psum.tile([P, NM, P], F32, tag="acc", bufs=6, name="fps")
+                for m in range(NM):
+                    nc.tensor.transpose(fps[:, m, :], ot[:, m * P : (m + 1) * P], ident[:])
+                of = ofpool.tile([P, NM, P], F32, name="of")
+                if t in FIN_V:
+                    nc.vector.tensor_copy(out=of[:], in_=fps[:])
+                else:
+                    nc.scalar.copy(out=of[:], in_=fps[:])
+                nc.sync.dma_start(out=outv[:, :, t * P : (t + 1) * P], in_=of[:])
 
         nbanks = NF * NT
+        total_cols = sum(t1 - t0 for (f, g, t0, t1) in units)
         next_bank = 0
+        done_cols = 0
         quant_due = []
-        for it in range(NU + 6):
-            if it < NU:
+        for it in range(nu + 6):
+            if it < nu:
                 s1(it)
-            if 0 <= it - 1 < NU:
+            if 0 <= it - 1 < nu:
                 s2(it - 1)
             if it == 1:
-                make_xt(1)
                 silu_part(0)
                 silu_part(1)
             if it == 2:
                 bias_part()
             if it == 3:
                 base_part()
-            if 0 <= it - 2 < NU:
+            if 0 <= it - 2 < nu:
                 s3(it - 2)
             for f in quant_due:
                 w_quant(f)
             quant_due = []
-            for i in range(BANKS_PER_IT):
-                if it >= 1 and next_bank < nbanks:
-                    w_bank(next_bank)
-                    if next_bank % NT == NT - 1:
-                        quant_due.append(next_bank // NT)
-                    next_bank += 1
-            if 0 <= it - 3 < NU:
+            if it < nu:
+                done_cols += units[it][3] - units[it][2]
+            want = min(nbanks, LEAD + (done_cols * (nbanks - LEAD) + total_cols - 1) // total_cols)
+            while next_bank < want:
+                w_bank(next_bank)
+                if next_bank % NT == NT - 1:
+                    quant_due.append(next_bank // NT)
+                next_bank += 1
+            if 0 <= it - 3 < nu:
                 s4(it - 3)
-            if 0 <= it - 5 < NU:
+            if 0 <= it - 5 < nu:
                 s6(it - 5)
-                if (it - 5) % (NF * NG) == NF * NG - 1:
-                    finish((it - 5) // (NF * NG))
-            if 0 <= it - 4 < NU:
+                if it - 5 == nu - 1:
+                    finish()
+            if 0 <= it - 4 < nu:
                 s5(it - 4)

@@ -24,14 +24,14 @@ NG = 2
 NT = OUT // P
 NM = TOK // P
 HT = 256
+NU = 2 * NF * NG
 
 FLOPS = 2 * TOK * K * OUT * (NF + 1)
 
-SPLIT_F = (0, 7)
-T_SET = (0, 1, 6, 12, 18)
+T_SET = (0, 1, 3, 4, 6, 7, 9, 10, 12, 13)
 EV_SET = ()
-FIN_V = (1, 3, 5)
-LEAD = 6
+FIN_V = ()
+BANKS_PER_IT = 3
 WB = 2
 
 
@@ -43,15 +43,13 @@ def tile_efficient_skan_batch_kernel(
         const = ctx.enter_context(tc.tile_pool(name="const", bufs=1))
         wpool = ctx.enter_context(tc.tile_pool(name="wraw", bufs=WB))
         wgpool = ctx.enter_context(tc.tile_pool(name="wg", bufs=2))
-        wqpool = ctx.enter_context(tc.tile_pool(name="wq", bufs=3))
-        kpool = ctx.enter_context(tc.tile_pool(name="k", bufs=3))
+        kpool = ctx.enter_context(tc.tile_pool(name="k", bufs=2))
         rpool = ctx.enter_context(tc.tile_pool(name="r", bufs=3))
         snpool = ctx.enter_context(tc.tile_pool(name="sn", bufs=2))
         scpool = ctx.enter_context(tc.tile_pool(name="sc", bufs=3))
-        gpool = ctx.enter_context(tc.tile_pool(name="grp", bufs=3))
-        swpool = ctx.enter_context(tc.tile_pool(name="sw", bufs=4))
-        otpool = ctx.enter_context(tc.tile_pool(name="ot", bufs=3))
-        ofpool = ctx.enter_context(tc.tile_pool(name="of", bufs=4))
+        gpool = ctx.enter_context(tc.tile_pool(name="grp", bufs=2))
+        swpool = ctx.enter_context(tc.tile_pool(name="sw", bufs=3))
+        opool = ctx.enter_context(tc.tile_pool(name="o", bufs=3))
         psum = ctx.enter_context(tc.psum_pool(name="psum", bufs=2))
 
         xv = x.rearrange("b n k -> (b n) k").rearrange("(m p) k -> m p k", p=P)
@@ -112,7 +110,7 @@ def tile_efficient_skan_batch_kernel(
             in_=craw[:].rearrange("p g (j f) -> p f g j", f=NF),
         )
 
-        xs = [const.tile([P, 2, TOK, 2], BF16, name="xs%d" % g) for g in range(NG)]
+        xs = {}
         xbank = {}
         silu_g = const.tile([P, NG, TOK, 4], BF16, name="silu_g", align_bytes=64)
 
@@ -127,12 +125,9 @@ def tile_efficient_skan_batch_kernel(
                             xw[:, 256 * g + u : 256 * (g + 1) : 2],
                             ident[:],
                         )
-                nc.scalar.copy(
-                    out=xs[g][:].rearrange("p u t e -> p u (t e)").bitcast(F32)[
-                        :, :, h * HT : (h + 1) * HT
-                    ],
-                    in_=xb[:],
-                )
+                if g == 0:
+                    xs[h] = const.tile([P, NG, 4 * HT], BF16, name="xs%d" % h)
+                nc.scalar.copy(out=xs[h][:, g, :].bitcast(F32), in_=xb[:].rearrange("p u t -> p (u t)"))
                 xbank[(h, g)] = xb
 
         def silu_part(h):
@@ -144,7 +139,6 @@ def tile_efficient_skan_batch_kernel(
                 )
 
         make_xt(0)
-        make_xt(1)
 
         wgs = {}
         wqs = {}
@@ -169,8 +163,8 @@ def tile_efficient_skan_batch_kernel(
                 load_w(f + WB)
 
         def w_quant(f):
-            wq = wqpool.tile([P, NT * NG * P], U32, name="wq", align_bytes=64)
-            wsc = wqpool.tile([P, NT * NG * P], U8, name="wsc", align_bytes=64)
+            wq = const.tile([P, NT * NG * P], U32, name="wq%d" % f, align_bytes=64)
+            wsc = const.tile([P, NT * NG * P], U8, name="wsc%d" % f, align_bytes=64)
             for lo, n in ((0, 1024), (1024, 512)):
                 nc.vector.quantize_mx(
                     out=wq[:, lo : lo + n].bitcast(FP8X4),
@@ -220,16 +214,6 @@ def tile_efficient_skan_batch_kernel(
                 nc.scalar.activation(out=bc[:], in_=bacc[:], func=ACT.Identity, bias=sbs[:, t : t + 1])
                 basec.append(bc)
 
-        units = []
-        for f in range(NF):
-            for g in range(NG):
-                if f in SPLIT_F:
-                    units.append((f, g, 0, HT))
-                    units.append((f, g, HT, TOK))
-                else:
-                    units.append((f, g, 0, TOK))
-        nu = len(units)
-
         kt = {}
         rt = {}
         sct = {}
@@ -237,167 +221,167 @@ def tile_efficient_skan_batch_kernel(
         swt = {}
         acc = []
 
-        def s1(n):
-            f, g, t0, t1 = units[n]
-            kk = kpool.tile([P, 2, t1 - t0, 2], I32, name="kk")
-            nc.vector.tensor_scalar(
-                out=kk[:].rearrange("p u t e -> p u (t e)"),
-                in0=xs[g][:, :, t0:t1, :].rearrange("p u t e -> p u (t e)"),
-                scalar1=cturn[:, f : f + 1],
-                scalar2=None,
-                op0=ALU.mult,
-            )
-            kt[n] = kk
+        def unit(n):
+            h, rest = divmod(n, NF * NG)
+            f, g = divmod(rest, NG)
+            return h, f, g
 
-        def s2(n):
-            f, g, t0, t1 = units[n]
-            rr = rpool.tile([P, 2, t1 - t0, 2], F32, name="rr")
+        def s1(q):
+            h, f = divmod(q, NF)
+            kk = kpool.tile([P, NG * 4 * HT], I32, name="kk")
+            nc.vector.tensor_scalar(
+                out=kk[:], in0=xs[h][:].rearrange("p g c -> p (g c)"), scalar1=cturn[:, f : f + 1],
+                scalar2=None, op0=ALU.mult,
+            )
+            kt[q] = kk
+
+        def s2(q):
+            h, f = divmod(q, NF)
+            rr = rpool.tile([P, NG, 4 * HT], F32, name="rr")
             nc.vector.scalar_tensor_tensor(
-                out=rr[:].rearrange("p u t e -> p u (t e)"),
-                in0=xs[g][:, :, t0:t1, :].rearrange("p u t e -> p u (t e)"),
+                out=rr[:].rearrange("p g c -> p (g c)"),
+                in0=xs[h][:].rearrange("p g c -> p (g c)"),
                 scalar=cturn[:, f : f + 1],
-                in1=kt[n][:].rearrange("p u t e -> p u (t e)"),
+                in1=kt[q][:],
                 op0=ALU.mult,
                 op1=ALU.subtract,
             )
-            rt[n] = rr
+            rt[q] = rr
 
         def s3(n):
-            f, g, t0, t1 = units[n]
-            rr = rt[n]
+            h, f, g = unit(n)
+            rr = rt[n // 2][:, g, :]
             ci = (f * NG + g) * 4
             if n in T_SET:
-                sn = snpool.tile([P, t1 - t0, 4], F32, name="sn")
+                sn = snpool.tile([P, HT, 4], F32, name="sn")
                 nc.scalar.activation(
                     out=sn[:].rearrange("p t (u e) -> p t u e", e=2),
-                    in_=rr[:].rearrange("p u t e -> p t u e"),
+                    in_=rr.rearrange("p (u t e) -> p t u e", u=2, e=2),
                     func=ACT.Sin,
                     scale=2.0 * math.pi,
                 )
                 sct[n] = sn
             else:
-                flat = rr[:].rearrange("p u t e -> p (u t e)")
-                nc.scalar.activation(out=flat, in_=flat, func=ACT.Sin, scale=2.0 * math.pi)
-                sc = scpool.tile([P, 4, t1 - t0], BF16, name="sc")
+                nc.scalar.activation(out=rr, in_=rr, func=ACT.Sin, scale=2.0 * math.pi)
+                sc = scpool.tile([P, 4, HT], BF16, name="sc")
+                rv = rr.rearrange("p (u t e) -> p u e t", u=2, e=2)
                 for j in range(4):
                     nc.scalar.activation(
                         out=sc[:, j, :],
-                        in_=rr[:, j // 2, :, j % 2],
+                        in_=rv[:, j // 2, j % 2, :],
                         func=ACT.Copy,
                         scale=coefT[:, ci + j : ci + j + 1],
                     )
                 sct[n] = sc
 
         def s4(n):
-            f, g, t0, t1 = units[n]
+            h, f, g = unit(n)
             ci = (f * NG + g) * 4
-            grp = gpool.tile([P, t1 - t0, 4], BF16, name="grp", align_bytes=64)
+            if g == 0:
+                grt[n // 2] = gpool.tile([P, NG, HT, 4], BF16, name="grp", align_bytes=64)
+            grp = grt[n // 2][:, g, :, :]
             if n in T_SET:
                 nc.vector.tensor_tensor(
-                    out=grp[:],
+                    out=grp,
                     in0=sct[n][:],
-                    in1=coefT[:, ci : ci + 4].unsqueeze(1).to_broadcast([P, t1 - t0, 4]),
+                    in1=coefT[:, ci : ci + 4].unsqueeze(1).to_broadcast([P, HT, 4]),
                     op=ALU.mult,
                 )
             else:
                 nc.vector.tensor_copy(
-                    out=grp[:].rearrange("p (c i) j -> p c j i", i=4),
+                    out=grp.rearrange("p (c i) j -> p c j i", i=4),
                     in_=sct[n][:].rearrange("p j (c i) -> p c j i", i=4),
                 )
-            grt[n] = grp
 
-        def s5(n):
-            f, g, t0, t1 = units[n]
-            if t0 == 0:
-                sw = swpool.tile([P, TOK], U32, name="sw", align_bytes=64)
-                ss = swpool.tile([P, TOK], U8, name="ss", align_bytes=64)
-                swt[(f, g)] = (sw, ss)
-            sw, ss = swt[(f, g)]
+        def s5(q):
+            sw = swpool.tile([P, NG, HT], U32, name="sw", align_bytes=64)
+            ss = swpool.tile([P, NG, HT], U8, name="ss", align_bytes=64)
             nc.vector.quantize_mx(
-                out=sw[:, t0:t1].bitcast(FP8X4),
-                scales=ss[:, t0:t1],
-                in_=grt[n][:].rearrange("p t j -> p (t j)"),
+                out=sw[:].rearrange("p g t -> p (g t)").bitcast(FP8X4),
+                scales=ss[:].rearrange("p g t -> p (g t)"),
+                in_=grt[q][:].rearrange("p g t j -> p (g t j)"),
             )
+            swt[q] = (sw, ss)
 
         def s6(n):
-            f, g, t0, t1 = units[n]
-            if t1 != TOK:
-                return
-            if f == 0 and g == 0:
+            h, f, g = unit(n)
+            if n == 0:
                 for t in range(NT):
                     acc.append(psum.tile([P, TOK], F32, tag="acc", bufs=6, name="acc%d" % t))
-            sw, ss = swt[(f, g)]
+            sw, ss = swt[n // 2]
             wq, wsc = wqs[f]
             for t in range(NT):
                 lo = (t * NG + g) * P
                 nc.tensor.matmul_mx(
-                    out=acc[t][:],
+                    out=acc[t][:, h * HT : (h + 1) * HT],
                     lhsT=wq[:, lo : lo + P].bitcast(FP8X4),
                     lhsT_scale=wsc[:, lo : lo + P],
-                    rhs=sw[:].bitcast(FP8X4),
-                    rhs_scale=ss[:],
+                    rhs=sw[:, g, :].bitcast(FP8X4),
+                    rhs_scale=ss[:, g, :],
                     start=(f == 0 and g == 0),
                     stop=(f == NF - 1 and g == NG - 1),
                 )
 
         outv = out.rearrange("b n o -> (b n) o").rearrange("(m p) o -> p m o", p=P)
 
-        def finish():
-            for t in range(NT):
-                ot = otpool.tile([P, TOK], F32, name="ot")
-                nc.vector.scalar_tensor_tensor(
-                    out=ot[:],
-                    in0=acc[t][:],
-                    scalar=bT[:, NF * NT + t : NF * NT + t + 1],
-                    in1=basec[t][:],
-                    op0=ALU.mult,
-                    op1=ALU.add,
-                )
-                fps = psum.tile([P, NM, P], F32, tag="acc", bufs=6, name="fps")
-                for m in range(NM):
-                    nc.tensor.transpose(fps[:, m, :], ot[:, m * P : (m + 1) * P], ident[:])
-                of = ofpool.tile([P, NM, P], F32, name="of")
-                if t in FIN_V:
-                    nc.vector.tensor_copy(out=of[:], in_=fps[:])
+        def finish(h):
+            for tp in range(NT // 2):
+                fps = psum.tile([P, 2, 2, P], F32, tag="w", name="fps")
+                for tt in range(2):
+                    t = 2 * tp + tt
+                    ot = opool.tile([P, HT], F32, name="ot")
+                    nc.vector.scalar_tensor_tensor(
+                        out=ot[:],
+                        in0=acc[t][:, h * HT : (h + 1) * HT],
+                        scalar=bT[:, NF * NT + t : NF * NT + t + 1],
+                        in1=basec[t][:, h * HT : (h + 1) * HT],
+                        op0=ALU.mult,
+                        op1=ALU.add,
+                    )
+                    for mi in range(2):
+                        nc.tensor.transpose(fps[:, mi, tt, :], ot[:, mi * P : (mi + 1) * P], ident[:])
+                of = opool.tile([P, 2, 2 * P], F32, name="of")
+                if (h, tp) in FIN_V:
+                    nc.vector.tensor_copy(out=of[:], in_=fps[:].rearrange("p m t o -> p m (t o)"))
                 else:
-                    nc.scalar.copy(out=of[:], in_=fps[:])
-                nc.sync.dma_start(out=outv[:, :, t * P : (t + 1) * P], in_=of[:])
+                    nc.scalar.copy(out=of[:], in_=fps[:].rearrange("p m t o -> p m (t o)"))
+                nc.sync.dma_start(
+                    out=outv[:, 2 * h : 2 * h + 2, 2 * P * tp : 2 * P * (tp + 1)], in_=of[:]
+                )
 
         nbanks = NF * NT
-        total_cols = sum(t1 - t0 for (f, g, t0, t1) in units)
         next_bank = 0
-        done_cols = 0
         quant_due = []
-        for it in range(nu + 6):
-            if it < nu:
-                s1(it)
-            if 0 <= it - 1 < nu:
-                s2(it - 1)
+        for it in range(NU + 8):
+            if it % 2 == 0 and it < NU:
+                s1(it // 2)
+            if it % 2 == 1 and it - 1 < NU:
+                s2((it - 1) // 2)
             if it == 1:
+                make_xt(1)
                 silu_part(0)
                 silu_part(1)
             if it == 2:
                 bias_part()
             if it == 3:
                 base_part()
-            if 0 <= it - 2 < nu:
+            if 0 <= it - 2 < NU:
                 s3(it - 2)
             for f in quant_due:
                 w_quant(f)
             quant_due = []
-            if it < nu:
-                done_cols += units[it][3] - units[it][2]
-            want = min(nbanks, LEAD + (done_cols * (nbanks - LEAD) + total_cols - 1) // total_cols)
-            while next_bank < want:
-                w_bank(next_bank)
-                if next_bank % NT == NT - 1:
-                    quant_due.append(next_bank // NT)
-                next_bank += 1
-            if 0 <= it - 3 < nu:
+            for i in range(BANKS_PER_IT):
+                if it >= 1 and next_bank < nbanks:
+                    w_bank(next_bank)
+                    if next_bank % NT == NT - 1:
+                        quant_due.append(next_bank // NT)
+                    next_bank += 1
+            if 0 <= it - 3 < NU:
                 s4(it - 3)
-            if 0 <= it - 5 < nu:
+            if it % 2 == 0 and 0 <= it - 6 < NU:
+                s6(it - 6)
                 s6(it - 5)
-                if it - 5 == nu - 1:
-                    finish()
-            if 0 <= it - 4 < nu:
-                s5(it - 4)
+                if (it - 5) % (NF * NG) == NF * NG - 1:
+                    finish((it - 5) // (NF * NG))
+            if it % 2 == 1 and 0 <= it - 5 < NU:
+                s5((it - 5) // 2)

@@ -28,11 +28,14 @@ NU = 2 * NF * NG
 
 FLOPS = 2 * TOK * K * OUT * (NF + 1)
 
-T_SET = (0, 1, 3, 4, 6, 7, 9, 10, 12, 13)
+K_SET = ()
+T_SET = (0, 1, 3, 4, 6, 8, 9, 11, 12, 14)
 EV_SET = ()
 FIN_V = ()
-BANKS_PER_IT = 3
-WB = 2
+W_START = 5
+MX_LAG = 9
+PIN = True
+WB = 3
 
 
 def tile_efficient_skan_batch_kernel(
@@ -43,14 +46,16 @@ def tile_efficient_skan_batch_kernel(
         const = ctx.enter_context(tc.tile_pool(name="const", bufs=1))
         wpool = ctx.enter_context(tc.tile_pool(name="wraw", bufs=WB))
         wgpool = ctx.enter_context(tc.tile_pool(name="wg", bufs=2))
-        kpool = ctx.enter_context(tc.tile_pool(name="k", bufs=2))
+        kpool = ctx.enter_context(tc.tile_pool(name="k", bufs=3))
         rpool = ctx.enter_context(tc.tile_pool(name="r", bufs=3))
         snpool = ctx.enter_context(tc.tile_pool(name="sn", bufs=2))
         scpool = ctx.enter_context(tc.tile_pool(name="sc", bufs=3))
-        gpool = ctx.enter_context(tc.tile_pool(name="grp", bufs=2))
-        swpool = ctx.enter_context(tc.tile_pool(name="sw", bufs=3))
+        gpool = ctx.enter_context(tc.tile_pool(name="grp", bufs=3))
+        swpool = ctx.enter_context(tc.tile_pool(name="sw", bufs=6))
         opool = ctx.enter_context(tc.tile_pool(name="o", bufs=3))
         psum = ctx.enter_context(tc.psum_pool(name="psum", bufs=2))
+        if PIN:
+            ctx.enter_context(tc.manual_schedule())
 
         xv = x.rearrange("b n k -> (b n) k").rearrange("(m p) k -> m p k", p=P)
         x_sb = const.tile([P, NM, K], BF16, name="x_sb")
@@ -125,9 +130,9 @@ def tile_efficient_skan_batch_kernel(
                             xw[:, 256 * g + u : 256 * (g + 1) : 2],
                             ident[:],
                         )
-                if g == 0:
-                    xs[h] = const.tile([P, NG, 4 * HT], BF16, name="xs%d" % h)
-                nc.scalar.copy(out=xs[h][:, g, :].bitcast(F32), in_=xb[:].rearrange("p u t -> p (u t)"))
+                xc = const.tile([P, 4 * HT], BF16, name="xs%d%d" % (h, g))
+                nc.scalar.copy(out=xc[:].bitcast(F32), in_=xb[:].rearrange("p u t -> p (u t)"))
+                xs[(h, g)] = xc
                 xbank[(h, g)] = xb
 
         def silu_part(h):
@@ -162,16 +167,17 @@ def tile_efficient_skan_batch_kernel(
             if t == NT - 1 and f + WB < NF:
                 load_w(f + WB)
 
-        def w_quant(f):
-            wq = const.tile([P, NT * NG * P], U32, name="wq%d" % f, align_bytes=64)
-            wsc = const.tile([P, NT * NG * P], U8, name="wsc%d" % f, align_bytes=64)
-            for lo, n in ((0, 1024), (1024, 512)):
-                nc.vector.quantize_mx(
-                    out=wq[:, lo : lo + n].bitcast(FP8X4),
-                    scales=wsc[:, lo : lo + n],
-                    in_=wgs[f][:, 4 * lo : 4 * (lo + n)],
-                )
-            wqs[f] = (wq, wsc)
+        def w_quant(f, c):
+            if c == 0:
+                wq = const.tile([P, NT * NG * P], U32, name="wq%d" % f, align_bytes=64)
+                wsc = const.tile([P, NT * NG * P], U8, name="wsc%d" % f, align_bytes=64)
+                wqs[f] = (wq, wsc)
+            wq, wsc = wqs[f]
+            nc.vector.quantize_mx(
+                out=wq[:, 512 * c : 512 * (c + 1)].bitcast(FP8X4),
+                scales=wsc[:, 512 * c : 512 * (c + 1)],
+                in_=wgs[f][:, 2048 * c : 2048 * (c + 1)],
+            )
 
         bT = const.tile([P, 64], F32, name="bT")
         bsum = const.tile([P, NT], F32, name="bsum")
@@ -192,27 +198,28 @@ def tile_efficient_skan_batch_kernel(
             )
             nc.vector.tensor_mul(out=sbs[:], in0=bsum[:], in1=bT[:, NF * NT : NF * NT + NT])
 
-        def base_part():
+        def base_quant():
             nc.vector.quantize_mx(
                 out=sil_w[:].rearrange("p g t -> p (g t)").bitcast(FP8X4),
                 scales=sil_s[:].rearrange("p g t -> p (g t)"),
                 in_=silu_g[:].rearrange("p g t j -> p (g t j)"),
             )
-            for t in range(NT):
-                bacc = psum.tile([P, TOK], F32, tag="acc", bufs=6, name="bacc")
-                for g in range(NG):
-                    nc.tensor.matmul_mx(
-                        out=bacc[:],
-                        lhsT=w4w[:, g, 2 * P * t : 2 * P * (t + 1)].bitcast(FP4X4),
-                        lhsT_scale=w4s[:, g, P * t : P * (t + 1)],
-                        rhs=sil_w[:, g, :].bitcast(FP8X4),
-                        rhs_scale=sil_s[:, g, :],
-                        start=(g == 0),
-                        stop=(g == NG - 1),
-                    )
-                bc = const.tile([P, TOK], F32, name="basec%d" % t)
-                nc.scalar.activation(out=bc[:], in_=bacc[:], func=ACT.Identity, bias=sbs[:, t : t + 1])
-                basec.append(bc)
+
+        def base_tile(t):
+            bacc = psum.tile([P, TOK], F32, tag="acc", bufs=6, name="bacc")
+            for g in range(NG):
+                nc.tensor.matmul_mx(
+                    out=bacc[:],
+                    lhsT=w4w[:, g, 2 * P * t : 2 * P * (t + 1)].bitcast(FP4X4),
+                    lhsT_scale=w4s[:, g, P * t : P * (t + 1)],
+                    rhs=sil_w[:, g, :].bitcast(FP8X4),
+                    rhs_scale=sil_s[:, g, :],
+                    start=(g == 0),
+                    stop=(g == NG - 1),
+                )
+            bc = const.tile([P, TOK], F32, name="basec%d" % t)
+            nc.scalar.activation(out=bc[:], in_=bacc[:], func=ACT.Identity, bias=sbs[:, t : t + 1])
+            basec.append(bc)
 
         kt = {}
         rt = {}
@@ -226,89 +233,96 @@ def tile_efficient_skan_batch_kernel(
             f, g = divmod(rest, NG)
             return h, f, g
 
-        def s1(q):
-            h, f = divmod(q, NF)
-            kk = kpool.tile([P, NG * 4 * HT], I32, name="kk")
-            nc.vector.tensor_scalar(
-                out=kk[:], in0=xs[h][:].rearrange("p g c -> p (g c)"), scalar1=cturn[:, f : f + 1],
-                scalar2=None, op0=ALU.mult,
-            )
-            kt[q] = kk
+        def s1(n):
+            h, f, g = unit(n)
+            kk = kpool.tile([P, 4 * HT], I32, name="kk")
+            if n in K_SET:
+                nc.gpsimd.tensor_scalar(
+                    out=kk[:], in0=xs[(h, g)][:], scalar1=cturn[:, f : f + 1], scalar2=0.0,
+                    op0=ALU.mult, op1=ALU.add,
+                )
+            else:
+                nc.vector.tensor_scalar(
+                    out=kk[:], in0=xs[(h, g)][:], scalar1=cturn[:, f : f + 1], scalar2=None,
+                    op0=ALU.mult,
+                )
+            kt[n] = kk
 
-        def s2(q):
-            h, f = divmod(q, NF)
-            rr = rpool.tile([P, NG, 4 * HT], F32, name="rr")
+        def s2(n):
+            h, f, g = unit(n)
+            rr = rpool.tile([P, 4 * HT], F32, name="rr")
             nc.vector.scalar_tensor_tensor(
-                out=rr[:].rearrange("p g c -> p (g c)"),
-                in0=xs[h][:].rearrange("p g c -> p (g c)"),
+                out=rr[:],
+                in0=xs[(h, g)][:],
                 scalar=cturn[:, f : f + 1],
-                in1=kt[q][:],
+                in1=kt[n][:],
                 op0=ALU.mult,
                 op1=ALU.subtract,
             )
-            rt[q] = rr
+            rt[n] = rr
 
-        def s3(n):
-            h, f, g = unit(n)
-            rr = rt[n // 2][:, g, :]
-            ci = (f * NG + g) * 4
+        def s3a(n):
+            rr = rt[n]
             if n in T_SET:
                 sn = snpool.tile([P, HT, 4], F32, name="sn")
                 nc.scalar.activation(
                     out=sn[:].rearrange("p t (u e) -> p t u e", e=2),
-                    in_=rr.rearrange("p (u t e) -> p t u e", u=2, e=2),
+                    in_=rr[:].rearrange("p (u t e) -> p t u e", u=2, e=2),
                     func=ACT.Sin,
                     scale=2.0 * math.pi,
                 )
                 sct[n] = sn
             else:
-                nc.scalar.activation(out=rr, in_=rr, func=ACT.Sin, scale=2.0 * math.pi)
-                sc = scpool.tile([P, 4, HT], BF16, name="sc")
-                rv = rr.rearrange("p (u t e) -> p u e t", u=2, e=2)
-                for j in range(4):
-                    nc.scalar.activation(
-                        out=sc[:, j, :],
-                        in_=rv[:, j // 2, j % 2, :],
-                        func=ACT.Copy,
-                        scale=coefT[:, ci + j : ci + j + 1],
-                    )
-                sct[n] = sc
+                nc.scalar.activation(out=rr[:], in_=rr[:], func=ACT.Sin, scale=2.0 * math.pi)
+
+        def s3b(n):
+            if n in T_SET:
+                return
+            h, f, g = unit(n)
+            ci = (f * NG + g) * 4
+            sc = scpool.tile([P, 4, HT], BF16, name="sc")
+            rv = rt[n][:].rearrange("p (u t e) -> p u e t", u=2, e=2)
+            for j in range(4):
+                nc.scalar.activation(
+                    out=sc[:, j, :],
+                    in_=rv[:, j // 2, j % 2, :],
+                    func=ACT.Copy,
+                    scale=coefT[:, ci + j : ci + j + 1],
+                )
+            sct[n] = sc
 
         def s4(n):
             h, f, g = unit(n)
             ci = (f * NG + g) * 4
-            if g == 0:
-                grt[n // 2] = gpool.tile([P, NG, HT, 4], BF16, name="grp", align_bytes=64)
-            grp = grt[n // 2][:, g, :, :]
+            grp = gpool.tile([P, HT, 4], BF16, name="grp", align_bytes=64)
             if n in T_SET:
                 nc.vector.tensor_tensor(
-                    out=grp,
+                    out=grp[:],
                     in0=sct[n][:],
                     in1=coefT[:, ci : ci + 4].unsqueeze(1).to_broadcast([P, HT, 4]),
                     op=ALU.mult,
                 )
             else:
                 nc.vector.tensor_copy(
-                    out=grp.rearrange("p (c i) j -> p c j i", i=4),
+                    out=grp[:].rearrange("p (c i) j -> p c j i", i=4),
                     in_=sct[n][:].rearrange("p j (c i) -> p c j i", i=4),
                 )
+            grt[n] = grp
 
-        def s5(q):
-            sw = swpool.tile([P, NG, HT], U32, name="sw", align_bytes=64)
-            ss = swpool.tile([P, NG, HT], U8, name="ss", align_bytes=64)
+        def s5(n):
+            sw = swpool.tile([P, HT], U32, name="sw", align_bytes=64)
+            ss = swpool.tile([P, HT], U8, name="ss", align_bytes=64)
             nc.vector.quantize_mx(
-                out=sw[:].rearrange("p g t -> p (g t)").bitcast(FP8X4),
-                scales=ss[:].rearrange("p g t -> p (g t)"),
-                in_=grt[q][:].rearrange("p g t j -> p (g t j)"),
+                out=sw[:].bitcast(FP8X4), scales=ss[:], in_=grt[n][:].rearrange("p t j -> p (t j)")
             )
-            swt[q] = (sw, ss)
+            swt[n] = (sw, ss)
 
         def s6(n):
             h, f, g = unit(n)
             if n == 0:
                 for t in range(NT):
                     acc.append(psum.tile([P, TOK], F32, tag="acc", bufs=6, name="acc%d" % t))
-            sw, ss = swt[n // 2]
+            sw, ss = swt[n]
             wq, wsc = wqs[f]
             for t in range(NT):
                 lo = (t * NG + g) * P
@@ -316,8 +330,8 @@ def tile_efficient_skan_batch_kernel(
                     out=acc[t][:, h * HT : (h + 1) * HT],
                     lhsT=wq[:, lo : lo + P].bitcast(FP8X4),
                     lhsT_scale=wsc[:, lo : lo + P],
-                    rhs=sw[:, g, :].bitcast(FP8X4),
-                    rhs_scale=ss[:, g, :],
+                    rhs=sw[:].bitcast(FP8X4),
+                    rhs_scale=ss[:],
                     start=(f == 0 and g == 0),
                     stop=(f == NF - 1 and g == NG - 1),
                 )
@@ -350,13 +364,32 @@ def tile_efficient_skan_batch_kernel(
                 )
 
         nbanks = NF * NT
-        next_bank = 0
-        quant_due = []
-        for it in range(NU + 8):
-            if it % 2 == 0 and it < NU:
-                s1(it // 2)
-            if it % 2 == 1 and it - 1 < NU:
-                s2((it - 1) // 2)
+        state = {"bank": 0}
+        quant_queue = []
+
+        def banks(count):
+            for i in range(count):
+                b = state["bank"]
+                if b < nbanks:
+                    w_bank(b)
+                    if b % NT == NT - 1:
+                        quant_queue.extend([(b // NT, c) for c in range(3)])
+                    state["bank"] = b + 1
+
+        def one_quant():
+            if quant_queue:
+                f, c = quant_queue.pop(0)
+                w_quant(f, c)
+
+        for it in range(NU + MX_LAG + 1):
+            if it < NU:
+                s1(it)
+            if 0 <= it - 1 < NU:
+                s2(it - 1)
+            if 0 <= it - 2 < NU:
+                s3a(it - 2)
+            if it >= W_START:
+                banks(2)
             if it == 1:
                 make_xt(1)
                 silu_part(0)
@@ -364,24 +397,20 @@ def tile_efficient_skan_batch_kernel(
             if it == 2:
                 bias_part()
             if it == 3:
-                base_part()
+                base_quant()
+            if 4 <= it < 4 + NT:
+                base_tile(it - 4)
             if 0 <= it - 2 < NU:
-                s3(it - 2)
-            for f in quant_due:
-                w_quant(f)
-            quant_due = []
-            for i in range(BANKS_PER_IT):
-                if it >= 1 and next_bank < nbanks:
-                    w_bank(next_bank)
-                    if next_bank % NT == NT - 1:
-                        quant_due.append(next_bank // NT)
-                    next_bank += 1
+                s3b(it - 2)
+            if it >= W_START and not (0 <= it - 2 < NU and (it - 2) in T_SET):
+                banks(2)
             if 0 <= it - 3 < NU:
                 s4(it - 3)
-            if it % 2 == 0 and 0 <= it - 6 < NU:
-                s6(it - 6)
-                s6(it - 5)
-                if (it - 5) % (NF * NG) == NF * NG - 1:
-                    finish((it - 5) // (NF * NG))
-            if it % 2 == 1 and 0 <= it - 5 < NU:
-                s5((it - 5) // 2)
+            one_quant()
+            if 0 <= it - MX_LAG < NU:
+                s6(it - MX_LAG)
+                if (it - MX_LAG) % (NF * NG) == NF * NG - 1:
+                    finish((it - MX_LAG) // (NF * NG))
+            if 0 <= it - 4 < NU:
+                s5(it - 4)
+            one_quant()

@@ -28,14 +28,14 @@ NU = 2 * NF * NG
 
 FLOPS = 2 * TOK * K * OUT * (NF + 1)
 
-K_SET = ()
-T_SET = (0, 1, 3, 4, 6, 8, 9, 11, 12, 14)
-EV_SET = ()
-FIN_V = ()
-W_START = 5
-MX_LAG = 9
-PIN = True
-WB = 3
+KV_SET = (0,)
+T_SET = (0, 1, 3, 5, 7, 9, 11, 13, 15, 17, 19, 21, 23, 31)
+W_START = 4
+BQ = 3
+W_HEAD = 3
+LAG4 = 3
+WB = 6
+KG_BUFS = 7
 
 
 def tile_efficient_skan_batch_kernel(
@@ -45,17 +45,15 @@ def tile_efficient_skan_batch_kernel(
     with ExitStack() as ctx:
         const = ctx.enter_context(tc.tile_pool(name="const", bufs=1))
         wpool = ctx.enter_context(tc.tile_pool(name="wraw", bufs=WB))
-        wgpool = ctx.enter_context(tc.tile_pool(name="wg", bufs=2))
-        kpool = ctx.enter_context(tc.tile_pool(name="k", bufs=3))
+        wgpool = ctx.enter_context(tc.tile_pool(name="wg", bufs=3))
+        kgpool = ctx.enter_context(tc.tile_pool(name="kgp", bufs=KG_BUFS))
         rpool = ctx.enter_context(tc.tile_pool(name="r", bufs=3))
         snpool = ctx.enter_context(tc.tile_pool(name="sn", bufs=2))
         scpool = ctx.enter_context(tc.tile_pool(name="sc", bufs=3))
-        gpool = ctx.enter_context(tc.tile_pool(name="grp", bufs=3))
-        swpool = ctx.enter_context(tc.tile_pool(name="sw", bufs=6))
+        swpool = ctx.enter_context(tc.tile_pool(name="sw", bufs=9))
         opool = ctx.enter_context(tc.tile_pool(name="o", bufs=3))
-        psum = ctx.enter_context(tc.psum_pool(name="psum", bufs=2))
-        if PIN:
-            ctx.enter_context(tc.manual_schedule())
+        psum = ctx.enter_context(tc.psum_pool(name="psum", bufs=1))
+        ctx.enter_context(tc.manual_schedule())
 
         xv = x.rearrange("b n k -> (b n) k").rearrange("(m p) k -> m p k", p=P)
         x_sb = const.tile([P, NM, K], BF16, name="x_sb")
@@ -77,6 +75,24 @@ def tile_efficient_skan_batch_kernel(
             out=braw[NF * NT : NF * NT + NT, :], in_=scale_sp.rearrange("(t c) -> t c", c=P)
         )
 
+        ident = const.tile([P, P], F32, name="ident")
+        make_identity(nc, ident[:])
+        identb = const.tile([P, P], BF16, name="identb")
+        make_identity(nc, identb[:])
+
+        raws = {}
+
+        def load_w(c):
+            g, f = divmod(c, NF)
+            wraw = wpool.tile([P, NT, K // NG], BF16, name="wraw")
+            nc.sync.dma_start(
+                out=wraw[:],
+                in_=conv_w[f].rearrange("(t p) (g k) -> g p t k", p=P, g=NG)[g],
+            )
+            raws[c] = wraw
+
+        for c in range(3):
+            load_w(c)
         w4w = const.tile([P, NG, 2 * OUT], U8, name="w4w", align_bytes=64)
         nc.sync.dma_start(
             out=w4w[:].bitcast(I32),
@@ -88,20 +104,8 @@ def tile_efficient_skan_batch_kernel(
         for r in range(4):
             nc.sync.dma_start(out=w4s[r:P:32, :, :].bitcast(I32), in_=w4sv[r].bitcast(I32))
 
-        ident = const.tile([P, P], F32, name="ident")
-        make_identity(nc, ident[:])
-        identb = const.tile([P, P], BF16, name="identb")
-        make_identity(nc, identb[:])
-
-        raws = {}
-
-        def load_w(f):
-            wraw = wpool.tile([P, NT, K], BF16, name="wraw")
-            nc.sync.dma_start(out=wraw[:], in_=conv_w[f].rearrange("(t p) k -> p t k", p=P))
-            raws[f] = wraw
-
-        for f in range(WB):
-            load_w(f)
+        for c in range(3, WB):
+            load_w(c)
 
         g32 = const.tile([P, NF], F32, name="g32")
         nc.vector.tensor_copy(out=g32[:], in_=gb[:])
@@ -119,21 +123,27 @@ def tile_efficient_skan_batch_kernel(
         xbank = {}
         silu_g = const.tile([P, NG, TOK, 4], BF16, name="silu_g", align_bytes=64)
 
-        def make_xt(h):
-            for g in range(NG):
-                xb = psum.tile([P, 2, HT], F32, tag="acc", bufs=6, name="xb")
-                for mi in range(2):
-                    xw = x_sb[:, 2 * h + mi, :].bitcast(F32)
-                    for u in range(2):
-                        nc.tensor.transpose(
-                            xb[:, u, mi * P : (mi + 1) * P],
-                            xw[:, 256 * g + u : 256 * (g + 1) : 2],
-                            ident[:],
-                        )
-                xc = const.tile([P, 4 * HT], BF16, name="xs%d%d" % (h, g))
-                nc.scalar.copy(out=xc[:].bitcast(F32), in_=xb[:].rearrange("p u t -> p (u t)"))
-                xs[(h, g)] = xc
-                xbank[(h, g)] = xb
+        def make_xt(h, g):
+            xb = psum.tile([P, 2, HT], F32, tag="acc", bufs=6, name="xb")
+            for mi in range(2):
+                xw = x_sb[:, 2 * h + mi, :].bitcast(F32)
+                for u in range(2):
+                    nc.tensor.transpose(
+                        xb[:, u, mi * P : (mi + 1) * P],
+                        xw[:, 256 * g + u : 256 * (g + 1) : 2],
+                        ident[:],
+                    )
+            xbank[(h, g)] = xb
+
+        def copy_xt(h, g):
+            xc = const.tile([P, 4 * HT], BF16, name="xs%d%d" % (h, g))
+            dst = xc[:].bitcast(F32)
+            src = xbank[(h, g)][:].rearrange("p u t -> p (u t)")
+            if h == 0 and g == 0:
+                nc.scalar.copy(out=dst, in_=src)
+            else:
+                nc.vector.tensor_copy(out=dst, in_=src)
+            xs[(h, g)] = xc
 
         def silu_part(h):
             for g in range(NG):
@@ -143,40 +153,56 @@ def tile_efficient_skan_batch_kernel(
                     func=ACT.Silu,
                 )
 
-        make_xt(0)
+        xp = {}
+
+        def fill_xp(h, g):
+            xt = psum.tile([P, 2, HT], F32, tag="x", name="xt")
+            for mi in range(2):
+                xw = x_sb[:, 2 * h + mi, :].bitcast(F32)
+                for u in range(2):
+                    nc.tensor.transpose(
+                        xt[:, u, mi * P : (mi + 1) * P],
+                        xw[:, 256 * g + u : 256 * (g + 1) : 2],
+                        ident[:],
+                    )
+            xp[(h, g)] = xt
+
+        make_xt(0, 0)
+        copy_xt(0, 0)
 
         wgs = {}
         wqs = {}
 
         def w_bank(b):
-            f, t = divmod(b, NT)
-            if t == 0:
-                wgs[f] = wgpool.tile([P, NT * NG * P * 4], BF16, name="wg", align_bytes=64)
-            wgw = wgs[f][:].bitcast(F32)
-            ww = raws[f][:, t, :].bitcast(F32)
-            wps = psum.tile([P, 4, P], F32, tag="w", name="wps")
-            for q in range(4):
-                g, u = divmod(q, 2)
-                nc.tensor.transpose(wps[:, q, :], ww[:, 256 * g + u : 256 * (g + 1) : 2], ident[:])
-            dst = wgw[:, 512 * t : 512 * (t + 1)].rearrange("p (g o u) -> p g o u", g=NG, u=2)
-            src = wps[:].rearrange("p (g u) o -> p g o u", u=2)
-            if b in EV_SET:
+            c, tp = divmod(b, NT // 2)
+            if tp == 0:
+                wgs[c] = wgpool.tile([P, NT * P * 4], BF16, name="wg", align_bytes=64)
+            wgw = wgs[c][:].bitcast(F32)
+            wps = psum.tile([P, 2, 2, P], F32, tag="acc" if b < W_HEAD else "w", bufs=6 if b < W_HEAD else 1, name="wps")
+            for tt in range(2):
+                ww = raws[c][:, 2 * tp + tt, :].bitcast(F32)
+                for u in range(2):
+                    nc.tensor.transpose(wps[:, tt, u, :], ww[:, u : 2 * P : 2], ident[:])
+            dst = wgw[:, 512 * tp : 512 * (tp + 1)].rearrange("p (t o u) -> p t o u", t=2, u=2)
+            src = wps[:].rearrange("p t u o -> p t o u")
+            if b < W_HEAD:
                 nc.vector.tensor_copy(out=dst, in_=src)
             else:
                 nc.scalar.copy(out=dst, in_=src)
-            if t == NT - 1 and f + WB < NF:
-                load_w(f + WB)
+            if tp == NT // 2 - 1 and c + WB < NF * NG:
+                load_w(c + WB)
 
-        def w_quant(f, c):
-            if c == 0:
-                wq = const.tile([P, NT * NG * P], U32, name="wq%d" % f, align_bytes=64)
-                wsc = const.tile([P, NT * NG * P], U8, name="wsc%d" % f, align_bytes=64)
-                wqs[f] = (wq, wsc)
-            wq, wsc = wqs[f]
+        def w_quant(c, part):
+            if part == 0:
+                wq = const.tile([P, NT * P], U32, name="wq%d" % c, align_bytes=64)
+                wsc = const.tile([P, NT * P], U8, name="wsc%d" % c, align_bytes=64)
+                wqs[c] = (wq, wsc)
+            wq, wsc = wqs[c]
+            lo, hi = ((0, 512), (512, 768))[part]
             nc.vector.quantize_mx(
-                out=wq[:, 512 * c : 512 * (c + 1)].bitcast(FP8X4),
-                scales=wsc[:, 512 * c : 512 * (c + 1)],
-                in_=wgs[f][:, 2048 * c : 2048 * (c + 1)],
+                out=wq[:, lo:hi].bitcast(FP8X4),
+                scales=wsc[:, lo:hi],
+                in_=wgs[c][:, 4 * lo : 4 * hi],
             )
 
         bT = const.tile([P, 64], F32, name="bT")
@@ -230,13 +256,13 @@ def tile_efficient_skan_batch_kernel(
 
         def unit(n):
             h, rest = divmod(n, NF * NG)
-            f, g = divmod(rest, NG)
+            g, f = divmod(rest, NF)
             return h, f, g
 
         def s1(n):
             h, f, g = unit(n)
-            kk = kpool.tile([P, 4 * HT], I32, name="kk")
-            if n in K_SET:
+            kk = kgpool.tile([P, 4 * HT], I32, tag="kg", name="kk", align_bytes=64)
+            if n not in KV_SET:
                 nc.gpsimd.tensor_scalar(
                     out=kk[:], in0=xs[(h, g)][:], scalar1=cturn[:, f : f + 1], scalar2=0.0,
                     op0=ALU.mult, op1=ALU.add,
@@ -251,15 +277,18 @@ def tile_efficient_skan_batch_kernel(
         def s2(n):
             h, f, g = unit(n)
             rr = rpool.tile([P, 4 * HT], F32, name="rr")
+            src = xp[(h, g)][:].rearrange("p u t -> p (u t)").bitcast(BF16)
             nc.vector.scalar_tensor_tensor(
                 out=rr[:],
-                in0=xs[(h, g)][:],
+                in0=src,
                 scalar=cturn[:, f : f + 1],
                 in1=kt[n][:],
                 op0=ALU.mult,
                 op1=ALU.subtract,
             )
             rt[n] = rr
+            if n % NF == NF - 1 and n + 1 < NU:
+                fill_xp(*unit(n + 1)[0::2])
 
         def s3a(n):
             rr = rt[n]
@@ -275,26 +304,25 @@ def tile_efficient_skan_batch_kernel(
             else:
                 nc.scalar.activation(out=rr[:], in_=rr[:], func=ACT.Sin, scale=2.0 * math.pi)
 
-        def s3b(n):
-            if n in T_SET:
-                return
+        def s3b(n, j0):
             h, f, g = unit(n)
             ci = (f * NG + g) * 4
-            sc = scpool.tile([P, 4, HT], BF16, name="sc")
+            if j0 == 0:
+                sct[n] = scpool.tile([P, 4, HT], BF16, name="sc")
+            sc = sct[n]
             rv = rt[n][:].rearrange("p (u t e) -> p u e t", u=2, e=2)
-            for j in range(4):
+            for j in range(j0, j0 + 2):
                 nc.scalar.activation(
                     out=sc[:, j, :],
                     in_=rv[:, j // 2, j % 2, :],
                     func=ACT.Copy,
                     scale=coefT[:, ci + j : ci + j + 1],
                 )
-            sct[n] = sc
 
         def s4(n):
             h, f, g = unit(n)
             ci = (f * NG + g) * 4
-            grp = gpool.tile([P, HT, 4], BF16, name="grp", align_bytes=64)
+            grp = kgpool.tile([P, HT, 4], BF16, tag="kg", name="grp", align_bytes=64)
             if n in T_SET:
                 nc.vector.tensor_tensor(
                     out=grp[:],
@@ -323,9 +351,9 @@ def tile_efficient_skan_batch_kernel(
                 for t in range(NT):
                     acc.append(psum.tile([P, TOK], F32, tag="acc", bufs=6, name="acc%d" % t))
             sw, ss = swt[n]
-            wq, wsc = wqs[f]
+            wq, wsc = wqs[g * NF + f]
             for t in range(NT):
-                lo = (t * NG + g) * P
+                lo = t * P
                 nc.tensor.matmul_mx(
                     out=acc[t][:, h * HT : (h + 1) * HT],
                     lhsT=wq[:, lo : lo + P].bitcast(FP8X4),
@@ -338,9 +366,9 @@ def tile_efficient_skan_batch_kernel(
 
         outv = out.rearrange("b n o -> (b n) o").rearrange("(m p) o -> p m o", p=P)
 
-        def finish(h):
-            for tp in range(NT // 2):
-                fps = psum.tile([P, 2, 2, P], F32, tag="w", name="fps")
+        def finish(h, parts):
+            for tp in parts:
+                fps = psum.tile([P, 2, 2, P], F32, tag=("w", "x")[tp % 2 if h == 1 else 0], name="fps")
                 for tt in range(2):
                     t = 2 * tp + tt
                     ot = opool.tile([P, HT], F32, name="ot")
@@ -355,62 +383,82 @@ def tile_efficient_skan_batch_kernel(
                     for mi in range(2):
                         nc.tensor.transpose(fps[:, mi, tt, :], ot[:, mi * P : (mi + 1) * P], ident[:])
                 of = opool.tile([P, 2, 2 * P], F32, name="of")
-                if (h, tp) in FIN_V:
-                    nc.vector.tensor_copy(out=of[:], in_=fps[:].rearrange("p m t o -> p m (t o)"))
-                else:
+                if True:
                     nc.scalar.copy(out=of[:], in_=fps[:].rearrange("p m t o -> p m (t o)"))
                 nc.sync.dma_start(
                     out=outv[:, 2 * h : 2 * h + 2, 2 * P * tp : 2 * P * (tp + 1)], in_=of[:]
                 )
 
-        nbanks = NF * NT
-        state = {"bank": 0}
+        nbanks = NF * NG * (NT // 2)
+        state = {"bank": 0, "mx": 0, "wq": 0}
         quant_queue = []
+        fin_queue = []
 
-        def banks(count):
+        def banks(it, count):
             for i in range(count):
                 b = state["bank"]
-                if b < nbanks:
+                if it >= W_START and b < nbanks:
                     w_bank(b)
-                    if b % NT == NT - 1:
-                        quant_queue.extend([(b // NT, c) for c in range(3)])
+                    if b % 3 == 2:
+                        quant_queue.extend([(b // 3, 0), (b // 3, 1)])
                     state["bank"] = b + 1
 
         def one_quant():
             if quant_queue:
-                f, c = quant_queue.pop(0)
-                w_quant(f, c)
+                c, part = quant_queue.pop(0)
+                w_quant(c, part)
+                state["wq"] = 2 * c + part + 1
 
-        for it in range(NU + MX_LAG + 1):
-            if it < NU:
-                s1(it)
+        fill_xp(0, 0)
+        make_xt(0, 1)
+        make_xt(1, 0)
+        make_xt(1, 1)
+        silu_part(0)
+        silu_part(1)
+        for it in range(-1, NU + LAG4 + 16):
+            if it + 1 < NU:
+                s1(it + 1)
             if 0 <= it - 1 < NU:
                 s2(it - 1)
             if 0 <= it - 2 < NU:
                 s3a(it - 2)
-            if it >= W_START:
-                banks(2)
+            banks(it, 1)
             if it == 1:
-                make_xt(1)
-                silu_part(0)
-                silu_part(1)
-            if it == 2:
-                bias_part()
+                copy_xt(0, 1)
+                copy_xt(1, 0)
+                copy_xt(1, 1)
             if it == 3:
+                for i in range(W_HEAD // 3):
+                    banks(W_START, 3)
+                    one_quant()
+                    one_quant()
+            if it == BQ:
                 base_quant()
-            if 4 <= it < 4 + NT:
-                base_tile(it - 4)
-            if 0 <= it - 2 < NU:
-                s3b(it - 2)
-            if it >= W_START and not (0 <= it - 2 < NU and (it - 2) in T_SET):
-                banks(2)
-            if 0 <= it - 3 < NU:
-                s4(it - 3)
+                bias_part()
+            if 4 <= it < 4 + NT // 2:
+                base_tile(2 * (it - 4))
+                base_tile(2 * (it - 4) + 1)
+            if 0 <= it - 2 < NU and it - 2 not in T_SET:
+                s3b(it - 2, 0)
+                banks(it, 1)
+                s3b(it - 2, 2)
+                banks(it, 1)
+            if 0 <= it - LAG4 < NU:
+                s4(it - LAG4)
             one_quant()
-            if 0 <= it - MX_LAG < NU:
-                s6(it - MX_LAG)
-                if (it - MX_LAG) % (NF * NG) == NF * NG - 1:
-                    finish((it - MX_LAG) // (NF * NG))
-            if 0 <= it - 4 < NU:
-                s5(it - 4)
-            one_quant()
+            if it % 2 or it < 5:
+                one_quant()
+            for i in range(2):
+                n = state["mx"]
+                if n < NU and it >= 4 + NT // 2 and n <= it - LAG4 - 2 and state["wq"] >= 2 * min(n % (NF * NG), NF * NG) + 2:
+                    s6(n)
+                    state["mx"] = n + 1
+                    if n % (NF * NG) == NF * NG - 1:
+                        if n + 1 < NU:
+                            fin_queue.extend([0, 1, 2])
+                        else:
+                            finish(1, (0, 1, 2))
+            if fin_queue:
+                finish(0, (fin_queue.pop(0),))
+            if 0 <= it - LAG4 - 1 < NU:
+                s5(it - LAG4 - 1)

@@ -29,12 +29,16 @@ NU = 2 * NF * NG
 FLOPS = 2 * TOK * K * OUT * (NF + 1)
 
 KV_SET = (0,)
-T_SET = (0, 1, 3, 5, 7, 9, 11, 13, 15, 17, 19, 21, 23, 31)
+T_SET = (0, 1, 3, 5, 7, 9, 11, 13, 15, 17, 19, 30, 31)
 W_START = 4
 BQ = 3
+SWB = 20
+LEAD = 5
+RT = 3
+MXR = 2
 W_HEAD = 3
 LAG4 = 3
-WB = 6
+WB = 5
 KG_BUFS = 7
 
 
@@ -50,7 +54,7 @@ def tile_efficient_skan_batch_kernel(
         rpool = ctx.enter_context(tc.tile_pool(name="r", bufs=3))
         snpool = ctx.enter_context(tc.tile_pool(name="sn", bufs=2))
         scpool = ctx.enter_context(tc.tile_pool(name="sc", bufs=3))
-        swpool = ctx.enter_context(tc.tile_pool(name="sw", bufs=9))
+        swpool = ctx.enter_context(tc.tile_pool(name="sw", bufs=SWB))
         opool = ctx.enter_context(tc.tile_pool(name="o", bufs=3))
         psum = ctx.enter_context(tc.psum_pool(name="psum", bufs=1))
         ctx.enter_context(tc.manual_schedule())
@@ -84,7 +88,7 @@ def tile_efficient_skan_batch_kernel(
 
         def load_w(c):
             g, f = divmod(c, NF)
-            wraw = wpool.tile([P, NT, K // NG], BF16, name="wraw")
+            wraw = wpool.tile([P, NT, K // NG], BF16, tag="wraw", name="wraw", align_bytes=64)
             nc.sync.dma_start(
                 out=wraw[:],
                 in_=conv_w[f].rearrange("(t p) (g k) -> g p t k", p=P, g=NG)[g],
@@ -104,8 +108,6 @@ def tile_efficient_skan_batch_kernel(
         for r in range(4):
             nc.sync.dma_start(out=w4s[r:P:32, :, :].bitcast(I32), in_=w4sv[r].bitcast(I32))
 
-        for c in range(3, WB):
-            load_w(c)
 
         g32 = const.tile([P, NF], F32, name="g32")
         nc.vector.tensor_copy(out=g32[:], in_=gb[:])
@@ -121,7 +123,10 @@ def tile_efficient_skan_batch_kernel(
 
         xs = {}
         xbank = {}
-        silu_g = const.tile([P, NG, TOK, 4], BF16, name="silu_g", align_bytes=64)
+        silu_g = []
+        for g in range(NG):
+            sg = wpool.tile([P, TOK, 4], BF16, tag="wraw", name="sg", align_bytes=64)
+            silu_g.append(sg)
 
         def make_xt(h, g):
             xb = psum.tile([P, 2, HT], F32, tag="acc", bufs=6, name="xb")
@@ -148,7 +153,7 @@ def tile_efficient_skan_batch_kernel(
         def silu_part(h):
             for g in range(NG):
                 nc.scalar.activation(
-                    out=silu_g[:, g, h * HT : (h + 1) * HT, :].rearrange("p t (u e) -> p t u e", e=2),
+                    out=silu_g[g][:, h * HT : (h + 1) * HT, :].rearrange("p t (u e) -> p t u e", e=2),
                     in_=xbank[(h, g)][:].bitcast(BF16).rearrange("p u (t e) -> p t u e", e=2),
                     func=ACT.Silu,
                 )
@@ -173,24 +178,30 @@ def tile_efficient_skan_batch_kernel(
         wgs = {}
         wqs = {}
 
-        def w_bank(b):
+        wbank = {}
+
+        def w_fill(b):
             c, tp = divmod(b, NT // 2)
-            if tp == 0:
-                wgs[c] = wgpool.tile([P, NT * P * 4], BF16, name="wg", align_bytes=64)
-            wgw = wgs[c][:].bitcast(F32)
-            wps = psum.tile([P, 2, 2, P], F32, tag="acc" if b < W_HEAD else "w", bufs=6 if b < W_HEAD else 1, name="wps")
+            wps = psum.tile([P, 2, 2, P], F32, tag="acc", bufs=6, name="wps")
             for tt in range(2):
                 ww = raws[c][:, 2 * tp + tt, :].bitcast(F32)
                 for u in range(2):
                     nc.tensor.transpose(wps[:, tt, u, :], ww[:, u : 2 * P : 2], ident[:])
+            wbank[b] = wps
+            if tp == NT // 2 - 1 and c + 3 < NF * NG:
+                load_w(c + 3)
+
+        def w_copy(b):
+            c, tp = divmod(b, NT // 2)
+            if tp == 0:
+                wgs[c] = wgpool.tile([P, NT * P * 4], BF16, name="wg", align_bytes=64)
+            wgw = wgs[c][:].bitcast(F32)
             dst = wgw[:, 512 * tp : 512 * (tp + 1)].rearrange("p (t o u) -> p t o u", t=2, u=2)
-            src = wps[:].rearrange("p t u o -> p t o u")
+            src = wbank[b][:].rearrange("p t u o -> p t o u")
             if b < W_HEAD:
                 nc.vector.tensor_copy(out=dst, in_=src)
             else:
                 nc.scalar.copy(out=dst, in_=src)
-            if tp == NT // 2 - 1 and c + WB < NF * NG:
-                load_w(c + WB)
 
         def w_quant(c, part):
             if part == 0:
@@ -225,14 +236,15 @@ def tile_efficient_skan_batch_kernel(
             nc.vector.tensor_mul(out=sbs[:], in0=bsum[:], in1=bT[:, NF * NT : NF * NT + NT])
 
         def base_quant():
-            nc.vector.quantize_mx(
-                out=sil_w[:].rearrange("p g t -> p (g t)").bitcast(FP8X4),
-                scales=sil_s[:].rearrange("p g t -> p (g t)"),
-                in_=silu_g[:].rearrange("p g t j -> p (g t j)"),
-            )
+            for g in range(NG):
+                nc.vector.quantize_mx(
+                    out=sil_w[:, g, :].bitcast(FP8X4),
+                    scales=sil_s[:, g, :],
+                    in_=silu_g[g][:].rearrange("p t j -> p (t j)"),
+                )
 
         def base_tile(t):
-            bacc = psum.tile([P, TOK], F32, tag="acc", bufs=6, name="bacc")
+            bacc = psum.tile([P, TOK], F32, tag="w", name="bacc")
             for g in range(NG):
                 nc.tensor.matmul_mx(
                     out=bacc[:],
@@ -390,15 +402,21 @@ def tile_efficient_skan_batch_kernel(
                 )
 
         nbanks = NF * NG * (NT // 2)
-        state = {"bank": 0, "mx": 0, "wq": 0}
+        state = {"bank": 0, "mx": 0, "wq": 0, "fill": 0}
         quant_queue = []
         fin_queue = []
+
+        def fill_to(e):
+            while state["fill"] < min(e, nbanks):
+                w_fill(state["fill"])
+                state["fill"] += 1
 
         def banks(it, count):
             for i in range(count):
                 b = state["bank"]
                 if it >= W_START and b < nbanks:
-                    w_bank(b)
+                    fill_to(b + LEAD)
+                    w_copy(b)
                     if b % 3 == 2:
                         quant_queue.extend([(b // 3, 0), (b // 3, 1)])
                     state["bank"] = b + 1
@@ -420,6 +438,7 @@ def tile_efficient_skan_batch_kernel(
                 s1(it + 1)
             if 0 <= it - 1 < NU:
                 s2(it - 1)
+            banks(it, 1)
             if 0 <= it - 2 < NU:
                 s3a(it - 2)
             banks(it, 1)
@@ -435,22 +454,19 @@ def tile_efficient_skan_batch_kernel(
             if it == BQ:
                 base_quant()
                 bias_part()
-            if 4 <= it < 4 + NT // 2:
-                base_tile(2 * (it - 4))
-                base_tile(2 * (it - 4) + 1)
+            if 4 <= it < 4 + NT:
+                base_tile(it - 4)
             if 0 <= it - 2 < NU and it - 2 not in T_SET:
                 s3b(it - 2, 0)
                 banks(it, 1)
                 s3b(it - 2, 2)
-                banks(it, 1)
             if 0 <= it - LAG4 < NU:
                 s4(it - LAG4)
-            one_quant()
-            if it % 2 or it < 5:
+            for i in range(min(2, len(quant_queue))):
                 one_quant()
-            for i in range(2):
+            for i in range(MXR):
                 n = state["mx"]
-                if n < NU and it >= 4 + NT // 2 and n <= it - LAG4 - 2 and state["wq"] >= 2 * min(n % (NF * NG), NF * NG) + 2:
+                if n < NU and n <= it - LAG4 - 2 and state["wq"] == 2 * NF * NG:
                     s6(n)
                     state["mx"] = n + 1
                     if n % (NF * NG) == NF * NG - 1:

@@ -32,10 +32,19 @@ KV_SET = (0,)
 T_SET = (0, 1, 3, 5, 7, 9, 11, 13, 15, 17, 19, 30, 31)
 W_START = 4
 BQ = 3
-SWB = 20
-LEAD = 5
+BASE_V = (1, 3, 5)
+SWB = 18
+LEAD = 4
+QLAG = 1
+RING = ("r", "r", "r", "w")
+NA = 3
 RT = 3
 MXR = 2
+MXB = 3
+GAIN_LAG = 2
+FB = (("w", "x", "w"), ("x", "acc", "acc"))
+OUT_V = ((1, 1),)
+WQ_LAG = 2
 W_HEAD = 3
 LAG4 = 3
 WB = 5
@@ -129,7 +138,8 @@ def tile_efficient_skan_batch_kernel(
             silu_g.append(sg)
 
         def make_xt(h, g):
-            xb = psum.tile([P, 2, HT], F32, tag="acc", bufs=6, name="xb")
+            r = 2 * h + g
+            xb = psum.tile([P, 2, HT], F32, tag=RING[r], bufs=3 if r < 3 else 1, name="xb")
             for mi in range(2):
                 xw = x_sb[:, 2 * h + mi, :].bitcast(F32)
                 for u in range(2):
@@ -182,7 +192,7 @@ def tile_efficient_skan_batch_kernel(
 
         def w_fill(b):
             c, tp = divmod(b, NT // 2)
-            wps = psum.tile([P, 2, 2, P], F32, tag="acc", bufs=6, name="wps")
+            wps = psum.tile([P, 2, 2, P], F32, tag=RING[b % 4], bufs=3 if b % 4 < 3 else 1, name="wps")
             for tt in range(2):
                 ww = raws[c][:, 2 * tp + tt, :].bitcast(F32)
                 for u in range(2):
@@ -224,7 +234,7 @@ def tile_efficient_skan_batch_kernel(
         basec = []
 
         def bias_part():
-            bps = psum.tile([P, P], BF16, tag="w", name="bps")
+            bps = psum.tile([P, P], BF16, tag="acc", bufs=NA, name="bps")
             nc.tensor.transpose(bps[:], braw[:], identb[:])
             nc.vector.tensor_copy(out=bT[:, 0 : NF * NT + NT], in_=bps[:, 0 : NF * NT + NT])
             nc.vector.tensor_reduce(
@@ -244,7 +254,7 @@ def tile_efficient_skan_batch_kernel(
                 )
 
         def base_tile(t):
-            bacc = psum.tile([P, TOK], F32, tag="w", name="bacc")
+            bacc = psum.tile([P, TOK], F32, tag="acc", bufs=NA, name="bacc")
             for g in range(NG):
                 nc.tensor.matmul_mx(
                     out=bacc[:],
@@ -255,8 +265,19 @@ def tile_efficient_skan_batch_kernel(
                     start=(g == 0),
                     stop=(g == NG - 1),
                 )
+            bacs[t] = bacc
+
+        bacs = {}
+
+        def base_out(t):
+            bacc = bacs[t]
             bc = const.tile([P, TOK], F32, name="basec%d" % t)
-            nc.scalar.activation(out=bc[:], in_=bacc[:], func=ACT.Identity, bias=sbs[:, t : t + 1])
+            if t in BASE_V:
+                nc.vector.tensor_scalar(
+                    out=bc[:], in0=bacc[:], scalar1=sbs[:, t : t + 1], scalar2=None, op0=ALU.add
+                )
+            else:
+                nc.scalar.activation(out=bc[:], in_=bacc[:], func=ACT.Identity, bias=sbs[:, t : t + 1])
             basec.append(bc)
 
         kt = {}
@@ -264,7 +285,7 @@ def tile_efficient_skan_batch_kernel(
         sct = {}
         grt = {}
         swt = {}
-        acc = []
+        acc = {}
 
         def unit(n):
             h, rest = divmod(n, NF * NG)
@@ -357,14 +378,16 @@ def tile_efficient_skan_batch_kernel(
             )
             swt[n] = (sw, ss)
 
-        def s6(n):
+        def s6(n, tiles):
             h, f, g = unit(n)
             if n == 0:
-                for t in range(NT):
-                    acc.append(psum.tile([P, TOK], F32, tag="acc", bufs=6, name="acc%d" % t))
+                for t in tiles:
+                    acc[t] = psum.tile(
+                        [P, TOK], F32, tag="acc" if t < NA else "r", bufs=3, name="acc%d" % t
+                    )
             sw, ss = swt[n]
             wq, wsc = wqs[g * NF + f]
-            for t in range(NT):
+            for t in tiles:
                 lo = t * P
                 nc.tensor.matmul_mx(
                     out=acc[t][:, h * HT : (h + 1) * HT],
@@ -378,33 +401,56 @@ def tile_efficient_skan_batch_kernel(
 
         outv = out.rearrange("b n o -> (b n) o").rearrange("(m p) o -> p m o", p=P)
 
-        def finish(h, parts):
-            for tp in parts:
-                fps = psum.tile([P, 2, 2, P], F32, tag=("w", "x")[tp % 2 if h == 1 else 0], name="fps")
-                for tt in range(2):
-                    t = 2 * tp + tt
-                    ot = opool.tile([P, HT], F32, name="ot")
-                    nc.vector.scalar_tensor_tensor(
-                        out=ot[:],
-                        in0=acc[t][:, h * HT : (h + 1) * HT],
-                        scalar=bT[:, NF * NT + t : NF * NT + t + 1],
-                        in1=basec[t][:, h * HT : (h + 1) * HT],
-                        op0=ALU.mult,
-                        op1=ALU.add,
-                    )
-                    for mi in range(2):
-                        nc.tensor.transpose(fps[:, mi, tt, :], ot[:, mi * P : (mi + 1) * P], ident[:])
-                of = opool.tile([P, 2, 2 * P], F32, name="of")
-                if True:
-                    nc.scalar.copy(out=of[:], in_=fps[:].rearrange("p m t o -> p m (t o)"))
-                nc.sync.dma_start(
-                    out=outv[:, 2 * h : 2 * h + 2, 2 * P * tp : 2 * P * (tp + 1)], in_=of[:]
+        fpss = {}
+
+        def gain(h, tiles):
+            for t in tiles:
+                bc = basec[t][:, h * HT : (h + 1) * HT]
+                nc.vector.scalar_tensor_tensor(
+                    out=bc,
+                    in0=acc[t][:, h * HT : (h + 1) * HT],
+                    scalar=bT[:, NF * NT + t : NF * NT + t + 1],
+                    in1=bc,
+                    op0=ALU.mult,
+                    op1=ALU.add,
                 )
 
+        def turn(h, tp):
+            fps = psum.tile([P, 2, 2, P], F32, tag=FB[h][tp], bufs=NA if FB[h][tp] == "acc" else 1, name="fps")
+            for tt in range(2):
+                for mi in range(2):
+                    lo = h * HT + mi * P
+                    nc.tensor.transpose(
+                        fps[:, mi, tt, :], basec[2 * tp + tt][:, lo : lo + P], ident[:]
+                    )
+            fpss[(h, tp)] = fps
+
+        def store(h, tp):
+            of = opool.tile([P, 2, 2 * P], F32, tag="of", bufs=6, name="of")
+            src = fpss[(h, tp)][:].rearrange("p m t o -> p m (t o)")
+            if (h, tp) in OUT_V:
+                nc.vector.tensor_copy(out=of[:], in_=src)
+            else:
+                nc.scalar.copy(out=of[:], in_=src)
+            nc.sync.dma_start(
+                out=outv[:, 2 * h : 2 * h + 2, 2 * P * tp : 2 * P * (tp + 1)], in_=of[:]
+            )
+
         nbanks = NF * NG * (NT // 2)
-        state = {"bank": 0, "mx": 0, "wq": 0, "fill": 0}
+        state = {"bank": 0, "mxa": 0, "gained": 0, "mxb": 0, "wq": 0, "fill": 0}
         quant_queue = []
-        fin_queue = []
+        later = []
+
+
+        def end_part(it, h, part):
+            if h == 0:
+                later.append((it + GAIN_LAG, h, part))
+
+        def finish_some(it):
+            while later and later[0][0] <= it:
+                h, part = later.pop(0)[1:]
+                gain(h, range(NA * part, NA * (part + 1)))
+                state["gained"] += 1
 
         def fill_to(e):
             while state["fill"] < min(e, nbanks):
@@ -418,12 +464,12 @@ def tile_efficient_skan_batch_kernel(
                     fill_to(b + LEAD)
                     w_copy(b)
                     if b % 3 == 2:
-                        quant_queue.extend([(b // 3, 0), (b // 3, 1)])
+                        quant_queue.extend([(it, b // 3, 0), (it, b // 3, 1)])
                     state["bank"] = b + 1
 
-        def one_quant():
-            if quant_queue:
-                c, part = quant_queue.pop(0)
+        def one_quant(it):
+            if quant_queue and quant_queue[0][0] + QLAG <= it:
+                c, part = quant_queue.pop(0)[1:]
                 w_quant(c, part)
                 state["wq"] = 2 * c + part + 1
 
@@ -449,32 +495,58 @@ def tile_efficient_skan_batch_kernel(
             if it == 3:
                 for i in range(W_HEAD // 3):
                     banks(W_START, 3)
-                    one_quant()
-                    one_quant()
+                    one_quant(it + 1)
+                    one_quant(it + 1)
             if it == BQ:
                 base_quant()
                 bias_part()
+            if 5 <= it < 5 + NT:
+                base_out(it - 5)
             if 4 <= it < 4 + NT:
                 base_tile(it - 4)
             if 0 <= it - 2 < NU and it - 2 not in T_SET:
                 s3b(it - 2, 0)
                 banks(it, 1)
                 s3b(it - 2, 2)
+            if it == NU + 2:
+                s5(it - LAG4 - 1)
             if 0 <= it - LAG4 < NU:
                 s4(it - LAG4)
             for i in range(min(2, len(quant_queue))):
-                one_quant()
+                one_quant(it)
+            finish_some(it)
             for i in range(MXR):
-                n = state["mx"]
-                if n < NU and n <= it - LAG4 - 2 and state["wq"] == 2 * NF * NG:
-                    s6(n)
-                    state["mx"] = n + 1
+                n = state["mxa"]
+                ready = state["wq"] >= min(2 * n + 2 + WQ_LAG, 2 * NF * NG)
+                if n == NU // 2 and not state["gained"]:
+                    ready = False
+                if it >= 5 + NT and n < NU and n <= it - LAG4 - 2 and ready:
+                    s6(n, range(NA))
+                    state["mxa"] = n + 1
                     if n % (NF * NG) == NF * NG - 1:
-                        if n + 1 < NU:
-                            fin_queue.extend([0, 1, 2])
-                        else:
-                            finish(1, (0, 1, 2))
-            if fin_queue:
-                finish(0, (fin_queue.pop(0),))
-            if 0 <= it - LAG4 - 1 < NU:
+                        end_part(it, n // (NF * NG), 0)
+            for i in range(MXB):
+                n = state["mxb"]
+                if n == NU // 2 and state["gained"] < 2:
+                    break
+                if n < state["mxa"] and state["bank"] == nbanks:
+                    s6(n, range(NA, NT))
+                    state["mxb"] = n + 1
+                    if n % (NF * NG) == NF * NG - 1:
+                        end_part(it, n // (NF * NG), 1)
+            if it == NU + 1:
+                turn(0, 0)
+                turn(0, 1)
+                store(0, 0)
+                store(0, 1)
+            if state["mxb"] == NU and "end" not in state:
+                state["end"] = 1
+                turn(0, 2)
+                store(0, 2)
+                for h, part in ((1, 0), (1, 1)):
+                    gain(h, range(NA * part, NA * (part + 1)))
+                    for tp in ((0,), (1, 2))[part]:
+                        turn(h, tp)
+                        store(h, tp)
+            if 0 <= it - LAG4 - 1 < NU and it != NU + 2:
                 s5(it - LAG4 - 1)

@@ -34,15 +34,15 @@ W_START = 4
 BQ = 3
 BASE_V = (1, 3, 5)
 SWB = 18
-LEAD = 4
+LEAD = 3
 QLAG = 1
-RING = ("r", "r", "r", "w")
+RING = 3
 NA = 3
 RT = 3
 MXR = 2
 MXB = 3
 GAIN_LAG = 2
-FB = (("w", "x", "w"), ("x", "acc", "acc"))
+FB = (("x", "w", "x"), ("acc", "acc", "acc"))
 OUT_V = ((1, 1),)
 WQ_LAG = 2
 W_HEAD = 3
@@ -138,8 +138,9 @@ def tile_efficient_skan_batch_kernel(
             silu_g.append(sg)
 
         def make_xt(h, g):
-            r = 2 * h + g
-            xb = psum.tile([P, 2, HT], F32, tag=RING[r], bufs=3 if r < 3 else 1, name="xb")
+            xb = psum.tile(
+                [P, 2, HT], F32, tag="r" if 2 * h + g < RING else "acc", bufs=3, name="xb"
+            )
             for mi in range(2):
                 xw = x_sb[:, 2 * h + mi, :].bitcast(F32)
                 for u in range(2):
@@ -168,6 +169,19 @@ def tile_efficient_skan_batch_kernel(
                     func=ACT.Silu,
                 )
 
+        coefp = []
+
+        def fill_coef():
+            cps = psum.tile([P, NF * NG * 4], F32, tag="w", name="cps")
+            nc.tensor.matmul(
+                cps[:],
+                identb[:],
+                craw[:].rearrange("p g (j f) -> p f g j", f=NF),
+                start=True,
+                stop=True,
+            )
+            coefp.append(cps)
+
         xp = {}
 
         def fill_xp(h, g):
@@ -192,7 +206,7 @@ def tile_efficient_skan_batch_kernel(
 
         def w_fill(b):
             c, tp = divmod(b, NT // 2)
-            wps = psum.tile([P, 2, 2, P], F32, tag=RING[b % 4], bufs=3 if b % 4 < 3 else 1, name="wps")
+            wps = psum.tile([P, 2, 2, P], F32, tag="r", bufs=RING, name="wps")
             for tt in range(2):
                 ww = raws[c][:, 2 * tp + tt, :].bitcast(F32)
                 for u in range(2):
@@ -360,7 +374,7 @@ def tile_efficient_skan_batch_kernel(
                 nc.vector.tensor_tensor(
                     out=grp[:],
                     in0=sct[n][:],
-                    in1=coefT[:, ci : ci + 4].unsqueeze(1).to_broadcast([P, HT, 4]),
+                    in1=coefp[0][:, ci : ci + 4].unsqueeze(1).to_broadcast([P, HT, 4]),
                     op=ALU.mult,
                 )
             else:
@@ -474,6 +488,7 @@ def tile_efficient_skan_batch_kernel(
                 state["wq"] = 2 * c + part + 1
 
         fill_xp(0, 0)
+        fill_coef()
         make_xt(0, 1)
         make_xt(1, 0)
         make_xt(1, 1)
@@ -536,8 +551,9 @@ def tile_efficient_skan_batch_kernel(
                         end_part(it, n // (NF * NG), 1)
             if it == NU + 1:
                 turn(0, 0)
-                turn(0, 1)
                 store(0, 0)
+            if it == NU + 2:
+                turn(0, 1)
                 store(0, 1)
             if state["mxb"] == NU and "end" not in state:
                 state["end"] = 1

@@ -34,15 +34,15 @@ W_START = 4
 BQ = 3
 BASE_V = (1, 3, 5)
 SWB = 18
-LEAD = 3
+LEAD = 4
 QLAG = 1
-RING = 3
-NA = 3
+RING = 4
+NA = 2
 RT = 3
 MXR = 2
 MXB = 3
 GAIN_LAG = 2
-FB = (("x", "w", "x"), ("acc", "acc", "acc"))
+FB = (("x", "w", "x"), ("acc", "acc", "w"))
 OUT_V = ((1, 1),)
 WQ_LAG = 2
 W_HEAD = 3
@@ -75,9 +75,9 @@ def tile_efficient_skan_batch_kernel(
 
         gb = const.tile([P, NF], BF16, name="gb")
         nc.scalar.dma_start(out=gb[:], in_=grid.partition_broadcast(P))
-        craw = const.tile([P, NG, 4 * NF], BF16, name="craw")
+        craw = const.tile([P, 2 * NG, 2 * NF], BF16, name="craw")
         nc.scalar.dma_start(
-            out=craw[:], in_=coef.rearrange("(g p j) f -> p g (j f)", g=NG, p=P)
+            out=craw[:], in_=coef.rearrange("(a p e) f -> p a (e f)", a=2 * NG, p=P)
         )
         braw = const.tile([P, P], BF16, name="braw")
         nc.vector.memset(braw[:], 0.0)
@@ -126,8 +126,8 @@ def tile_efficient_skan_batch_kernel(
         )
         coefT = const.tile([P, NF * NG * 4], F32, name="coefT")
         nc.vector.tensor_copy(
-            out=coefT[:].rearrange("p (f g j) -> p f g j", f=NF, g=NG),
-            in_=craw[:].rearrange("p g (j f) -> p f g j", f=NF),
+            out=coefT[:].rearrange("p (f a e) -> p f a e", f=NF, e=2),
+            in_=craw[:].rearrange("p a (e f) -> p f a e", f=NF),
         )
 
         xs = {}
@@ -139,7 +139,7 @@ def tile_efficient_skan_batch_kernel(
 
         def make_xt(h, g):
             xb = psum.tile(
-                [P, 2, HT], F32, tag="r" if 2 * h + g < RING else "acc", bufs=3, name="xb"
+                [P, 2, HT], F32, tag="r", bufs=RING, name="xb"
             )
             for mi in range(2):
                 xw = x_sb[:, 2 * h + mi, :].bitcast(F32)
@@ -154,7 +154,7 @@ def tile_efficient_skan_batch_kernel(
         def copy_xt(h, g):
             xc = const.tile([P, 4 * HT], BF16, name="xs%d%d" % (h, g))
             dst = xc[:].bitcast(F32)
-            src = xbank[(h, g)][:].rearrange("p u t -> p (u t)")
+            src = xp[(h, g)][:].rearrange("p u t -> p (u t)")
             if h == 0 and g == 0:
                 nc.scalar.copy(out=dst, in_=src)
             else:
@@ -176,7 +176,7 @@ def tile_efficient_skan_batch_kernel(
             nc.tensor.matmul(
                 cps[:],
                 identb[:],
-                craw[:].rearrange("p g (j f) -> p f g j", f=NF),
+                craw[:].rearrange("p a (e f) -> p f a e", f=NF),
                 start=True,
                 stop=True,
             )
@@ -184,19 +184,18 @@ def tile_efficient_skan_batch_kernel(
 
         xp = {}
 
-        def fill_xp(h, g):
-            xt = psum.tile([P, 2, HT], F32, tag="x", name="xt")
+        def fill_xp(h, g, tag="x", bufs=1):
+            xt = psum.tile([P, 2, HT], F32, tag=tag, bufs=bufs, name="xt")
             for mi in range(2):
                 xw = x_sb[:, 2 * h + mi, :].bitcast(F32)
                 for u in range(2):
+                    lo = 256 * g + P * u
                     nc.tensor.transpose(
-                        xt[:, u, mi * P : (mi + 1) * P],
-                        xw[:, 256 * g + u : 256 * (g + 1) : 2],
-                        ident[:],
+                        xt[:, u, mi * P : (mi + 1) * P], xw[:, lo : lo + P], ident[:]
                     )
             xp[(h, g)] = xt
 
-        make_xt(0, 0)
+        fill_xp(0, 0)
         copy_xt(0, 0)
 
         wgs = {}
@@ -210,7 +209,7 @@ def tile_efficient_skan_batch_kernel(
             for tt in range(2):
                 ww = raws[c][:, 2 * tp + tt, :].bitcast(F32)
                 for u in range(2):
-                    nc.tensor.transpose(wps[:, tt, u, :], ww[:, u : 2 * P : 2], ident[:])
+                    nc.tensor.transpose(wps[:, tt, u, :], ww[:, u * P : (u + 1) * P], ident[:])
             wbank[b] = wps
             if tp == NT // 2 - 1 and c + 3 < NF * NG:
                 load_w(c + 3)
@@ -397,7 +396,7 @@ def tile_efficient_skan_batch_kernel(
             if n == 0:
                 for t in tiles:
                     acc[t] = psum.tile(
-                        [P, TOK], F32, tag="acc" if t < NA else "r", bufs=3, name="acc%d" % t
+                        [P, TOK], F32, tag="acc" if t < NA else "r", bufs=NA if t < NA else RING, name="acc%d" % t
                     )
             sw, ss = swt[n]
             wq, wsc = wqs[g * NF + f]
@@ -463,7 +462,7 @@ def tile_efficient_skan_batch_kernel(
         def finish_some(it):
             while later and later[0][0] <= it:
                 h, part = later.pop(0)[1:]
-                gain(h, range(NA * part, NA * (part + 1)))
+                gain(h, (range(NA), range(NA, NT))[part])
                 state["gained"] += 1
 
         def fill_to(e):
@@ -487,13 +486,15 @@ def tile_efficient_skan_batch_kernel(
                 w_quant(c, part)
                 state["wq"] = 2 * c + part + 1
 
-        fill_xp(0, 0)
         fill_coef()
+        make_xt(0, 0)
         make_xt(0, 1)
         make_xt(1, 0)
         make_xt(1, 1)
         silu_part(0)
         silu_part(1)
+        fill_xp(0, 1, "acc", NA)
+        fill_xp(1, 0, "acc", NA)
         for it in range(-1, NU + LAG4 + 16):
             if it + 1 < NU:
                 s1(it + 1)
@@ -506,6 +507,7 @@ def tile_efficient_skan_batch_kernel(
             if it == 1:
                 copy_xt(0, 1)
                 copy_xt(1, 0)
+                fill_xp(1, 1, "acc", NA)
                 copy_xt(1, 1)
             if it == 3:
                 for i in range(W_HEAD // 3):
@@ -523,7 +525,8 @@ def tile_efficient_skan_batch_kernel(
                 s3b(it - 2, 0)
                 banks(it, 1)
                 s3b(it - 2, 2)
-            if it == NU + 2:
+            tail = it > NU
+            if tail and it - LAG4 - 1 < NU:
                 s5(it - LAG4 - 1)
             if 0 <= it - LAG4 < NU:
                 s4(it - LAG4)
@@ -535,7 +538,7 @@ def tile_efficient_skan_batch_kernel(
                 ready = state["wq"] >= min(2 * n + 2 + WQ_LAG, 2 * NF * NG)
                 if n == NU // 2 and not state["gained"]:
                     ready = False
-                if it >= 5 + NT and n < NU and n <= it - LAG4 - 2 and ready:
+                if it >= 5 + NT and n < NU and n <= it - LAG4 - 2 + tail and ready:
                     s6(n, range(NA))
                     state["mxa"] = n + 1
                     if n % (NF * NG) == NF * NG - 1:
@@ -560,9 +563,9 @@ def tile_efficient_skan_batch_kernel(
                 turn(0, 2)
                 store(0, 2)
                 for h, part in ((1, 0), (1, 1)):
-                    gain(h, range(NA * part, NA * (part + 1)))
+                    gain(h, (range(NA), range(NA, NT))[part])
                     for tp in ((0,), (1, 2))[part]:
                         turn(h, tp)
                         store(h, tp)
-            if 0 <= it - LAG4 - 1 < NU and it != NU + 2:
+            if 0 <= it - LAG4 - 1 < NU and not tail:
                 s5(it - LAG4 - 1)

@@ -28,27 +28,24 @@ NU = 2 * NF * NG
 
 FLOPS = 2 * TOK * K * OUT * (NF + 1)
 
-KV_SET = (0,)
-T_SET = (0, 1, 3, 5, 7, 9, 11, 13, 15, 17, 19, 30, 31)
-W_START = 4
-BQ = 3
-BASE_V = (1, 3, 5)
-SWB = 18
-LEAD = 4
-QLAG = 1
+NP = NU // 2
+BASE_V = (0, 2, 4)
+W_S = (1, 1, 1, 1, 1)
+W_S0 = 4
+W_V = 0
+W_HEAD = 2
 RING = 4
 NA = 2
-RT = 3
-MXR = 2
-MXB = 3
-GAIN_LAG = 2
+LEAD = 4
+MXA = 4
+MXB = 4
+GAIN_LAG = 1
 FB = (("x", "w", "x"), ("acc", "acc", "w"))
 OUT_V = ((1, 1),)
-WQ_LAG = 2
-W_HEAD = 3
-LAG4 = 3
+SWB = 9
 WB = 5
-KG_BUFS = 7
+WGB = 6
+NN = (11, 12, 13, 14)
 
 
 def tile_efficient_skan_batch_kernel(
@@ -58,33 +55,39 @@ def tile_efficient_skan_batch_kernel(
     with ExitStack() as ctx:
         const = ctx.enter_context(tc.tile_pool(name="const", bufs=1))
         wpool = ctx.enter_context(tc.tile_pool(name="wraw", bufs=WB))
-        wgpool = ctx.enter_context(tc.tile_pool(name="wg", bufs=3))
-        kgpool = ctx.enter_context(tc.tile_pool(name="kgp", bufs=KG_BUFS))
-        rpool = ctx.enter_context(tc.tile_pool(name="r", bufs=3))
+        wgpool = ctx.enter_context(tc.tile_pool(name="wg", bufs=WGB))
+        kgpool = ctx.enter_context(tc.tile_pool(name="kgp", bufs=1))
+        rpool = ctx.enter_context(tc.tile_pool(name="r", bufs=4))
         snpool = ctx.enter_context(tc.tile_pool(name="sn", bufs=2))
-        scpool = ctx.enter_context(tc.tile_pool(name="sc", bufs=3))
+        scpool = ctx.enter_context(tc.tile_pool(name="sc", bufs=4))
         swpool = ctx.enter_context(tc.tile_pool(name="sw", bufs=SWB))
         opool = ctx.enter_context(tc.tile_pool(name="o", bufs=3))
         psum = ctx.enter_context(tc.psum_pool(name="psum", bufs=1))
         ctx.enter_context(tc.manual_schedule())
 
-        xv = x.rearrange("b n k -> (b n) k").rearrange("(m p) k -> m p k", p=P)
-        x_sb = const.tile([P, NM, K], BF16, name="x_sb")
-        for m in range(NM):
-            nc.sync.dma_start(out=x_sb[:, m, :], in_=xv[m])
+        xv = x.rearrange("b n k -> (b n) k").rearrange("(m p) k -> p m k", p=P)
+        x_sb = {}
+        for h in range(2):
+            for g in range(NG):
+                xt_in = const.tile([P, 2, K // NG], BF16, name="x_in%d%d" % (h, g))
+                nc.sync.dma_start(
+                    out=xt_in[:],
+                    in_=xv[:, 2 * h : 2 * h + 2, K // NG * g : K // NG * (g + 1)],
+                )
+                x_sb[(h, g)] = xt_in
 
         gb = const.tile([P, NF], BF16, name="gb")
         nc.scalar.dma_start(out=gb[:], in_=grid.partition_broadcast(P))
         craw = const.tile([P, 2 * NG, 2 * NF], BF16, name="craw")
-        nc.scalar.dma_start(
+        nc.sync.dma_start(
             out=craw[:], in_=coef.rearrange("(a p e) f -> p a (e f)", a=2 * NG, p=P)
         )
         braw = const.tile([P, P], BF16, name="braw")
         nc.vector.memset(braw[:], 0.0)
-        nc.scalar.dma_start(
+        nc.sync.dma_start(
             out=braw[0 : NF * NT, :], in_=conv_b.rearrange("f (t c) -> (f t) c", c=P)
         )
-        nc.scalar.dma_start(
+        nc.sync.dma_start(
             out=braw[NF * NT : NF * NT + NT, :], in_=scale_sp.rearrange("(t c) -> t c", c=P)
         )
 
@@ -125,10 +128,6 @@ def tile_efficient_skan_batch_kernel(
             out=cturn[:], in0=g32[:], scalar1=1.0 / (2.0 * math.pi), scalar2=None, op0=ALU.mult
         )
         coefT = const.tile([P, NF * NG * 4], F32, name="coefT")
-        nc.vector.tensor_copy(
-            out=coefT[:].rearrange("p (f a e) -> p f a e", f=NF, e=2),
-            in_=craw[:].rearrange("p a (e f) -> p f a e", f=NF),
-        )
 
         xs = {}
         xbank = {}
@@ -142,11 +141,11 @@ def tile_efficient_skan_batch_kernel(
                 [P, 2, HT], F32, tag="r", bufs=RING, name="xb"
             )
             for mi in range(2):
-                xw = x_sb[:, 2 * h + mi, :].bitcast(F32)
+                xw = x_sb[(h, g)][:, mi, :].bitcast(F32)
                 for u in range(2):
                     nc.tensor.transpose(
                         xb[:, u, mi * P : (mi + 1) * P],
-                        xw[:, 256 * g + u : 256 * (g + 1) : 2],
+                        xw[:, u : 2 * P : 2],
                         ident[:],
                     )
             xbank[(h, g)] = xb
@@ -155,10 +154,7 @@ def tile_efficient_skan_batch_kernel(
             xc = const.tile([P, 4 * HT], BF16, name="xs%d%d" % (h, g))
             dst = xc[:].bitcast(F32)
             src = xp[(h, g)][:].rearrange("p u t -> p (u t)")
-            if h == 0 and g == 0:
-                nc.scalar.copy(out=dst, in_=src)
-            else:
-                nc.vector.tensor_copy(out=dst, in_=src)
+            nc.vector.tensor_copy(out=dst, in_=src)
             xs[(h, g)] = xc
 
         def silu_part(h):
@@ -187,11 +183,10 @@ def tile_efficient_skan_batch_kernel(
         def fill_xp(h, g, tag="x", bufs=1):
             xt = psum.tile([P, 2, HT], F32, tag=tag, bufs=bufs, name="xt")
             for mi in range(2):
-                xw = x_sb[:, 2 * h + mi, :].bitcast(F32)
+                xw = x_sb[(h, g)][:, mi, :].bitcast(F32)
                 for u in range(2):
-                    lo = 256 * g + P * u
                     nc.tensor.transpose(
-                        xt[:, u, mi * P : (mi + 1) * P], xw[:, lo : lo + P], ident[:]
+                        xt[:, u, mi * P : (mi + 1) * P], xw[:, P * u : P * (u + 1)], ident[:]
                     )
             xp[(h, g)] = xt
 
@@ -214,30 +209,23 @@ def tile_efficient_skan_batch_kernel(
             if tp == NT // 2 - 1 and c + 3 < NF * NG:
                 load_w(c + 3)
 
-        def w_copy(b):
-            c, tp = divmod(b, NT // 2)
-            if tp == 0:
-                wgs[c] = wgpool.tile([P, NT * P * 4], BF16, name="wg", align_bytes=64)
+        def w_copy(b, by_vector):
+            c, half = divmod(b, 2)
+            if half == 0:
+                wgs[c] = wgpool.tile([P, 4 * P * 4], BF16, name="wg", align_bytes=64)
             wgw = wgs[c][:].bitcast(F32)
-            dst = wgw[:, 512 * tp : 512 * (tp + 1)].rearrange("p (t o u) -> p t o u", t=2, u=2)
+            dst = wgw[:, 512 * half : 512 * (half + 1)].rearrange("p (t o u) -> p t o u", t=2, u=2)
             src = wbank[b][:].rearrange("p t u o -> p t o u")
-            if b < W_HEAD:
+            if by_vector:
                 nc.vector.tensor_copy(out=dst, in_=src)
             else:
                 nc.scalar.copy(out=dst, in_=src)
 
-        def w_quant(c, part):
-            if part == 0:
-                wq = const.tile([P, NT * P], U32, name="wq%d" % c, align_bytes=64)
-                wsc = const.tile([P, NT * P], U8, name="wsc%d" % c, align_bytes=64)
-                wqs[c] = (wq, wsc)
-            wq, wsc = wqs[c]
-            lo, hi = ((0, 512), (512, 768))[part]
-            nc.vector.quantize_mx(
-                out=wq[:, lo:hi].bitcast(FP8X4),
-                scales=wsc[:, lo:hi],
-                in_=wgs[c][:, 4 * lo : 4 * hi],
-            )
+        def w_quant(c):
+            wq = const.tile([P, 4 * P], U32, name="wq%d" % c, align_bytes=64)
+            wsc = const.tile([P, 4 * P], U8, name="wsc%d" % c, align_bytes=64)
+            wqs[c] = (wq, wsc)
+            nc.vector.quantize_mx(out=wq[:].bitcast(FP8X4), scales=wsc[:], in_=wgs[c][:])
 
         bT = const.tile([P, 64], F32, name="bT")
         bsum = const.tile([P, NT], F32, name="bsum")
@@ -305,109 +293,117 @@ def tile_efficient_skan_batch_kernel(
             g, f = divmod(rest, NF)
             return h, f, g
 
-        def s1(n):
-            h, f, g = unit(n)
-            kk = kgpool.tile([P, 4 * HT], I32, tag="kg", name="kk", align_bytes=64)
-            if n not in KV_SET:
+        def turns(m):
+            kk = kgpool.tile([P, 2, 4 * HT], I32, tag=("kg0", "kg1")[m % 2], name="kk", align_bytes=64)
+            for i in range(2):
+                h, f, g = unit(2 * m + i)
                 nc.gpsimd.tensor_scalar(
-                    out=kk[:], in0=xs[(h, g)][:], scalar1=cturn[:, f : f + 1], scalar2=0.0,
+                    out=kk[:, i, :], in0=xs[(h, g)][:], scalar1=cturn[:, f : f + 1], scalar2=0.0,
                     op0=ALU.mult, op1=ALU.add,
                 )
-            else:
-                nc.vector.tensor_scalar(
-                    out=kk[:], in0=xs[(h, g)][:], scalar1=cturn[:, f : f + 1], scalar2=None,
-                    op0=ALU.mult,
-                )
-            kt[n] = kk
+            kt[m] = kk
 
-        def s2(n):
-            h, f, g = unit(n)
-            rr = rpool.tile([P, 4 * HT], F32, name="rr")
-            src = xp[(h, g)][:].rearrange("p u t -> p (u t)").bitcast(BF16)
-            nc.vector.scalar_tensor_tensor(
-                out=rr[:],
-                in0=src,
-                scalar=cturn[:, f : f + 1],
-                in1=kt[n][:],
-                op0=ALU.mult,
-                op1=ALU.subtract,
-            )
-            rt[n] = rr
+        def reduce(m):
+            for i in range(2):
+                n = 2 * m + i
+                h, f, g = unit(n)
+                rr = rpool.tile([P, 4 * HT], F32, name="rr")
+                nc.vector.scalar_tensor_tensor(
+                    out=rr[:],
+                    in0=xp[(h, g)][:].rearrange("p u t -> p (u t)").bitcast(BF16),
+                    scalar=cturn[:, f : f + 1],
+                    in1=kt[m][:, i, :],
+                    op0=ALU.mult,
+                    op1=ALU.subtract,
+                )
+                rt[n] = rr
             if n % NF == NF - 1 and n + 1 < NU:
                 fill_xp(*unit(n + 1)[0::2])
 
-        def s3a(n):
-            rr = rt[n]
-            if n in T_SET:
-                sn = snpool.tile([P, HT, 4], F32, name="sn")
-                nc.scalar.activation(
-                    out=sn[:].rearrange("p t (u e) -> p t u e", e=2),
-                    in_=rr[:].rearrange("p (u t e) -> p t u e", u=2, e=2),
-                    func=ACT.Sin,
-                    scale=2.0 * math.pi,
-                )
-                sct[n] = sn
-            else:
-                nc.scalar.activation(out=rr[:], in_=rr[:], func=ACT.Sin, scale=2.0 * math.pi)
+        def sine_even(m):
+            if m in NN:
+                sine(2 * m)
+                return
+            sn = snpool.tile([P, HT, 4], F32, name="sn")
+            nc.scalar.activation(
+                out=sn[:].rearrange("p t (u e) -> p t u e", e=2),
+                in_=rt[2 * m][:].rearrange("p (u t e) -> p t u e", u=2, e=2),
+                func=ACT.Sin,
+                scale=2.0 * math.pi,
+            )
+            sct[2 * m] = sn
 
-        def s3b(n, j0):
+        def sine(n):
+            rr = rt[n]
+            nc.scalar.activation(out=rr[:], in_=rr[:], func=ACT.Sin, scale=2.0 * math.pi)
+
+        def coef_rows(n, js):
             h, f, g = unit(n)
             ci = (f * NG + g) * 4
-            if j0 == 0:
+            if js[0] == 0:
                 sct[n] = scpool.tile([P, 4, HT], BF16, name="sc")
-            sc = sct[n]
             rv = rt[n][:].rearrange("p (u t e) -> p u e t", u=2, e=2)
-            for j in range(j0, j0 + 2):
+            for j in js:
                 nc.scalar.activation(
-                    out=sc[:, j, :],
+                    out=sct[n][:, j, :],
                     in_=rv[:, j // 2, j % 2, :],
                     func=ACT.Copy,
                     scale=coefT[:, ci + j : ci + j + 1],
                 )
 
-        def s4(n):
-            h, f, g = unit(n)
+        def product_even(m):
+            h, f, g = unit(2 * m)
             ci = (f * NG + g) * 4
-            grp = kgpool.tile([P, HT, 4], BF16, tag="kg", name="grp", align_bytes=64)
-            if n in T_SET:
-                nc.vector.tensor_tensor(
-                    out=grp[:],
-                    in0=sct[n][:],
-                    in1=coefp[0][:, ci : ci + 4].unsqueeze(1).to_broadcast([P, HT, 4]),
-                    op=ALU.mult,
-                )
-            else:
-                nc.vector.tensor_copy(
-                    out=grp[:].rearrange("p (c i) j -> p c j i", i=4),
-                    in_=sct[n][:].rearrange("p j (c i) -> p c j i", i=4),
-                )
-            grt[n] = grp
-
-        def s5(n):
-            sw = swpool.tile([P, HT], U32, name="sw", align_bytes=64)
-            ss = swpool.tile([P, HT], U8, name="ss", align_bytes=64)
-            nc.vector.quantize_mx(
-                out=sw[:].bitcast(FP8X4), scales=ss[:], in_=grt[n][:].rearrange("p t j -> p (t j)")
+            grp = kgpool.tile([P, 2, HT, 4], BF16, tag=("kg1", "kg0")[m % 2], name="grp", align_bytes=64)
+            if m in NN:
+                grt[m] = grp
+                group(2 * m)
+                return
+            nc.vector.tensor_tensor(
+                out=grp[:, 0],
+                in0=sct[2 * m][:],
+                in1=coefp[0][:, ci : ci + 4].unsqueeze(1).to_broadcast([P, HT, 4]),
+                op=ALU.mult,
             )
-            swt[n] = (sw, ss)
+            grt[m] = grp
 
-        def s6(n, tiles):
+        def group(n):
+            nc.vector.tensor_copy(
+                out=grt[n // 2][:, n % 2].rearrange("p (c i) j -> p c j i", i=4),
+                in_=sct[n][:].rearrange("p j (c i) -> p c j i", i=4),
+            )
+
+        def quant_pair(m, parts):
+            if parts != (1,):
+                sw = swpool.tile([P, 2, HT], U32, name="sw", align_bytes=64)
+                ss = swpool.tile([P, 2, HT], U8, name="ss", align_bytes=64)
+                swt[m] = (sw, ss)
+            sw, ss = swt[m]
+            lo, hi = parts[0], parts[-1] + 1
+            nc.vector.quantize_mx(
+                out=sw[:, lo:hi].rearrange("p i t -> p (i t)").bitcast(FP8X4),
+                scales=ss[:, lo:hi].rearrange("p i t -> p (i t)"),
+                in_=grt[m][:, lo:hi].rearrange("p i t j -> p (i t j)"),
+            )
+
+        def multiply(n, tiles):
             h, f, g = unit(n)
             if n == 0:
                 for t in tiles:
                     acc[t] = psum.tile(
                         [P, TOK], F32, tag="acc" if t < NA else "r", bufs=NA if t < NA else RING, name="acc%d" % t
                     )
-            sw, ss = swt[n]
-            wq, wsc = wqs[g * NF + f]
+            sw, ss = swt[n // 2]
             for t in tiles:
-                lo = t * P
+                c, i = divmod((g * NF + f) * NT + t, 4)
+                wq, wsc = wqs[c]
+                lo = i * P
                 nc.tensor.matmul_mx(
                     out=acc[t][:, h * HT : (h + 1) * HT],
                     lhsT=wq[:, lo : lo + P].bitcast(FP8X4),
                     lhsT_scale=wsc[:, lo : lo + P],
-                    rhs=sw[:].bitcast(FP8X4),
-                    rhs_scale=ss[:],
+                    rhs=sw[:, n % 2, :].bitcast(FP8X4),
+                    rhs_scale=ss[:, n % 2, :],
                     start=(f == 0 and g == 0),
                     stop=(f == NF - 1 and g == NG - 1),
                 )
@@ -454,39 +450,57 @@ def tile_efficient_skan_batch_kernel(
         quant_queue = []
         later = []
 
-
-        def end_part(it, h, part):
-            if h == 0:
-                later.append((it + GAIN_LAG, h, part))
-
-        def finish_some(it):
-            while later and later[0][0] <= it:
-                h, part = later.pop(0)[1:]
-                gain(h, (range(NA), range(NA, NT))[part])
-                state["gained"] += 1
-
         def fill_to(e):
             while state["fill"] < min(e, nbanks):
                 w_fill(state["fill"])
                 state["fill"] += 1
 
-        def banks(it, count):
+        def banks(m, count, by_vector=False):
             for i in range(count):
                 b = state["bank"]
-                if it >= W_START and b < nbanks:
+                if b < nbanks:
                     fill_to(b + LEAD)
-                    w_copy(b)
-                    if b % 3 == 2:
-                        quant_queue.extend([(it, b // 3, 0), (it, b // 3, 1)])
+                    w_copy(b, by_vector)
+                    if b % 2 == 1:
+                        quant_queue.append((m, b // 2))
                     state["bank"] = b + 1
 
-        def one_quant(it):
-            if quant_queue and quant_queue[0][0] + QLAG <= it:
-                c, part = quant_queue.pop(0)[1:]
-                w_quant(c, part)
-                state["wq"] = 2 * c + part + 1
+        def w_quants(m):
+            done = 0
+            while quant_queue and quant_queue[0][0] < m:
+                c = quant_queue.pop(0)[1]
+                w_quant(c)
+                state["wq"] = c + 1
+                done += 1
+            return done
 
-        fill_coef()
+        def multiply_some(m, last):
+            for i in range(MXA):
+                n = state["mxa"]
+                ready = 2 * state["wq"] >= min(3 * (n + 1), nbanks)
+                if n == NU // 2 and state["gained"] < 1:
+                    ready = False
+                if m >= 5 and n < NU and n // 2 <= last and ready:
+                    multiply(n, range(NA))
+                    state["mxa"] = n + 1
+                    if n == NU // 2 - 1:
+                        later.append((m + GAIN_LAG, 0))
+            for i in range(MXB):
+                n = state["mxb"]
+                if n == NU // 2 and state["gained"] < 2:
+                    break
+                if n < state["mxa"] and state["bank"] == nbanks:
+                    multiply(n, range(NA, NT))
+                    state["mxb"] = n + 1
+                    if n == NU // 2 - 1:
+                        later.append((m + GAIN_LAG, 1))
+
+        def gains(m):
+            while later and later[0][0] <= m:
+                part = later.pop(0)[1]
+                gain(0, (range(NA), range(NA, NT))[part])
+                state["gained"] += 1
+
         make_xt(0, 0)
         make_xt(0, 1)
         make_xt(1, 0)
@@ -495,77 +509,83 @@ def tile_efficient_skan_batch_kernel(
         silu_part(1)
         fill_xp(0, 1, "acc", NA)
         fill_xp(1, 0, "acc", NA)
-        for it in range(-1, NU + LAG4 + 16):
-            if it + 1 < NU:
-                s1(it + 1)
-            if 0 <= it - 1 < NU:
-                s2(it - 1)
-            banks(it, 1)
-            if 0 <= it - 2 < NU:
-                s3a(it - 2)
-            banks(it, 1)
-            if it == 1:
-                copy_xt(0, 1)
-                copy_xt(1, 0)
-                fill_xp(1, 1, "acc", NA)
-                copy_xt(1, 1)
-            if it == 3:
-                for i in range(W_HEAD // 3):
-                    banks(W_START, 3)
-                    one_quant(it + 1)
-                    one_quant(it + 1)
-            if it == BQ:
+        fill_coef()
+        turns(0)
+        copy_xt(0, 1)
+        copy_xt(1, 0)
+        nc.vector.tensor_copy(
+            out=coefT[:].rearrange("p (f a e) -> p f a e", f=NF, e=2),
+            in_=craw[:].rearrange("p a (e f) -> p f a e", f=NF),
+        )
+        fill_xp(1, 1, "acc", NA)
+        copy_xt(1, 1)
+
+        for m in range(NP + 1):
+            if m + 1 < NP:
+                turns(m + 1)
+            if m < NP:
+                reduce(m)
+                sine_even(m)
+            if m == 0:
+                banks(-1, W_HEAD, True)
+                w_quants(0)
                 base_quant()
                 bias_part()
-            if 5 <= it < 5 + NT:
-                base_out(it - 5)
-            if 4 <= it < 4 + NT:
-                base_tile(it - 4)
-            if 0 <= it - 2 < NU and it - 2 not in T_SET:
-                s3b(it - 2, 0)
-                banks(it, 1)
-                s3b(it - 2, 2)
-            tail = it > NU
-            if tail and it - LAG4 - 1 < NU:
-                s5(it - LAG4 - 1)
-            if 0 <= it - LAG4 < NU:
-                s4(it - LAG4)
-            for i in range(min(2, len(quant_queue))):
-                one_quant(it)
-            finish_some(it)
-            for i in range(MXR):
-                n = state["mxa"]
-                ready = state["wq"] >= min(2 * n + 2 + WQ_LAG, 2 * NF * NG)
-                if n == NU // 2 and not state["gained"]:
-                    ready = False
-                if it >= 5 + NT and n < NU and n <= it - LAG4 - 2 + tail and ready:
-                    s6(n, range(NA))
-                    state["mxa"] = n + 1
-                    if n % (NF * NG) == NF * NG - 1:
-                        end_part(it, n // (NF * NG), 0)
-            for i in range(MXB):
-                n = state["mxb"]
-                if n == NU // 2 and state["gained"] < 2:
-                    break
-                if n < state["mxa"] and state["bank"] == nbanks:
-                    s6(n, range(NA, NT))
-                    state["mxb"] = n + 1
-                    if n % (NF * NG) == NF * NG - 1:
-                        end_part(it, n // (NF * NG), 1)
-            if it == NU + 1:
-                turn(0, 0)
-                store(0, 0)
-            if it == NU + 2:
-                turn(0, 1)
-                store(0, 1)
-            if state["mxb"] == NU and "end" not in state:
-                state["end"] = 1
-                turn(0, 2)
-                store(0, 2)
-                for h, part in ((1, 0), (1, 1)):
-                    gain(h, (range(NA), range(NA, NT))[part])
-                    for tp in ((0,), (1, 2))[part]:
-                        turn(h, tp)
-                        store(h, tp)
-            if 0 <= it - LAG4 - 1 < NU and not tail:
-                s5(it - LAG4 - 1)
+            if m > 0:
+                banks(m, W_S[0])
+            if m in NN:
+                coef_rows(2 * m, (0, 1, 2, 3))
+            if m < NP:
+                sine(2 * m + 1)
+            if m > 0:
+                banks(m, W_S[1])
+            if m < NP:
+                coef_rows(2 * m + 1, (0, 1))
+            if m > 0:
+                banks(m, W_S[2])
+            if m < NP:
+                coef_rows(2 * m + 1, (2, 3))
+            if m > 0:
+                banks(m, W_S[3])
+            if 2 <= m < 2 + NT // 2:
+                base_out(2 * (m - 2))
+                base_out(2 * (m - 2) + 1)
+            if 1 <= m < 1 + NT // 2:
+                base_tile(2 * (m - 1))
+                base_tile(2 * (m - 1) + 1)
+            if m > 0:
+                banks(m, W_V, True)
+            gains(m)
+            if m > 0:
+                product_even(m - 1)
+                if m == NP:
+                    quant_pair(m - 1, (0,))
+                    multiply_some(m, m - 2)
+                    multiply(NU - 2, range(NT))
+                    turn(0, 0)
+                    store(0, 0)
+                group(2 * m - 1)
+                if m == NP:
+                    quant_pair(m - 1, (1,))
+                elif w_quants(m):
+                    quant_pair(m - 1, (0, 1))
+                else:
+                    quant_pair(m - 1, (0,))
+                    quant_pair(m - 1, (1,))
+            if m == 0:
+                banks(m, W_S0)
+            if m > 0:
+                banks(m, W_S[4])
+            if m < NP:
+                multiply_some(m, m - 2)
+
+        multiply(NU - 1, range(NT))
+        turn(0, 1)
+        store(0, 1)
+        turn(0, 2)
+        store(0, 2)
+        for tp in range(NT // 2):
+            gain(1, (2 * tp, 2 * tp + 1))
+            turn(1, tp)
+        for tp in range(NT // 2):
+            store(1, tp)

@@ -29,11 +29,11 @@ NU = 2 * NF * NG
 FLOPS = 2 * TOK * K * OUT * (NF + 1)
 
 NP = NU // 2
-BASE_V = (0, 2, 4)
+BASE_V = ()
 W_S = (1, 1, 1, 1, 1)
 W_S0 = 4
 W_V = 0
-W_HEAD = 2
+W_HEAD = 3
 RING = 4
 NA = 2
 LEAD = 4
@@ -42,7 +42,8 @@ MXB = 4
 GAIN_LAG = 1
 FB = (("x", "w", "x"), ("acc", "acc", "w"))
 OUT_V = ((1, 1),)
-SWB = 9
+SWB = 13
+KV = 1
 WB = 5
 WGB = 6
 NN = (11, 12, 13, 14)
@@ -61,7 +62,6 @@ def tile_efficient_skan_batch_kernel(
         snpool = ctx.enter_context(tc.tile_pool(name="sn", bufs=2))
         scpool = ctx.enter_context(tc.tile_pool(name="sc", bufs=4))
         swpool = ctx.enter_context(tc.tile_pool(name="sw", bufs=SWB))
-        opool = ctx.enter_context(tc.tile_pool(name="o", bufs=3))
         psum = ctx.enter_context(tc.psum_pool(name="psum", bufs=1))
         ctx.enter_context(tc.manual_schedule())
 
@@ -297,10 +297,16 @@ def tile_efficient_skan_batch_kernel(
             kk = kgpool.tile([P, 2, 4 * HT], I32, tag=("kg0", "kg1")[m % 2], name="kk", align_bytes=64)
             for i in range(2):
                 h, f, g = unit(2 * m + i)
-                nc.gpsimd.tensor_scalar(
-                    out=kk[:, i, :], in0=xs[(h, g)][:], scalar1=cturn[:, f : f + 1], scalar2=0.0,
-                    op0=ALU.mult, op1=ALU.add,
-                )
+                if m == 0 and i < KV:
+                    nc.vector.tensor_scalar(
+                        out=kk[:, i, :], in0=xs[(h, g)][:], scalar1=cturn[:, f : f + 1],
+                        scalar2=None, op0=ALU.mult,
+                    )
+                else:
+                    nc.gpsimd.tensor_scalar(
+                        out=kk[:, i, :], in0=xs[(h, g)][:], scalar1=cturn[:, f : f + 1],
+                        scalar2=0.0, op0=ALU.mult, op1=ALU.add,
+                    )
             kt[m] = kk
 
         def reduce(m):
@@ -435,7 +441,7 @@ def tile_efficient_skan_batch_kernel(
             fpss[(h, tp)] = fps
 
         def store(h, tp):
-            of = opool.tile([P, 2, 2 * P], F32, tag="of", bufs=6, name="of")
+            of = wpool.tile([P, 2, 2 * P], F32, tag="wraw", name="of", align_bytes=64)
             src = fpss[(h, tp)][:].rearrange("p m t o -> p m (t o)")
             if (h, tp) in OUT_V:
                 nc.vector.tensor_copy(out=of[:], in_=src)
@@ -502,23 +508,15 @@ def tile_efficient_skan_batch_kernel(
                 state["gained"] += 1
 
         make_xt(0, 0)
+        fill_xp(0, 1, "acc", NA)
         make_xt(0, 1)
+        fill_xp(1, 0, "acc", NA)
         make_xt(1, 0)
         make_xt(1, 1)
         silu_part(0)
         silu_part(1)
-        fill_xp(0, 1, "acc", NA)
-        fill_xp(1, 0, "acc", NA)
         fill_coef()
         turns(0)
-        copy_xt(0, 1)
-        copy_xt(1, 0)
-        nc.vector.tensor_copy(
-            out=coefT[:].rearrange("p (f a e) -> p f a e", f=NF, e=2),
-            in_=craw[:].rearrange("p a (e f) -> p f a e", f=NF),
-        )
-        fill_xp(1, 1, "acc", NA)
-        copy_xt(1, 1)
 
         for m in range(NP + 1):
             if m + 1 < NP:
@@ -527,7 +525,16 @@ def tile_efficient_skan_batch_kernel(
                 reduce(m)
                 sine_even(m)
             if m == 0:
+                copy_xt(0, 1)
+                copy_xt(1, 0)
+                nc.vector.tensor_copy(
+                    out=coefT[:].rearrange("p (f a e) -> p f a e", f=NF, e=2),
+                    in_=craw[:].rearrange("p a (e f) -> p f a e", f=NF),
+                )
+                fill_xp(1, 1, "acc", NA)
+                copy_xt(1, 1)
                 banks(-1, W_HEAD, True)
+            if m == 1:
                 w_quants(0)
                 base_quant()
                 bias_part()
@@ -557,13 +564,16 @@ def tile_efficient_skan_batch_kernel(
                 banks(m, W_V, True)
             gains(m)
             if m > 0:
-                product_even(m - 1)
                 if m == NP:
-                    quant_pair(m - 1, (0,))
-                    multiply_some(m, m - 2)
-                    multiply(NU - 2, range(NT))
                     turn(0, 0)
                     store(0, 0)
+                    multiply_some(m, m - 2)
+                product_even(m - 1)
+                if m == NP:
+                    turn(0, 1)
+                    store(0, 1)
+                    quant_pair(m - 1, (0,))
+                    multiply(NU - 2, range(NT))
                 group(2 * m - 1)
                 if m == NP:
                     quant_pair(m - 1, (1,))
@@ -580,8 +590,6 @@ def tile_efficient_skan_batch_kernel(
                 multiply_some(m, m - 2)
 
         multiply(NU - 1, range(NT))
-        turn(0, 1)
-        store(0, 1)
         turn(0, 2)
         store(0, 2)
         for tp in range(NT // 2):

@@ -32,6 +32,7 @@ NP = NU // 2
 BASE_V = ()
 W_S = (1, 1, 1, 1, 1)
 W_S0 = 4
+W_N = (1, 1, 0, 1, 0)
 W_V = 0
 W_HEAD = 3
 RING = 4
@@ -46,7 +47,9 @@ SWB = 13
 KV = 1
 WB = 5
 WGB = 6
-NN = (11, 12, 13, 14)
+NN = (4, 7, 10, 12, 14)
+TT = ()
+VEC = [n for n in range(NU) if (n % 2 == 0 and n // 2 not in NN) or n // 2 in TT]
 
 
 def tile_efficient_skan_batch_kernel(
@@ -326,24 +329,23 @@ def tile_efficient_skan_batch_kernel(
             if n % NF == NF - 1 and n + 1 < NU:
                 fill_xp(*unit(n + 1)[0::2])
 
-        def sine_even(m):
-            if m in NN:
-                sine(2 * m)
-                return
-            sn = snpool.tile([P, HT, 4], F32, name="sn")
-            nc.scalar.activation(
-                out=sn[:].rearrange("p t (u e) -> p t u e", e=2),
-                in_=rt[2 * m][:].rearrange("p (u t e) -> p t u e", u=2, e=2),
-                func=ACT.Sin,
-                scale=2.0 * math.pi,
-            )
-            sct[2 * m] = sn
-
         def sine(n):
             rr = rt[n]
-            nc.scalar.activation(out=rr[:], in_=rr[:], func=ACT.Sin, scale=2.0 * math.pi)
+            if n in VEC:
+                sn = snpool.tile([P, HT, 4], F32, name="sn")
+                nc.scalar.activation(
+                    out=sn[:].rearrange("p t (u e) -> p t u e", e=2),
+                    in_=rr[:].rearrange("p (u t e) -> p t u e", u=2, e=2),
+                    func=ACT.Sin,
+                    scale=2.0 * math.pi,
+                )
+                sct[n] = sn
+            else:
+                nc.scalar.activation(out=rr[:], in_=rr[:], func=ACT.Sin, scale=2.0 * math.pi)
 
         def coef_rows(n, js):
+            if n in VEC:
+                return
             h, f, g = unit(n)
             ci = (f * NG + g) * 4
             if js[0] == 0:
@@ -357,27 +359,29 @@ def tile_efficient_skan_batch_kernel(
                     scale=coefT[:, ci + j : ci + j + 1],
                 )
 
-        def product_even(m):
-            h, f, g = unit(2 * m)
-            ci = (f * NG + g) * 4
-            grp = kgpool.tile([P, 2, HT, 4], BF16, tag=("kg1", "kg0")[m % 2], name="grp", align_bytes=64)
-            if m in NN:
-                grt[m] = grp
-                group(2 * m)
-                return
-            nc.vector.tensor_tensor(
-                out=grp[:, 0],
-                in0=sct[2 * m][:],
-                in1=coefp[0][:, ci : ci + 4].unsqueeze(1).to_broadcast([P, HT, 4]),
-                op=ALU.mult,
-            )
-            grt[m] = grp
-
-        def group(n):
-            nc.vector.tensor_copy(
-                out=grt[n // 2][:, n % 2].rearrange("p (c i) j -> p c j i", i=4),
-                in_=sct[n][:].rearrange("p j (c i) -> p c j i", i=4),
-            )
+        def groups(m, vec):
+            if m not in grt:
+                grt[m] = kgpool.tile(
+                    [P, 2, HT, 4], BF16, tag=("kg1", "kg0")[m % 2], name="grp", align_bytes=64
+                )
+            for i in range(2):
+                n = 2 * m + i
+                if (n in VEC) != vec:
+                    continue
+                h, f, g = unit(n)
+                ci = (f * NG + g) * 4
+                if vec:
+                    nc.vector.tensor_tensor(
+                        out=grt[m][:, i],
+                        in0=sct[n][:],
+                        in1=coefp[0][:, ci : ci + 4].unsqueeze(1).to_broadcast([P, HT, 4]),
+                        op=ALU.mult,
+                    )
+                else:
+                    nc.vector.tensor_copy(
+                        out=grt[m][:, i].rearrange("p (c i) j -> p c j i", i=4),
+                        in_=sct[n][:].rearrange("p j (c i) -> p c j i", i=4),
+                    )
 
         def quant_pair(m, parts):
             if parts != (1,):
@@ -523,7 +527,7 @@ def tile_efficient_skan_batch_kernel(
                 turns(m + 1)
             if m < NP:
                 reduce(m)
-                sine_even(m)
+                sine(2 * m)
             if m == 0:
                 copy_xt(0, 1)
                 copy_xt(1, 0)
@@ -539,21 +543,20 @@ def tile_efficient_skan_batch_kernel(
                 base_quant()
                 bias_part()
             if m > 0:
-                banks(m, W_S[0])
-            if m in NN:
-                coef_rows(2 * m, (0, 1, 2, 3))
+                banks(m, (W_N if m in NN else W_S)[0])
             if m < NP:
+                coef_rows(2 * m, (0, 1, 2, 3))
                 sine(2 * m + 1)
             if m > 0:
-                banks(m, W_S[1])
+                banks(m, (W_N if m in NN else W_S)[1])
             if m < NP:
                 coef_rows(2 * m + 1, (0, 1))
             if m > 0:
-                banks(m, W_S[2])
+                banks(m, (W_N if m in NN else W_S)[2])
             if m < NP:
                 coef_rows(2 * m + 1, (2, 3))
             if m > 0:
-                banks(m, W_S[3])
+                banks(m, (W_N if m in NN else W_S)[3])
             if 2 <= m < 2 + NT // 2:
                 base_out(2 * (m - 2))
                 base_out(2 * (m - 2) + 1)
@@ -568,13 +571,13 @@ def tile_efficient_skan_batch_kernel(
                     turn(0, 0)
                     store(0, 0)
                     multiply_some(m, m - 2)
-                product_even(m - 1)
+                groups(m - 1, True)
                 if m == NP:
                     turn(0, 1)
                     store(0, 1)
                     quant_pair(m - 1, (0,))
                     multiply(NU - 2, range(NT))
-                group(2 * m - 1)
+                groups(m - 1, False)
                 if m == NP:
                     quant_pair(m - 1, (1,))
                 elif w_quants(m):
@@ -585,7 +588,7 @@ def tile_efficient_skan_batch_kernel(
             if m == 0:
                 banks(m, W_S0)
             if m > 0:
-                banks(m, W_S[4])
+                banks(m, (W_N if m in NN else W_S)[4])
             if m < NP:
                 multiply_some(m, m - 2)
 

@@ -525,8 +525,10 @@ def tile_efficient_skan_batch_kernel(
         for m in range(NP + 1):
             if m + 1 < NP:
                 turns(m + 1)
+            wv = 1 if 0 < m < 10 and m - 1 in NN else 0
             if m < NP:
                 reduce(m)
+                banks(m, wv, True)
                 sine(2 * m)
             if m == 0:
                 copy_xt(0, 1)
@@ -570,7 +572,8 @@ def tile_efficient_skan_batch_kernel(
                 if m == NP:
                     turn(0, 0)
                     store(0, 0)
-                    multiply_some(m, m - 2)
+                    while state["mxb"] < NU - 2:
+                        multiply_some(m, m - 2)
                 groups(m - 1, True)
                 if m == NP:
                     turn(0, 1)
@@ -587,7 +590,7 @@ def tile_efficient_skan_batch_kernel(
                     quant_pair(m - 1, (1,))
             if m == 0:
                 banks(m, W_S0)
-            if m > 0:
+            if m > 0 and not wv:
                 banks(m, (W_N if m in NN else W_S)[4])
             if m < NP:
                 multiply_some(m, m - 2)

import math
from contextlib import ExitStack

import concourse.mybir as mybir
from concourse.masks import make_identity

F32 = mybir.dt.float32
BF16 = mybir.dt.bfloat16
I32 = mybir.dt.int32
U32 = mybir.dt.uint32
U8 = mybir.dt.uint8
FP8X4 = mybir.dt.float8_e4m3fn_x4
FP4X4 = mybir.dt.float4_e2m1fn_x4
ACT = mybir.ActivationFunctionType
ALU = mybir.AluOpType
AX = mybir.AxisListType

P = 128
TOK = 512
K = 1024
OUT = 768
NF = 8
NG = 2
NT = OUT // P
NM = TOK // P
HT = 256
NU = 2 * NF * NG

FLOPS = 2 * TOK * K * OUT * (NF + 1)

NP = NU // 2
BASE_V = ()
W_S = (1, 1, 1, 1, 1)
W_S0 = 4
W_N = (1, 1, 0, 1, 0)
W_V = 0
W_HEAD = 3
RING = 4
NA = 2
LEAD = 4
MXA = 4
MXB = 4
GAIN_LAG = 1
FB = (("x", "w", "x"), ("acc", "acc", "w"))
OUT_V = ((1, 1),)
SWB = 13
KV = 1
WB = 5
WGB = 6
NN = (4, 7, 10, 12, 14)
TT = ()
VEC = [n for n in range(NU) if (n % 2 == 0 and n // 2 not in NN) or n // 2 in TT]


def tile_efficient_skan_batch_kernel(
    tc, x, base_weight_words, base_weight_scales, grid, scale_sp, coef, conv_w, conv_b, out
):
    nc = tc.nc
    with ExitStack() as ctx:
        const = ctx.enter_context(tc.tile_pool(name="const", bufs=1))
        wpool = ctx.enter_context(tc.tile_pool(name="wraw", bufs=WB))
        wgpool = ctx.enter_context(tc.tile_pool(name="wg", bufs=WGB))
        kgpool = ctx.enter_context(tc.tile_pool(name="kgp", bufs=1))
        rpool = ctx.enter_context(tc.tile_pool(name="r", bufs=4))
        snpool = ctx.enter_context(tc.tile_pool(name="sn", bufs=2))
        scpool = ctx.enter_context(tc.tile_pool(name="sc", bufs=4))
        swpool = ctx.enter_context(tc.tile_pool(name="sw", bufs=SWB))
        psum = ctx.enter_context(tc.psum_pool(name="psum", bufs=1))
        ctx.enter_context(tc.manual_schedule())

        xv = x.rearrange("b n k -> (b n) k").rearrange("(m p) k -> p m k", p=P)
        x_sb = {}
        for h in range(2):
            for g in range(NG):
                xt_in = const.tile([P, 2, K // NG], BF16, name="x_in%d%d" % (h, g))
                nc.sync.dma_start(
                    out=xt_in[:],
                    in_=xv[:, 2 * h : 2 * h + 2, K // NG * g : K // NG * (g + 1)],
                )
                x_sb[(h, g)] = xt_in

        gb = const.tile([P, NF], BF16, name="gb")
        nc.scalar.dma_start(out=gb[:], in_=grid.partition_broadcast(P))
        craw = const.tile([P, 2 * NG, 2 * NF], BF16, name="craw")
        nc.sync.dma_start(
            out=craw[:], in_=coef.rearrange("(a p e) f -> p a (e f)", a=2 * NG, p=P)
        )
        braw = const.tile([P, P], BF16, name="braw")
        nc.vector.memset(braw[:], 0.0)
        nc.sync.dma_start(
            out=braw[0 : NF * NT, :], in_=conv_b.rearrange("f (t c) -> (f t) c", c=P)
        )
        nc.sync.dma_start(
            out=braw[NF * NT : NF * NT + NT, :], in_=scale_sp.rearrange("(t c) -> t c", c=P)
        )

        ident = const.tile([P, P], F32, name="ident")
        make_identity(nc, ident[:])
        identb = const.tile([P, P], BF16, name="identb")
        make_identity(nc, identb[:])

        raws = {}

        def load_w(c):
            g, f = divmod(c, NF)
            wraw = wpool.tile([P, NT, K // NG], BF16, tag="wraw", name="wraw", align_bytes=64)
            nc.sync.dma_start(
                out=wraw[:],
                in_=conv_w[f].rearrange("(t p) (g k) -> g p t k", p=P, g=NG)[g],
            )
            raws[c] = wraw

        for c in range(3):
            load_w(c)
        w4w = const.tile([P, NG, 2 * OUT], U8, name="w4w", align_bytes=64)
        nc.sync.dma_start(
            out=w4w[:].bitcast(I32),
            in_=base_weight_words.rearrange("g p n -> p g n").bitcast(I32),
        )
        w4s = const.tile([P, NG, OUT], U8, name="w4s", align_bytes=64)
        nc.vector.memset(w4s[:].bitcast(I32), 0)
        w4sv = base_weight_scales.rearrange("g (q r) n -> r q g n", r=4)
        for r in range(4):
            nc.sync.dma_start(out=w4s[r:P:32, :, :].bitcast(I32), in_=w4sv[r].bitcast(I32))


        g32 = const.tile([P, NF], F32, name="g32")
        nc.vector.tensor_copy(out=g32[:], in_=gb[:])
        cturn = const.tile([P, NF], F32, name="cturn")
        nc.vector.tensor_scalar(
            out=cturn[:], in0=g32[:], scalar1=1.0 / (2.0 * math.pi), scalar2=None, op0=ALU.mult
        )
        coefT = const.tile([P, NF * NG * 4], F32, name="coefT")

        xs = {}
        xbank = {}
        silu_g = []
        for g in range(NG):
            sg = wpool.tile([P, TOK, 4], BF16, tag="wraw", name="sg", align_bytes=64)
            silu_g.append(sg)

        def make_xt(h, g):
            xb = psum.tile(
                [P, 2, HT], F32, tag="r", bufs=RING, name="xb"
            )
            for mi in range(2):
                xw = x_sb[(h, g)][:, mi, :].bitcast(F32)
                for u in range(2):
                    nc.tensor.transpose(
                        xb[:, u, mi * P : (mi + 1) * P],
                        xw[:, u : 2 * P : 2],
                        ident[:],
                    )
            xbank[(h, g)] = xb

        def copy_xt(h, g):
            xc = const.tile([P, 4 * HT], BF16, name="xs%d%d" % (h, g))
            dst = xc[:].bitcast(F32)
            src = xp[(h, g)][:].rearrange("p u t -> p (u t)")
            nc.vector.tensor_copy(out=dst, in_=src)
            xs[(h, g)] = xc

        def silu_part(h):
            for g in range(NG):
                nc.scalar.activation(
                    out=silu_g[g][:, h * HT : (h + 1) * HT, :].rearrange("p t (u e) -> p t u e", e=2),
                    in_=xbank[(h, g)][:].bitcast(BF16).rearrange("p u (t e) -> p t u e", e=2),
                    func=ACT.Silu,
                )

        coefp = []

        def fill_coef():
            cps = psum.tile([P, NF * NG * 4], F32, tag="w", name="cps")
            nc.tensor.matmul(
                cps[:],
                identb[:],
                craw[:].rearrange("p a (e f) -> p f a e", f=NF),
                start=True,
                stop=True,
            )
            coefp.append(cps)

        xp = {}

        def fill_xp(h, g, tag="x", bufs=1):
            xt = psum.tile([P, 2, HT], F32, tag=tag, bufs=bufs, name="xt")
            for mi in range(2):
                xw = x_sb[(h, g)][:, mi, :].bitcast(F32)
                for u in range(2):
                    nc.tensor.transpose(
                        xt[:, u, mi * P : (mi + 1) * P], xw[:, P * u : P * (u + 1)], ident[:]
                    )
            xp[(h, g)] = xt

        fill_xp(0, 0)
        copy_xt(0, 0)

        wgs = {}
        wqs = {}

        wbank = {}

        def w_fill(b):
            c, tp = divmod(b, NT // 2)
            wps = psum.tile([P, 2, 2, P], F32, tag="r", bufs=RING, name="wps")
            for tt in range(2):
                ww = raws[c][:, 2 * tp + tt, :].bitcast(F32)
                for u in range(2):
                    nc.tensor.transpose(wps[:, tt, u, :], ww[:, u * P : (u + 1) * P], ident[:])
            wbank[b] = wps
            if tp == NT // 2 - 1 and c + 3 < NF * NG:
                load_w(c + 3)

        def w_copy(b, by_vector):
            c, half = divmod(b, 2)
            if half == 0:
                wgs[c] = wgpool.tile([P, 4 * P * 4], BF16, name="wg", align_bytes=64)
            wgw = wgs[c][:].bitcast(F32)
            dst = wgw[:, 512 * half : 512 * (half + 1)].rearrange("p (t o u) -> p t o u", t=2, u=2)
            src = wbank[b][:].rearrange("p t u o -> p t o u")
            if by_vector:
                nc.vector.tensor_copy(out=dst, in_=src)
            else:
                nc.scalar.copy(out=dst, in_=src)

        def w_quant(c):
            wq = const.tile([P, 4 * P], U32, name="wq%d" % c, align_bytes=64)
            wsc = const.tile([P, 4 * P], U8, name="wsc%d" % c, align_bytes=64)
            wqs[c] = (wq, wsc)
            nc.vector.quantize_mx(out=wq[:].bitcast(FP8X4), scales=wsc[:], in_=wgs[c][:])

        bT = const.tile([P, 64], F32, name="bT")
        bsum = const.tile([P, NT], F32, name="bsum")
        sbs = const.tile([P, NT], F32, name="sbs")
        sil_w = const.tile([P, NG, TOK], U32, name="sil_w", align_bytes=64)
        sil_s = const.tile([P, NG, TOK], U8, name="sil_s", align_bytes=64)
        basec = []

        def bias_part():
            bps = psum.tile([P, P], BF16, tag="acc", bufs=NA, name="bps")
            nc.tensor.transpose(bps[:], braw[:], identb[:])
            nc.vector.tensor_copy(out=bT[:, 0 : NF * NT + NT], in_=bps[:, 0 : NF * NT + NT])
            nc.vector.tensor_reduce(
                out=bsum[:],
                in_=bT[:, 0 : NF * NT].rearrange("p (f t) -> p t f", t=NT),
                axis=AX.X,
                op=ALU.add,
            )
            nc.vector.tensor_mul(out=sbs[:], in0=bsum[:], in1=bT[:, NF * NT : NF * NT + NT])

        def base_quant():
            for g in range(NG):
                nc.vector.quantize_mx(
                    out=sil_w[:, g, :].bitcast(FP8X4),
                    scales=sil_s[:, g, :],
                    in_=silu_g[g][:].rearrange("p t j -> p (t j)"),
                )

        def base_tile(t):
            bacc = psum.tile([P, TOK], F32, tag="acc", bufs=NA, name="bacc")
            for g in range(NG):
                nc.tensor.matmul_mx(
                    out=bacc[:],
                    lhsT=w4w[:, g, 2 * P * t : 2 * P * (t + 1)].bitcast(FP4X4),
                    lhsT_scale=w4s[:, g, P * t : P * (t + 1)],
                    rhs=sil_w[:, g, :].bitcast(FP8X4),
                    rhs_scale=sil_s[:, g, :],
                    start=(g == 0),
                    stop=(g == NG - 1),
                )
            bacs[t] = bacc

        bacs = {}

        def base_out(t):
            bacc = bacs[t]
            bc = const.tile([P, TOK], F32, name="basec%d" % t)
            if t in BASE_V:
                nc.vector.tensor_scalar(
                    out=bc[:], in0=bacc[:], scalar1=sbs[:, t : t + 1], scalar2=None, op0=ALU.add
                )
            else:
                nc.scalar.activation(out=bc[:], in_=bacc[:], func=ACT.Identity, bias=sbs[:, t : t + 1])
            basec.append(bc)

        kt = {}
        rt = {}
        sct = {}
        grt = {}
        swt = {}
        acc = {}

        def unit(n):
            h, rest = divmod(n, NF * NG)
            g, f = divmod(rest, NF)
            return h, f, g

        def turns(m):
            kk = kgpool.tile([P, 2, 4 * HT], I32, tag=("kg0", "kg1")[m % 2], name="kk", align_bytes=64)
            for i in range(2):
                h, f, g = unit(2 * m + i)
                if m == 0 and i < KV:
                    nc.vector.tensor_scalar(
                        out=kk[:, i, :], in0=xs[(h, g)][:], scalar1=cturn[:, f : f + 1],
                        scalar2=None, op0=ALU.mult,
                    )
                else:
                    nc.gpsimd.tensor_scalar(
                        out=kk[:, i, :], in0=xs[(h, g)][:], scalar1=cturn[:, f : f + 1],
                        scalar2=0.0, op0=ALU.mult, op1=ALU.add,
                    )
            kt[m] = kk

        def reduce(m):
            for i in range(2):
                n = 2 * m + i
                h, f, g = unit(n)
                rr = rpool.tile([P, 4 * HT], F32, name="rr")
                nc.vector.scalar_tensor_tensor(
                    out=rr[:],
                    in0=xp[(h, g)][:].rearrange("p u t -> p (u t)").bitcast(BF16),
                    scalar=cturn[:, f : f + 1],
                    in1=kt[m][:, i, :],
                    op0=ALU.mult,
                    op1=ALU.subtract,
                )
                rt[n] = rr
            if n % NF == NF - 1 and n + 1 < NU:
                fill_xp(*unit(n + 1)[0::2])

        def sine(n):
            rr = rt[n]
            if n in VEC:
                sn = snpool.tile([P, HT, 4], F32, name="sn")
                nc.scalar.activation(
                    out=sn[:].rearrange("p t (u e) -> p t u e", e=2),
                    in_=rr[:].rearrange("p (u t e) -> p t u e", u=2, e=2),
                    func=ACT.Sin,
                    scale=2.0 * math.pi,
                )
                sct[n] = sn
            else:
                nc.scalar.activation(out=rr[:], in_=rr[:], func=ACT.Sin, scale=2.0 * math.pi)

        def coef_rows(n, js):
            if n in VEC:
                return
            h, f, g = unit(n)
            ci = (f * NG + g) * 4
            if js[0] == 0:
                sct[n] = scpool.tile([P, 4, HT], BF16, name="sc")
            rv = rt[n][:].rearrange("p (u t e) -> p u e t", u=2, e=2)
            for j in js:
                nc.scalar.activation(
                    out=sct[n][:, j, :],
                    in_=rv[:, j // 2, j % 2, :],
                    func=ACT.Copy,
                    scale=coefT[:, ci + j : ci + j + 1],
                )

        def groups(m, vec):
            if m not in grt:
                grt[m] = kgpool.tile(
                    [P, 2, HT, 4], BF16, tag=("kg1", "kg0")[m % 2], name="grp", align_bytes=64
                )
            for i in range(2):
                n = 2 * m + i
                if (n in VEC) != vec:
                    continue
                h, f, g = unit(n)
                ci = (f * NG + g) * 4
                if vec:
                    nc.vector.tensor_tensor(
                        out=grt[m][:, i],
                        in0=sct[n][:],
                        in1=coefp[0][:, ci : ci + 4].unsqueeze(1).to_broadcast([P, HT, 4]),
                        op=ALU.mult,
                    )
                else:
                    nc.vector.tensor_copy(
                        out=grt[m][:, i].rearrange("p (c i) j -> p c j i", i=4),
                        in_=sct[n][:].rearrange("p j (c i) -> p c j i", i=4),
                    )

        def quant_pair(m, parts):
            if parts != (1,):
                sw = swpool.tile([P, 2, HT], U32, name="sw", align_bytes=64)
                ss = swpool.tile([P, 2, HT], U8, name="ss", align_bytes=64)
                swt[m] = (sw, ss)
            sw, ss = swt[m]
            lo, hi = parts[0], parts[-1] + 1
            nc.vector.quantize_mx(
                out=sw[:, lo:hi].rearrange("p i t -> p (i t)").bitcast(FP8X4),
                scales=ss[:, lo:hi].rearrange("p i t -> p (i t)"),
                in_=grt[m][:, lo:hi].rearrange("p i t j -> p (i t j)"),
            )

        def multiply(n, tiles):
            h, f, g = unit(n)
            if n == 0:
                for t in tiles:
                    acc[t] = psum.tile(
                        [P, TOK], F32, tag="acc" if t < NA else "r", bufs=NA if t < NA else RING, name="acc%d" % t
                    )
            sw, ss = swt[n // 2]
            for t in tiles:
                c, i = divmod((g * NF + f) * NT + t, 4)
                wq, wsc = wqs[c]
                lo = i * P
                nc.tensor.matmul_mx(
                    out=acc[t][:, h * HT : (h + 1) * HT],
                    lhsT=wq[:, lo : lo + P].bitcast(FP8X4),
                    lhsT_scale=wsc[:, lo : lo + P],
                    rhs=sw[:, n % 2, :].bitcast(FP8X4),
                    rhs_scale=ss[:, n % 2, :],
                    start=(f == 0 and g == 0),
                    stop=(f == NF - 1 and g == NG - 1),
                )

        outv = out.rearrange("b n o -> (b n) o").rearrange("(m p) o -> p m o", p=P)

        fpss = {}

        def gain(h, tiles):
            for t in tiles:
                bc = basec[t][:, h * HT : (h + 1) * HT]
                nc.vector.scalar_tensor_tensor(
                    out=bc,
                    in0=acc[t][:, h * HT : (h + 1) * HT],
                    scalar=bT[:, NF * NT + t : NF * NT + t + 1],
                    in1=bc,
                    op0=ALU.mult,
                    op1=ALU.add,
                )

        def turn(h, tp):
            fps = psum.tile([P, 2, 2, P], F32, tag=FB[h][tp], bufs=NA if FB[h][tp] == "acc" else 1, name="fps")
            for tt in range(2):
                for mi in range(2):
                    lo = h * HT + mi * P
                    nc.tensor.transpose(
                        fps[:, mi, tt, :], basec[2 * tp + tt][:, lo : lo + P], ident[:]
                    )
            fpss[(h, tp)] = fps

        def store(h, tp):
            of = wpool.tile([P, 2, 2 * P], F32, tag="wraw", name="of", align_bytes=64)
            src = fpss[(h, tp)][:].rearrange("p m t o -> p m (t o)")
            if (h, tp) in OUT_V:
                nc.vector.tensor_copy(out=of[:], in_=src)
            else:
                nc.scalar.copy(out=of[:], in_=src)
            nc.sync.dma_start(
                out=outv[:, 2 * h : 2 * h + 2, 2 * P * tp : 2 * P * (tp + 1)], in_=of[:]
            )

        nbanks = NF * NG * (NT // 2)
        state = {"bank": 0, "mxa": 0, "gained": 0, "mxb": 0, "wq": 0, "fill": 0}
        quant_queue = []
        later = []

        def fill_to(e):
            while state["fill"] < min(e, nbanks):
                w_fill(state["fill"])
                state["fill"] += 1

        def banks(m, count, by_vector=False):
            for i in range(count):
                b = state["bank"]
                if b < nbanks:
                    fill_to(b + LEAD)
                    w_copy(b, by_vector)
                    if b % 2 == 1:
                        quant_queue.append((m, b // 2))
                    state["bank"] = b + 1

        def w_quants(m):
            done = 0
            while quant_queue and quant_queue[0][0] < m:
                c = quant_queue.pop(0)[1]
                w_quant(c)
                state["wq"] = c + 1
                done += 1
            return done

        def multiply_some(m, last):
            for i in range(MXA):
                n = state["mxa"]
                ready = 2 * state["wq"] >= min(3 * (n + 1), nbanks)
                if n == NU // 2 and state["gained"] < 1:
                    ready = False
                if m >= 5 and n < NU and n // 2 <= last and ready:
                    multiply(n, range(NA))
                    state["mxa"] = n + 1
                    if n == NU // 2 - 1:
                        later.append((m + GAIN_LAG, 0))
            for i in range(MXB):
                n = state["mxb"]
                if n == NU // 2 and state["gained"] < 2:
                    break
                if n < state["mxa"] and state["bank"] == nbanks:
                    multiply(n, range(NA, NT))
                    state["mxb"] = n + 1
                    if n == NU // 2 - 1:
                        later.append((m + GAIN_LAG, 1))

        def gains(m):
            while later and later[0][0] <= m:
                part = later.pop(0)[1]
                gain(0, (range(NA), range(NA, NT))[part])
                state["gained"] += 1

        make_xt(0, 0)
        fill_xp(0, 1, "acc", NA)
        make_xt(0, 1)
        fill_xp(1, 0, "acc", NA)
        make_xt(1, 0)
        make_xt(1, 1)
        silu_part(0)
        silu_part(1)
        fill_coef()
        turns(0)

        for m in range(NP + 1):
            if m + 1 < NP:
                turns(m + 1)
            wv = 1 if 0 < m < 10 and m - 1 in NN else 0
            if m < NP:
                reduce(m)
                banks(m, wv, True)
                sine(2 * m)
            if m == 0:
                copy_xt(0, 1)
                copy_xt(1, 0)
                nc.vector.tensor_copy(
                    out=coefT[:].rearrange("p (f a e) -> p f a e", f=NF, e=2),
                    in_=craw[:].rearrange("p a (e f) -> p f a e", f=NF),
                )
                fill_xp(1, 1, "acc", NA)
                copy_xt(1, 1)
                banks(-1, W_HEAD, True)
            if m == 1:
                w_quants(0)
                base_quant()
                bias_part()
            if m > 0:
                banks(m, (W_N if m in NN else W_S)[0])
            if m < NP:
                coef_rows(2 * m, (0, 1, 2, 3))
                sine(2 * m + 1)
            if m > 0:
                banks(m, (W_N if m in NN else W_S)[1])
            if m < NP:
                coef_rows(2 * m + 1, (0, 1))
            if m > 0:
                banks(m, (W_N if m in NN else W_S)[2])
            if m < NP:
                coef_rows(2 * m + 1, (2, 3))
            if m > 0:
                banks(m, (W_N if m in NN else W_S)[3])
            if 2 <= m < 2 + NT // 2:
                base_out(2 * (m - 2))
                base_out(2 * (m - 2) + 1)
            if 1 <= m < 1 + NT // 2:
                base_tile(2 * (m - 1))
                base_tile(2 * (m - 1) + 1)
            if m > 0:
                banks(m, W_V, True)
            gains(m)
            if m > 0:
                if m == NP:
                    turn(0, 0)
                    store(0, 0)
                    while state["mxb"] < NU - 2:
                        multiply_some(m, m - 2)
                groups(m - 1, True)
                if m == NP:
                    turn(0, 1)
                    store(0, 1)
                    quant_pair(m - 1, (0,))
                    multiply(NU - 2, range(NT))
                groups(m - 1, False)
                if m == NP:
                    quant_pair(m - 1, (1,))
                elif w_quants(m):
                    quant_pair(m - 1, (0, 1))
                else:
                    quant_pair(m - 1, (0,))
                    quant_pair(m - 1, (1,))
            if m == 0:
                banks(m, W_S0)
            if m > 0 and not wv:
                banks(m, (W_N if m in NN else W_S)[4])
            if m < NP:
                multiply_some(m, m - 2)

        multiply(NU - 1, range(NT))
        turn(0, 2)
        store(0, 2)
        for tp in range(NT // 2):
            gain(1, (2 * tp, 2 * tp + 1))
            turn(1, tp)
        for tp in range(NT // 2):
            store(1, tp)
